import numpy as np
import ml_dtypes


def mxq(x, axis, fmt="e4m3"):
    dtype, down = {"e4m3": (ml_dtypes.float8_e4m3fn, 7), "e5m2": (ml_dtypes.float8_e5m2, 14)}[fmt]
    v = np.moveaxis(np.asarray(x, np.float32).astype(ml_dtypes.bfloat16).astype(np.float64), axis, -1)
    blocks = v.reshape(v.shape[:-1] + (-1, 32))
    amax = np.abs(blocks).max(-1, keepdims=True)
    byte = np.maximum(np.where(amax > 0, np.frexp(amax)[1] - 1 + 127, 0) - down, 1)
    scale = np.exp2(byte - 127.0)
    codes = (blocks / scale).astype(np.float32).astype(dtype).astype(np.float64)
    return np.moveaxis((codes * scale).reshape(v.shape), -1, axis)


WIDE = False


def mx_kscale(k):
    if not WIDE:
        return np.ones(k)
    levels = np.array([18, -18])
    if k % 512:
        return np.exp2(np.random.permutation(np.resize(levels, k // 32))).repeat(32)
    a = np.empty((k // 512, 16))
    for p in range(k // 512):
        a[p, :8] = np.random.permutation(np.resize(levels, 8))
        for g in range(8):
            far = levels[np.abs(levels - a[p, g]) >= 10]
            a[p, g + 8] = far[np.random.randint(len(far))]
    return np.exp2(a.ravel()).repeat(32)


BF16 = ml_dtypes.bfloat16


def bf(x):
    return np.asarray(x, np.float32).astype(BF16)


def f64(x):
    return np.asarray(x).astype(np.float64)


I, M, O, B = 1024, 1024, 1024, 1024


def sigmoid(v):
    return 1.0 / (1.0 + np.exp(-v))


def setup_inputs():
    u = mx_kscale(O)
    v = mx_kscale(M)
    s = mx_kscale(B)
    x0 = bf(np.random.standard_normal((I, B)))
    out0 = bf(np.tanh(np.random.standard_normal((O, B))))
    mem0 = bf(np.random.standard_normal((M, B)) * 0.8)
    inp_out = bf(sigmoid(np.random.standard_normal((M, B)) * 1.2) * sigmoid(np.random.standard_normal((M, B)) * 1.4))
    w_readgate0 = bf(np.random.standard_normal((M, I)) / np.sqrt(I))
    w_rec_readgate = bf(np.random.standard_normal((M, O)) / np.sqrt(O))
    w_mem_readgate = bf(np.random.standard_normal((M, M)) / np.sqrt(M))
    w_hid_out0 = bf(np.random.standard_normal((O, M)) / np.sqrt(M))
    g = bf(np.random.standard_normal((O, B)) * np.exp2(np.random.randint(-6, 1, (1, B))) * 8.0 * u[:, None] / s[None, :])
    mem_out = sigmoid(f64(w_readgate0) @ f64(x0) + f64(w_rec_readgate) @ f64(out0) + f64(w_mem_readgate) @ f64(mem0))
    y = np.tanh(f64(w_hid_out0) @ (mem_out + f64(inp_out)))
    return {
        "x": bf(f64(x0) * s[None, :]),
        "out0": out0,
        "mem0": mem0,
        "inp_out": inp_out,
        "w_readgate": bf(f64(w_readgate0) / v[:, None]),
        "w_rec_readgate": w_rec_readgate,
        "w_mem_readgate": w_mem_readgate,
        "w_hid_out": bf(f64(w_hid_out0) * v[None, :] / u[:, None]),
        "mem_out": np.asarray(mem_out, np.float32),
        "y": np.asarray(y, np.float32),
        "grad_out": g,
    }


def reference(x, out0, mem0, inp_out, w_readgate, w_rec_readgate, w_mem_readgate, w_hid_out, mem_out, y, grad_out):
    m = f64(mem_out)
    yf = f64(y)
    dz2 = f64(grad_out) * (1.0 - yf * yf)
    dh = mxq(f64(w_hid_out), 0, "e4m3").T @ mxq(dz2, 0, "e5m2")
    dz1 = dh * (m * (1.0 - m))
    dx = mxq(f64(w_readgate), 0, "e4m3").T @ mxq(dz1, 0, "e5m2")
    dw = mxq(dz1, 1, "e5m2") @ mxq(f64(x), 1, "e4m3").T
    return dx, dw

@@ -1,0 +1,291 @@
+from contextlib import ExitStack
+
+import concourse.mybir as mybir
+from concourse.masks import make_identity
+
+F32 = mybir.dt.float32
+BF16 = mybir.dt.bfloat16
+U32 = mybir.dt.uint32
+U8 = mybir.dt.uint8
+E4M3 = mybir.dt.float8_e4m3fn_x4
+E5M2 = mybir.dt.float8_e5m2_x4
+ACT = mybir.ActivationFunctionType
+ALU = mybir.AluOpType
+
+SIZE = 1024
+P = 128
+PACK = 4
+HALF = 512
+
+FLOPS = 3 * 2 * SIZE * SIZE * SIZE
+BYTES = 4 * SIZE * SIZE * 2 + 2 * SIZE * SIZE * 4 + 2 * SIZE * SIZE * 4
+
+ORDER = """
+Lh0 Lh1 Ly00 Lg00 Ly10 Lg10 Lr0
+Ih00V Ih11S Ih01V Ih10V Qh00 Qh01 Qh10 Qh11
+Lr1 Lm00 Lm10 Lx0
+Sy00 Zz00 Qz00 Hp0000 Hp0001 Hp0002 Hp0003 Hp0100 Hp0101 Hp0102 Hp0103 Ly01 Lg01 Sy10 Zz10 Ir00S Ir01V Ir10V Qz10 Hp1000 Hp1001 Hp1002 Hp1003 Ir11S Qr00 Qr01 Qr10 Qr11
+Ly11 Lg11 Lx1 Sm00 Hp1100 Hp1101 Hp1102 Hp1103 Dz000 Dz001 Dz002 Dz003 Lm01 Sm10 Tt000 Xt000 Cc000S I100S Dz100 Dz101 Dz102 Dz103 Lm11 Tt001 Xt001 Tt100 Tt101
+Sy01 Xc000V Q100 I110V Cc001V Xc001S Q110 Cc101V Sy11 Cc100S
+P0000 P0001 P0010 P0011 E0000S E0010S Zz01 Zz11 Xt011 Xc011S P0020 P0021 E0001V W000 E0011S W001 E0020S Qz01 Qz11 E0021S W002 Sm01
+P0030 P0031 Xt110 Xt111 Xt010 E0030S Qt00 Qt01 Xc110S Xc111S Sm11 Xc010V E0031V W003
+Hp0010 Hp1010 Dz010 Hp0011 Hp1011 Dz011 Hp0012 Hp1012 Dz012 Hp0013 Hp1013 Dz013 Qx00 Qx10
+Hp0110 Hp1110 Xt100 Tt010 Tt011 Xt101 Cc010V Cc011S Dz110 Qt10 Xc100S Xc101S Qx01 Qx11 Hp0111 Hp0112 Hp0113 Hp1111 Hp1112 Hp1113 I101S Dz111 Dz112 Dz113
+P10000 P10001 P10100 P10101 E10000S E10001S W1000 E10100S E10101S W1010 I111V P10010 P10011 P10110 P10111 Q101 Q111 E10010S E10011S W1001 E10110S E10111V W1011
+Tt110 Tt111 Cc110S P0100 P0101 P0110 Cc111V E0100S E0101V W010 P0111 E0110S E0111V W011 P0120 P0121 Qt11 E0120S E0121V W012 P0130 P0131 E0130S E0131V W013
+P11000 P11001 E11000S E11001V W1100 P11100 P11101 E11100S E11101V W1110 P11010 P11011 E11010S E11011V W1101 P11110 P11111 E11110S E11111V W1111
+"""
+
+
+def tile_pt_grumb_pb_v_kernel(
+    tc, x, out0, mem0, inp_out, w_readgate, w_rec_readgate, w_mem_readgate, w_hid_out, mem_out, y, grad_out, out_0, out_1
+):
+    nc = tc.nc
+    w_hid_hbm = w_hid_out.rearrange("(k p j) m -> k p j m", p=P, j=PACK)
+    w_rg_hbm = w_readgate.rearrange("(k p j) i -> k p j i", p=P, j=PACK)
+    y_hbm = y.rearrange("(k p j) b -> k p j b", p=P, j=PACK)
+    grad_hbm = grad_out.rearrange("(k p j) b -> k p j b", p=P, j=PACK)
+    mem_hbm = mem_out.rearrange("(g p t) b -> g p t b", p=P, t=PACK)
+    x_hbm = x.rearrange("(n a p) b -> n p a b", p=P, a=PACK)
+    out_0_hbm = out_0.rearrange("(z a p) b -> z p a b", p=P, a=2)
+    out_1_hbm = out_1.rearrange("(g p t) i -> g p t i", p=P, t=PACK)
+
+    with ExitStack() as ctx:
+        keep = ctx.enter_context(tc.tile_pool(name="keep", bufs=1))
+        raw = ctx.enter_context(tc.tile_pool(name="raw", bufs=1))
+        work = ctx.enter_context(tc.tile_pool(name="work", bufs=1))
+        psum = ctx.enter_context(tc.psum_pool(name="psum", bufs=8))
+
+        def keep_tile(shape, dtype, name):
+            return keep.tile(shape, dtype, name=name, tag=name, align_bytes=64)
+
+        def codes_pair(name):
+            return keep_tile([P, 2, SIZE], U32, name + "_codes"), keep_tile([P, 2, SIZE], U8, name + "_scales")
+
+        w_hid_q = codes_pair("w_hid")
+        w_rg_q = codes_pair("w_rg")
+        dz2_q = codes_pair("dz2")
+        dz1_q = codes_pair("dz1")
+        dz1_t_q = codes_pair("dz1_t")
+        x_t_q = codes_pair("x_t")
+        dz1 = [keep_tile([P, PACK, SIZE], BF16, "dz1_%d" % g) for g in range(2)]
+        ident = keep_tile([P, P], F32, "ident")
+        minus_half = keep_tile([P, 1], F32, "minus_half")
+        held = {}
+
+        def raw_tile(shape, dtype, tag, bufs):
+            return raw.tile(shape, dtype, name=tag, tag=tag, align_bytes=64, bufs=bufs)
+
+        def grouped_tile():
+            return work.tile([P, HALF, PACK], BF16, name="grouped", tag="grouped", align_bytes=64, bufs=8)
+
+        def bank(shape):
+            return psum.tile(shape, F32, name="bank", tag="bank")
+
+        def half(n):
+            return slice(n * HALF, (n + 1) * HALF)
+
+        def move(engine, out, in_):
+            if engine == "S":
+                nc.scalar.copy(out=out, in_=in_)
+            else:
+                nc.vector.tensor_copy(out=out, in_=in_)
+
+        def quantize(pair, dtype, row, col, grouped):
+            codes, scales = pair
+            nc.vector.quantize_mx(
+                out=codes[:, row, half(col)].bitcast(dtype),
+                scales=scales[:, row, half(col)],
+                in_=grouped[:].rearrange("p n j -> p (n j)"),
+            )
+
+        def product_pass(k, out, lhs, lhs_dtype, lhs_first, rhs, rhs_dtype, rhs_half):
+            lhs_cols = slice(lhs_first, lhs_first + P)
+            nc.tensor.matmul_mx(
+                out=out,
+                lhsT=lhs[0][:, k, lhs_cols].bitcast(lhs_dtype),
+                lhsT_scale=lhs[1][:, k, lhs_cols],
+                rhs=rhs[0][:, k, half(rhs_half)].bitcast(rhs_dtype),
+                rhs_scale=rhs[1][:, k, half(rhs_half)],
+                start=(k == 0),
+                stop=(k == 1),
+            )
+
+        def load_weight(key, hbm, k, pieces):
+            held[key, k] = raw_tile([P, PACK, SIZE], BF16, "w_raw", 3)
+            for cols in pieces:
+                nc.sync.dma_start(out=held[key, k][:, :, cols], in_=hbm[k][:, :, cols])
+
+        def load_w_hid(k):
+            load_weight("w_hid_raw", w_hid_hbm, k, [half(0), half(1)] if k == 0 else [slice(0, SIZE)])
+
+        def load_w_rg(k):
+            load_weight("w_rg_raw", w_rg_hbm, k, [slice(0, SIZE)])
+
+        def load_part(key, hbm, dtype, tag, bufs, k, h):
+            held[key, k, h] = raw_tile([P, PACK, HALF], dtype, tag, bufs)
+            nc.sync.dma_start(out=held[key, k, h][:], in_=hbm[k][:, :, half(h)])
+
+        def load_y(k, h):
+            load_part("y_raw", y_hbm, F32, "f32_raw", 4, k, h)
+
+        def load_mem(g, h):
+            load_part("mem_raw", mem_hbm, F32, "f32_raw", 4, g, h)
+
+        def load_grad(k, h):
+            load_part("grad_raw", grad_hbm, BF16, "grad_raw", 4, k, h)
+
+        def load_x(n):
+            held["x_raw", n] = raw_tile([P, PACK, SIZE], BF16, "x_raw", 2)
+            nc.sync.dma_start(out=held["x_raw", n][:], in_=x_hbm[n])
+
+        def square_y(k, h):
+            t = work.tile([P, HALF, PACK], F32, name="y_squared", tag="y_squared", align_bytes=64, bufs=2)
+            nc.scalar.activation(
+                out=t[:].rearrange("p (c i) j -> p c j i", i=4),
+                in_=held["y_raw", k, h][:].rearrange("p j (c i) -> p c j i", i=4),
+                func=ACT.Square,
+            )
+            held["y_squared", k, h] = t
+
+        def square_mem(g, h):
+            t = held["mem_raw", g, h]
+            nc.scalar.activation(out=t[:], in_=t[:], func=ACT.Square, bias=minus_half[:])
+
+        def make_dz2(k, h):
+            grouped = grouped_tile()
+            nc.vector.scalar_tensor_tensor(
+                out=grouped[:],
+                in0=held["y_squared", k, h][:],
+                scalar=1.0,
+                in1=held["grad_raw", k, h][:].rearrange("p j b -> p b j"),
+                op0=ALU.subtract,
+                op1=ALU.mult,
+            )
+            held["dz2", k, h] = grouped
+
+        def interleave_w_hid(k, c, engine):
+            grouped = grouped_tile()
+            move(
+                engine,
+                grouped[:].rearrange("p (t m) j -> p t m j", t=PACK),
+                held["w_hid_raw", k][:, :, half(c)].rearrange("p j (m t) -> p t m j", t=PACK),
+            )
+            held["w_hid", k, c] = grouped
+
+        def interleave(engine, source):
+            grouped = grouped_tile()
+            move(
+                engine,
+                grouped[:].rearrange("p (c i) j -> p c j i", i=4),
+                source.rearrange("p j (c i) -> p c j i", i=4),
+            )
+            return grouped
+
+        def interleave_w_rg(k, c, engine):
+            held["w_rg", k, c] = interleave(engine, held["w_rg_raw", k][:, :, half(c)])
+
+        def interleave_dz1(g, h, engine):
+            held["dz1", g, h] = interleave(engine, dz1[g][:, :, half(h)])
+
+        def hidden_pass(k, g, h, t):
+            if k == 0:
+                held["dh", g, h, t] = bank([P, HALF])
+            product_pass(k, held["dh", g, h, t][:], w_hid_q, E4M3, g * HALF + t * P, dz2_q, E5M2, h)
+
+        def make_dz1(g, h, t):
+            nc.vector.scalar_tensor_tensor(
+                out=dz1[g][:, t, half(h)],
+                in0=held["mem_raw", g, h][:, t, :],
+                scalar=0.25,
+                in1=held["dh", g, h, t][:],
+                op0=ALU.subtract,
+                op1=ALU.mult,
+            )
+
+        def transpose(key, source, h, z):
+            words = source[:].rearrange("p a b -> p (a b)").bitcast(F32)
+            ps = bank([P, 2, 2, P])
+            for a in range(2):
+                for u in range(2):
+                    first = (2 * z + a) * HALF + h * 2 * P + u
+                    nc.tensor.transpose(ps[:, a, u, :], words[:, first : first + 2 * P - 1 : 2], ident[:])
+            held[key, h, z] = ps
+
+        def copy_transposed(key, h, z, engine):
+            if (key, h) not in held:
+                held[key, h] = grouped_tile()
+            words = held[key, h][:].rearrange("p n j -> p (n j)").bitcast(F32)
+            move(
+                engine,
+                words[:, half(z)].rearrange("p (a r u) -> p a r u", a=2, u=2),
+                held[key, h, z][:].rearrange("p a u r -> p a r u"),
+            )
+
+        def stage_for(key):
+            if key not in held:
+                held[key] = work.tile([P, 2, HALF], F32, name="stage", tag="stage", align_bytes=64, bufs=5)
+            return held[key]
+
+        def out_0_product(h, z, a):
+            held["ps_0", h, z, a] = bank([P, HALF])
+            for k in range(2):
+                product_pass(k, held["ps_0", h, z, a][:], w_rg_q, E4M3, (2 * z + a) * P, dz1_q, E5M2, h)
+
+        def out_0_copy(h, z, a, engine):
+            move(engine, stage_for(("stage_0", h, z))[:, a, :], held["ps_0", h, z, a][:])
+
+        def out_0_store(h, z):
+            nc.sync.dma_start(out=out_0_hbm[z][:, :, half(h)], in_=held["stage_0", h, z][:])
+
+        def out_1_product(g, z, n, a):
+            held["ps_1", g, z, n, a] = bank([P, HALF])
+            for k in range(2):
+                product_pass(k, held["ps_1", g, z, n, a][:], dz1_t_q, E5M2, g * HALF + (2 * z + a) * P, x_t_q, E4M3, n)
+
+        def out_1_copy(g, z, n, a, engine):
+            move(engine, stage_for(("stage_1", g, z, n))[:, a, :], held["ps_1", g, z, n, a][:])
+
+        def out_1_store(g, z, n):
+            nc.sync.dma_start(out=out_1_hbm[g][:, 2 * z : 2 * z + 2, half(n)], in_=held["stage_1", g, z, n][:])
+
+        steps = {
+            "Lr": load_w_rg,
+            "Lh": load_w_hid,
+            "Ly": load_y,
+            "Lm": load_mem,
+            "Lg": load_grad,
+            "Lx": load_x,
+            "Sy": square_y,
+            "Sm": square_mem,
+            "Zz": make_dz2,
+            "Ih": interleave_w_hid,
+            "Ir": interleave_w_rg,
+            "I1": interleave_dz1,
+            "Hp": hidden_pass,
+            "Dz": make_dz1,
+            "Qh": lambda k, c: quantize(w_hid_q, E4M3, k, c, held["w_hid", k, c]),
+            "Qr": lambda k, c: quantize(w_rg_q, E4M3, k, c, held["w_rg", k, c]),
+            "Qz": lambda k, h: quantize(dz2_q, E5M2, k, h, held["dz2", k, h]),
+            "Q1": lambda g, h: quantize(dz1_q, E5M2, g, h, held["dz1", g, h]),
+            "Qt": lambda h, g: quantize(dz1_t_q, E5M2, h, g, held[("dz1_t", g), h]),
+            "Qx": lambda h, n: quantize(x_t_q, E4M3, h, n, held[("x_t", n), h]),
+            "Tt": lambda g, h, z: transpose(("dz1_t", g), dz1[g], h, z),
+            "Cc": lambda g, h, z, engine: copy_transposed(("dz1_t", g), h, z, engine),
+            "Xt": lambda n, h, z: transpose(("x_t", n), held["x_raw", n], h, z),
+            "Xc": lambda n, h, z, engine: copy_transposed(("x_t", n), h, z, engine),
+            "P0": out_0_product,
+            "E0": out_0_copy,
+            "W0": out_0_store,
+            "P1": out_1_product,
+            "E1": out_1_copy,
+            "W1": out_1_store,
+        }
+
+        nc.vector.memset(minus_half[:], -0.5)
+        make_identity(nc, ident[:])
+
+        with tc.manual_schedule():
+            for step in ORDER.split():
+                arguments = [int(c) if c in "0123" else c for c in step[2:]]
+                steps[step[:2]](*arguments)

@@ -16,51 +16,46 @@ SIZE = 1024
 P = 128
 PACK = 4
 HALF = 512
+QUARTER = 256
+SLABS = 7
+GROUPED = 4
+TURNED = 4
+MEMSQ = 4
+HALVES = 2
 
 FLOPS = 3 * 2 * SIZE * SIZE * SIZE
 BYTES = 4 * SIZE * SIZE * 2 + 2 * SIZE * SIZE * 4 + 2 * SIZE * SIZE * 4
-
-ORDER = """
-Lh0 Lh1 Ly00 Lg00 Ly10 Lg10 Lr0
-Ih00V Ih11S Ih01V Ih10V Qh00 Qh01 Qh10 Qh11
-Lr1 Lm00 Lm10 Lx0
-Sy00 Zz00 Qz00 Hp0000 Hp0001 Hp0002 Hp0003 Hp0100 Hp0101 Hp0102 Hp0103 Ly01 Lg01 Sy10 Zz10 Ir00S Ir01V Ir10V Qz10 Hp1000 Hp1001 Hp1002 Hp1003 Ir11S Qr00 Qr01 Qr10 Qr11
-Ly11 Lg11 Lx1 Sm00 Hp1100 Hp1101 Hp1102 Hp1103 Dz000 Dz001 Dz002 Dz003 Lm01 Sm10 Tt000 Xt000 Cc000S I100S Dz100 Dz101 Dz102 Dz103 Lm11 Tt001 Xt001 Tt100 Tt101
-Sy01 Xc000V Q100 I110V Cc001V Xc001S Q110 Cc101V Sy11 Cc100S
-P0000 P0001 P0010 P0011 E0000S E0010S Zz01 Zz11 Xt011 Xc011S P0020 P0021 E0001V W000 E0011S W001 E0020S Qz01 Qz11 E0021S W002 Sm01
-P0030 P0031 Xt110 Xt111 Xt010 E0030S Qt00 Qt01 Xc110S Xc111S Sm11 Xc010V E0031V W003
-Hp0010 Hp1010 Dz010 Hp0011 Hp1011 Dz011 Hp0012 Hp1012 Dz012 Hp0013 Hp1013 Dz013 Qx00 Qx10
-Hp0110 Hp1110 Xt100 Tt010 Tt011 Xt101 Cc010V Cc011S Dz110 Qt10 Xc100S Xc101S Qx01 Qx11 Hp0111 Hp0112 Hp0113 Hp1111 Hp1112 Hp1113 I101S Dz111 Dz112 Dz113
-P10000 P10001 P10100 P10101 E10000S E10001S W1000 E10100S E10101S W1010 I111V P10010 P10011 P10110 P10111 Q101 Q111 E10010S E10011S W1001 E10110S E10111V W1011
-Tt110 Tt111 Cc110S P0100 P0101 P0110 Cc111V E0100S E0101V W010 P0111 E0110S E0111V W011 P0120 P0121 Qt11 E0120S E0121V W012 P0130 P0131 E0130S E0131V W013
-P11000 P11001 E11000S E11001V W1100 P11100 P11101 E11100S E11101V W1110 P11010 P11011 E11010S E11011V W1101 P11110 P11111 E11110S E11111V W1111
-"""
 
 
 def tile_pt_grumb_pb_v_kernel(
     tc, x, out0, mem0, inp_out, w_readgate, w_rec_readgate, w_mem_readgate, w_hid_out, mem_out, y, grad_out, out_0, out_1
 ):
     nc = tc.nc
-    w_hid_hbm = w_hid_out.rearrange("(k p j) m -> k p j m", p=P, j=PACK)
-    w_rg_hbm = w_readgate.rearrange("(k p j) i -> k p j i", p=P, j=PACK)
-    y_hbm = y.rearrange("(k p j) b -> k p j b", p=P, j=PACK)
-    grad_hbm = grad_out.rearrange("(k p j) b -> k p j b", p=P, j=PACK)
-    mem_hbm = mem_out.rearrange("(g p t) b -> g p t b", p=P, t=PACK)
-    x_hbm = x.rearrange("(n a p) b -> n p a b", p=P, a=PACK)
-    out_0_hbm = out_0.rearrange("(z a p) b -> z p a b", p=P, a=2)
-    out_1_hbm = out_1.rearrange("(g p t) i -> g p t i", p=P, t=PACK)
+
+    def rows_by_four(hbm):
+        return hbm.rearrange("(k p j) c -> k p j c", p=P, j=PACK)
+
+    w_hid_hbm = rows_by_four(w_hid_out)
+    w_rg_hbm = rows_by_four(w_readgate)
+    y_hbm = rows_by_four(y)
+    grad_hbm = rows_by_four(grad_out)
+    mem_hbm = rows_by_four(mem_out)
+    x_hbm = rows_by_four(x)
+    out_0_hbm = rows_by_four(out_0)
+    out_1_hbm = rows_by_four(out_1)
 
     with ExitStack() as ctx:
         keep = ctx.enter_context(tc.tile_pool(name="keep", bufs=1))
-        raw = ctx.enter_context(tc.tile_pool(name="raw", bufs=1))
         work = ctx.enter_context(tc.tile_pool(name="work", bufs=1))
-        psum = ctx.enter_context(tc.psum_pool(name="psum", bufs=8))
+        psum = ctx.enter_context(tc.psum_pool(name="psum", bufs=1))
 
         def keep_tile(shape, dtype, name):
             return keep.tile(shape, dtype, name=name, tag=name, align_bytes=64)
 
         def codes_pair(name):
-            return keep_tile([P, 2, SIZE], U32, name + "_codes"), keep_tile([P, 2, SIZE], U8, name + "_scales")
+            codes = [keep_tile([P, SIZE], U32, "%s_codes_%d" % (name, k)) for k in range(2)]
+            scales = [keep_tile([P, SIZE], U8, "%s_scales_%d" % (name, k)) for k in range(2)]
+            return codes, scales
 
         w_hid_q = codes_pair("w_hid")
         w_rg_q = codes_pair("w_rg")
@@ -68,34 +63,43 @@ def tile_pt_grumb_pb_v_kernel(
         dz1_q = codes_pair("dz1")
         dz1_t_q = codes_pair("dz1_t")
         x_t_q = codes_pair("x_t")
-        dz1 = [keep_tile([P, PACK, SIZE], BF16, "dz1_%d" % g) for g in range(2)]
+        dz1 = [[keep_tile([P, PACK, HALF], BF16, "dz1_%d_%d" % (g, h)) for h in range(2)] for g in range(2)]
         ident = keep_tile([P, P], F32, "ident")
+        ident_bf16 = keep_tile([P, P], BF16, "ident_bf16")
         minus_half = keep_tile([P, 1], F32, "minus_half")
         held = {}
 
-        def raw_tile(shape, dtype, tag, bufs):
-            return raw.tile(shape, dtype, name=tag, tag=tag, align_bytes=64, bufs=bufs)
+        def work_tile(shape, dtype, tag, bufs):
+            return work.tile(shape, dtype, name=tag, tag=tag, align_bytes=64, bufs=bufs)
+
+        def slab(shape):
+            return work_tile(shape, F32, "slab", SLABS)
 
         def grouped_tile():
-            return work.tile([P, HALF, PACK], BF16, name="grouped", tag="grouped", align_bytes=64, bufs=8)
+            return work_tile([P, HALF, PACK], BF16, "grouped", GROUPED)
 
-        def bank(shape):
-            return psum.tile(shape, F32, name="bank", tag="bank")
+        def bank(side, shape, dtype=F32):
+            return psum.tile(shape, dtype, name="bank_%d" % side, tag="bank_%d" % side)
 
         def half(n):
             return slice(n * HALF, (n + 1) * HALF)
 
+        def pair(z):
+            return slice(2 * z, 2 * z + 2)
+
         def move(engine, out, in_):
             if engine == "S":
                 nc.scalar.copy(out=out, in_=in_)
+            elif engine == "G":
+                nc.gpsimd.tensor_scalar(out=out, in0=in_, scalar1=1.0, scalar2=-0.0, op0=ALU.mult, op1=ALU.add)
             else:
                 nc.vector.tensor_copy(out=out, in_=in_)
 
-        def quantize(pair, dtype, row, col, grouped):
-            codes, scales = pair
+        def quantize(operand, dtype, k, col, grouped):
+            codes, scales = operand
             nc.vector.quantize_mx(
-                out=codes[:, row, half(col)].bitcast(dtype),
-                scales=scales[:, row, half(col)],
+                out=codes[k][:, half(col)].bitcast(dtype),
+                scales=scales[k][:, half(col)],
                 in_=grouped[:].rearrange("p n j -> p (n j)"),
             )
 
@@ -103,189 +107,396 @@ def tile_pt_grumb_pb_v_kernel(
             lhs_cols = slice(lhs_first, lhs_first + P)
             nc.tensor.matmul_mx(
                 out=out,
-                lhsT=lhs[0][:, k, lhs_cols].bitcast(lhs_dtype),
-                lhsT_scale=lhs[1][:, k, lhs_cols],
-                rhs=rhs[0][:, k, half(rhs_half)].bitcast(rhs_dtype),
-                rhs_scale=rhs[1][:, k, half(rhs_half)],
+                lhsT=lhs[0][k][:, lhs_cols].bitcast(lhs_dtype),
+                lhsT_scale=lhs[1][k][:, lhs_cols],
+                rhs=rhs[0][k][:, half(rhs_half)].bitcast(rhs_dtype),
+                rhs_scale=rhs[1][k][:, half(rhs_half)],
                 start=(k == 0),
                 stop=(k == 1),
             )
 
-        def load_weight(key, hbm, k, pieces):
-            held[key, k] = raw_tile([P, PACK, SIZE], BF16, "w_raw", 3)
-            for cols in pieces:
-                nc.sync.dma_start(out=held[key, k][:, :, cols], in_=hbm[k][:, :, cols])
+        def load_rows(key, hbm, k, tag, bufs):
+            held[key, k] = work_tile([P, PACK, SIZE], BF16, tag, bufs)
+            nc.sync.dma_start(out=held[key, k][:], in_=hbm[k])
+
+        def load_halves(key, hbm, k, c, tag, bufs):
+            held[key, k, c] = work_tile([P, PACK, HALF], BF16, tag, bufs)
+            nc.sync.dma_start(out=held[key, k, c][:], in_=hbm[k][:, :, half(c)])
+
+        def whole(key, k):
+            for c in range(2):
+                held[key, k, c] = held[key, k][:, :, half(c)]
 
         def load_w_hid(k):
-            load_weight("w_hid_raw", w_hid_hbm, k, [half(0), half(1)] if k == 0 else [slice(0, SIZE)])
+            load_rows("w_hid_raw", w_hid_hbm, k, "w_raw", 2)
+            whole("w_hid_raw", k)
+
+        def load_w_hid_half(k, c):
+            load_halves("w_hid_raw", w_hid_hbm, k, c, "half_raw", HALVES)
+
+        def load_grad_half(k, h):
+            load_halves("grad_raw", grad_hbm, k, h, "half_raw", HALVES)
 
         def load_w_rg(k):
-            load_weight("w_rg_raw", w_rg_hbm, k, [slice(0, SIZE)])
+            load_rows("w_rg_raw", w_rg_hbm, k, "w_raw", 2)
+            whole("w_rg_raw", k)
 
-        def load_part(key, hbm, dtype, tag, bufs, k, h):
-            held[key, k, h] = raw_tile([P, PACK, HALF], dtype, tag, bufs)
-            nc.sync.dma_start(out=held[key, k, h][:], in_=hbm[k][:, :, half(h)])
-
-        def load_y(k, h):
-            load_part("y_raw", y_hbm, F32, "f32_raw", 4, k, h)
-
-        def load_mem(g, h):
-            load_part("mem_raw", mem_hbm, F32, "f32_raw", 4, g, h)
-
-        def load_grad(k, h):
-            load_part("grad_raw", grad_hbm, BF16, "grad_raw", 4, k, h)
+        def load_grad(k):
+            load_rows("grad_raw", grad_hbm, k, "grad_x_raw", 3)
+            whole("grad_raw", k)
 
         def load_x(n):
-            held["x_raw", n] = raw_tile([P, PACK, SIZE], BF16, "x_raw", 2)
-            nc.sync.dma_start(out=held["x_raw", n][:], in_=x_hbm[n])
+            load_rows("x_raw", x_hbm, n, "x_raw", 2)
 
-        def square_y(k, h):
-            t = work.tile([P, HALF, PACK], F32, name="y_squared", tag="y_squared", align_bytes=64, bufs=2)
+        def load_y(k, h):
+            held["y_raw", k, h] = slab([P, PACK, HALF])
+            nc.sync.dma_start(out=held["y_raw", k, h][:], in_=y_hbm[k][:, :, half(h)])
+
+        def load_mem(g, h):
+            held["mem_raw", g, h] = slab([P, PACK, HALF])
+            nc.sync.dma_start(out=held["mem_raw", g, h][:], in_=mem_hbm[g][:, :, half(h)])
+
+        def square_y(k, h, u):
+            t = work_tile([P, P, 2, PACK], F32, "y_squared", 3)
             nc.scalar.activation(
-                out=t[:].rearrange("p (c i) j -> p c j i", i=4),
-                in_=held["y_raw", k, h][:].rearrange("p j (c i) -> p c j i", i=4),
+                out=t[:].rearrange("p w e j -> p w j e"),
+                in_=held["y_raw", k, h][:].rearrange("p j (w u e) -> p u w j e", u=2, e=2)[:, u],
                 func=ACT.Square,
             )
-            held["y_squared", k, h] = t
+            held["y_squared", k, h, u] = t
 
-        def square_mem(g, h):
-            t = held["mem_raw", g, h]
-            nc.scalar.activation(out=t[:], in_=t[:], func=ACT.Square, bias=minus_half[:])
+        def park_grad(k, h, u, side):
+            ps = bank(side, [P, PACK, P, 2], BF16)
+            source = held["grad_raw", k, h][:].rearrange("p j (w u e) -> p u j w e", u=2, e=2)[:, u]
+            for z in range(2):
+                nc.tensor.matmul(out=ps[:, pair(z)], lhsT=ident_bf16[:], rhs=source[:, pair(z)], start=True, stop=True)
+            held["grad_ps", k, h, u] = ps
 
-        def make_dz2(k, h):
-            grouped = grouped_tile()
+        def make_dz2(k, h, u):
+            if u == 0:
+                held["dz2", k, h] = grouped_tile()
             nc.vector.scalar_tensor_tensor(
-                out=grouped[:],
-                in0=held["y_squared", k, h][:],
+                out=held["dz2", k, h][:, u * QUARTER : (u + 1) * QUARTER, :],
+                in0=held["y_squared", k, h, u][:].rearrange("p w e j -> p (w e) j"),
                 scalar=1.0,
-                in1=held["grad_raw", k, h][:].rearrange("p j b -> p b j"),
+                in1=held["grad_ps", k, h, u][:].rearrange("p j w e -> p (w e) j"),
                 op0=ALU.subtract,
                 op1=ALU.mult,
             )
-            held["dz2", k, h] = grouped
 
-        def interleave_w_hid(k, c, engine):
+        def square_mem(g, h, z):
+            sq = work_tile([P, 2, 2, QUARTER], F32, "mem_squared", MEMSQ)
+            nc.scalar.activation(
+                out=sq[:].rearrange("p u a (w e) -> p u (a w) e", e=2),
+                in_=held["mem_raw", g, h][:, pair(z), :].rearrange("p a (w u e) -> p u (a w) e", u=2, e=2),
+                func=ACT.Square,
+                bias=minus_half[:],
+            )
+            held["mem_squared", g, h, z] = sq
+
+        def interleave_weight(key, k, c, engine):
             grouped = grouped_tile()
             move(
                 engine,
-                grouped[:].rearrange("p (t m) j -> p t m j", t=PACK),
-                held["w_hid_raw", k][:, :, half(c)].rearrange("p j (m t) -> p t m j", t=PACK),
+                grouped[:].rearrange("p (t m) j -> p m j t", t=PACK),
+                held[key + "_raw", k, c][:].rearrange("p j (m t) -> p m j t", t=PACK),
             )
-            held["w_hid", k, c] = grouped
+            held[key, k, c] = grouped
 
-        def interleave(engine, source):
+        def interleave_dz1(g, h, engine):
             grouped = grouped_tile()
             move(
                 engine,
                 grouped[:].rearrange("p (c i) j -> p c j i", i=4),
-                source.rearrange("p j (c i) -> p c j i", i=4),
+                dz1[g][h][:].rearrange("p j (c i) -> p c j i", i=4),
             )
-            return grouped
+            held["dz1", g, h] = grouped
 
-        def interleave_w_rg(k, c, engine):
-            held["w_rg", k, c] = interleave(engine, held["w_rg_raw", k][:, :, half(c)])
-
-        def interleave_dz1(g, h, engine):
-            held["dz1", g, h] = interleave(engine, dz1[g][:, :, half(h)])
-
-        def hidden_pass(k, g, h, t):
+        def hidden_pass(k, g, h, t, side):
             if k == 0:
-                held["dh", g, h, t] = bank([P, HALF])
+                held["dh", g, h, t] = bank(side, [P, HALF])
             product_pass(k, held["dh", g, h, t][:], w_hid_q, E4M3, g * HALF + t * P, dz2_q, E5M2, h)
 
         def make_dz1(g, h, t):
             nc.vector.scalar_tensor_tensor(
-                out=dz1[g][:, t, half(h)],
-                in0=held["mem_raw", g, h][:, t, :],
+                out=dz1[g][h][:, t, :].rearrange("p (u n) -> p u n", u=2),
+                in0=held["mem_squared", g, h, t // 2][:, :, t % 2, :],
                 scalar=0.25,
-                in1=held["dh", g, h, t][:],
+                in1=held["dh", g, h, t][:].rearrange("p (u n) -> p u n", u=2),
                 op0=ALU.subtract,
                 op1=ALU.mult,
             )
 
-        def transpose(key, source, h, z):
-            words = source[:].rearrange("p a b -> p (a b)").bitcast(F32)
-            ps = bank([P, 2, 2, P])
+        def transpose_dz1(g, h, z, side):
+            words = dz1[g][h][:].rearrange("p t n -> p (t n)").bitcast(F32)
+            ps = bank(side, [P, 2, 2, P])
             for a in range(2):
                 for u in range(2):
-                    first = (2 * z + a) * HALF + h * 2 * P + u
-                    nc.tensor.transpose(ps[:, a, u, :], words[:, first : first + 2 * P - 1 : 2], ident[:])
-            held[key, h, z] = ps
+                    first = (2 * z + a) * QUARTER + u * P
+                    nc.tensor.transpose(ps[:, a, u, :], words[:, first : first + P], ident[:])
+            held["dz1_t_ps", g, h, z] = ps
 
-        def copy_transposed(key, h, z, engine):
-            if (key, h) not in held:
-                held[key, h] = grouped_tile()
-            words = held[key, h][:].rearrange("p n j -> p (n j)").bitcast(F32)
+        def transpose_x(n, h, z, side):
+            words = held["x_raw", n][:].rearrange("p a b -> p (a b)").bitcast(F32)
+            ps = bank(side, [P, 2, 2, P])
+            for a in range(2):
+                for u in range(2):
+                    first = (2 * z + a) * HALF + h * QUARTER + u
+                    nc.tensor.transpose(ps[:, a, u, :], words[:, first : first + QUARTER - 1 : 2], ident[:])
+            held["x_t_ps", n, h, z] = ps
+
+        def grouped_words(key, z):
+            if z == 0:
+                tag, bufs = ("turned_kept", 1) if key == ("dz1_t", 1, 0) else ("turned", TURNED)
+                held[key] = work_tile([P, HALF, PACK], BF16, tag, bufs)
+            return held[key][:].rearrange("p n j -> p (n j)").bitcast(F32)
+
+        def copy_dz1_t(g, h, z, engine):
+            words = grouped_words(("dz1_t", g, h), z)
             move(
                 engine,
                 words[:, half(z)].rearrange("p (a r u) -> p a r u", a=2, u=2),
-                held[key, h, z][:].rearrange("p a u r -> p a r u"),
+                held["dz1_t_ps", g, h, z][:].rearrange("p a u r -> p a r u"),
             )
 
-        def stage_for(key):
+        def copy_x_t(n, h, z, engine):
+            words = grouped_words(("x_t", n, h), z)
+            move(
+                engine,
+                words.rearrange("p (r z a u) -> p z r a u", z=2, a=2, u=2)[:, z],
+                held["x_t_ps", n, h, z][:].rearrange("p a u r -> p r a u"),
+            )
+
+        def quantize_w_hid(k, c):
+            quantize(w_hid_q, E4M3, k, c, held["w_hid", k, c])
+
+        def quantize_w_rg(k, c):
+            quantize(w_rg_q, E4M3, k, c, held["w_rg", k, c])
+
+        def interleave_w_rg_pair(k, c, z):
+            grouped = work_tile([P, QUARTER, PACK], BF16, "grouped", GROUPED)
+            nc.vector.tensor_copy(
+                out=grouped[:].rearrange("p (a m) j -> p m j a", a=2),
+                in_=held["w_rg_raw", k, c][:].rearrange("p j (m t) -> p m j t", t=PACK)[:, :, :, pair(z)],
+            )
+            held["w_rg", k, c, z] = grouped
+
+        def quantize_w_rg_pair(k, c, z):
+            cols = slice(c * HALF + z * QUARTER, c * HALF + (z + 1) * QUARTER)
+            nc.vector.quantize_mx(
+                out=w_rg_q[0][k][:, cols].bitcast(E4M3),
+                scales=w_rg_q[1][k][:, cols],
+                in_=held["w_rg", k, c, z][:].rearrange("p n j -> p (n j)"),
+            )
+
+        def quantize_dz2(k, h):
+            quantize(dz2_q, E5M2, k, h, held["dz2", k, h])
+
+        def quantize_dz1(g, h):
+            quantize(dz1_q, E5M2, g, h, held["dz1", g, h])
+
+        def quantize_dz1_t(g, h):
+            quantize(dz1_t_q, E5M2, h, g, held["dz1_t", g, h])
+
+        def quantize_x_t(n, h):
+            quantize(x_t_q, E4M3, h, n, held["x_t", n, h])
+
+        def stage_for(key, shape):
             if key not in held:
-                held[key] = work.tile([P, 2, HALF], F32, name="stage", tag="stage", align_bytes=64, bufs=5)
+                held[key] = slab(shape)
             return held[key]
 
-        def out_0_product(h, z, a):
-            held["ps_0", h, z, a] = bank([P, HALF])
+        def out_0_product(c, t, h, side):
+            held["ps_0", c, t, h] = bank(side, [P, HALF])
             for k in range(2):
-                product_pass(k, held["ps_0", h, z, a][:], w_rg_q, E4M3, (2 * z + a) * P, dz1_q, E5M2, h)
+                product_pass(k, held["ps_0", c, t, h][:], w_rg_q, E4M3, c * HALF + t * P, dz1_q, E5M2, h)
 
-        def out_0_copy(h, z, a, engine):
-            move(engine, stage_for(("stage_0", h, z))[:, a, :], held["ps_0", h, z, a][:])
+        def out_0_copy(c, t, h, engine):
+            move(
+                engine,
+                stage_for(("stage_0", c, t // 2), [P, 2, SIZE])[:, t % 2, half(h)].rearrange("p (w u e) -> p w u e", u=2, e=2),
+                held["ps_0", c, t, h][:].rearrange("p (u w e) -> p w u e", u=2, e=2),
+            )
 
-        def out_0_store(h, z):
-            nc.sync.dma_start(out=out_0_hbm[z][:, :, half(h)], in_=held["stage_0", h, z][:])
-
-        def out_1_product(g, z, n, a):
-            held["ps_1", g, z, n, a] = bank([P, HALF])
+        def out_1_product(g, t, n, side):
+            held["ps_1", g, t, n] = bank(side, [P, HALF])
             for k in range(2):
-                product_pass(k, held["ps_1", g, z, n, a][:], dz1_t_q, E5M2, g * HALF + (2 * z + a) * P, x_t_q, E4M3, n)
+                product_pass(k, held["ps_1", g, t, n][:], dz1_t_q, E5M2, g * HALF + t * P, x_t_q, E4M3, n)
 
-        def out_1_copy(g, z, n, a, engine):
-            move(engine, stage_for(("stage_1", g, z, n))[:, a, :], held["ps_1", g, z, n, a][:])
+        def out_1_copy(g, t, n, engine):
+            move(engine, stage_for(("stage_1", g, t // 2), [P, 2, SIZE])[:, t % 2, half(n)], held["ps_1", g, t, n][:])
 
-        def out_1_store(g, z, n):
-            nc.sync.dma_start(out=out_1_hbm[g][:, 2 * z : 2 * z + 2, half(n)], in_=held["stage_1", g, z, n][:])
-
-        steps = {
-            "Lr": load_w_rg,
-            "Lh": load_w_hid,
-            "Ly": load_y,
-            "Lm": load_mem,
-            "Lg": load_grad,
-            "Lx": load_x,
-            "Sy": square_y,
-            "Sm": square_mem,
-            "Zz": make_dz2,
-            "Ih": interleave_w_hid,
-            "Ir": interleave_w_rg,
-            "I1": interleave_dz1,
-            "Hp": hidden_pass,
-            "Dz": make_dz1,
-            "Qh": lambda k, c: quantize(w_hid_q, E4M3, k, c, held["w_hid", k, c]),
-            "Qr": lambda k, c: quantize(w_rg_q, E4M3, k, c, held["w_rg", k, c]),
-            "Qz": lambda k, h: quantize(dz2_q, E5M2, k, h, held["dz2", k, h]),
-            "Q1": lambda g, h: quantize(dz1_q, E5M2, g, h, held["dz1", g, h]),
-            "Qt": lambda h, g: quantize(dz1_t_q, E5M2, h, g, held[("dz1_t", g), h]),
-            "Qx": lambda h, n: quantize(x_t_q, E4M3, h, n, held[("x_t", n), h]),
-            "Tt": lambda g, h, z: transpose(("dz1_t", g), dz1[g], h, z),
-            "Cc": lambda g, h, z, engine: copy_transposed(("dz1_t", g), h, z, engine),
-            "Xt": lambda n, h, z: transpose(("x_t", n), held["x_raw", n], h, z),
-            "Xc": lambda n, h, z, engine: copy_transposed(("x_t", n), h, z, engine),
-            "P0": out_0_product,
-            "E0": out_0_copy,
-            "W0": out_0_store,
-            "P1": out_1_product,
-            "E1": out_1_copy,
-            "W1": out_1_store,
-        }
+        def store(key, hbm, c, first, count):
+            rows = slice(first % 2, first % 2 + count)
+            nc.sync.dma_start(out=hbm[c][:, first : first + count, :], in_=held[key, c, first // 2][:, rows, :])
 
         nc.vector.memset(minus_half[:], -0.5)
+        make_identity(nc, ident_bf16[:])
         make_identity(nc, ident[:])
 
         with tc.manual_schedule():
-            for step in ORDER.split():
-                arguments = [int(c) if c in "0123" else c for c in step[2:]]
-                steps[step[:2]](*arguments)
+            def both(fn, *args):
+                for u in range(2):
+                    fn(*args, u)
+
+            def hidden(g, h, side):
+                for t in range(4):
+                    for k in range(2):
+                        hidden_pass(k, g, h, t, side)
+
+            def dz1_quarter(g, h):
+                for t in range(4):
+                    make_dz1(g, h, t)
+
+            load_w_hid(0)
+            load_y(0, 0)
+            load_grad_half(0, 0)
+            load_y(1, 0)
+            load_grad_half(1, 0)
+            load_w_hid(1)
+            load_mem(0, 0)
+            load_mem(1, 0)
+
+            for c in range(2):
+                interleave_weight("w_hid", 0, c, "V")
+            for c in range(2):
+                quantize_w_hid(0, c)
+            for k in range(2):
+                for u in range(2):
+                    square_y(k, 0, u)
+                    park_grad(k, 0, u, 4 + 2 * k + u)
+                both(make_dz2, k, 0)
+                if k == 0:
+                    quantize_dz2(0, 0)
+            for k in range(2):
+                load_y(k, 1)
+                load_grad_half(k, 1)
+            load_x(0)
+            load_mem(0, 1)
+            load_x(1)
+            for g in range(2):
+                for t in range(4):
+                    hidden_pass(0, g, 0, t, 4 * g + t)
+            interleave_weight("w_hid", 1, 0, "V")
+            interleave_weight("w_hid", 1, 1, "S")
+            load_mem(1, 1)
+            load_w_rg(0)
+            load_w_rg(1)
+            quantize_dz2(1, 0)
+            for g in range(2):
+                quantize_w_hid(1, g)
+            for g in range(2):
+                for t in range(4):
+                    hidden_pass(1, g, 0, t, None)
+            for g in range(2):
+                both(square_mem, g, 0)
+                dz1_quarter(g, 0)
+            for z in range(2):
+                transpose_dz1(0, 0, z, z)
+            for u in range(2):
+                square_y(0, 1, u)
+                park_grad(0, 1, u, 2 + u)
+            for z in range(2):
+                transpose_dz1(1, 0, z, 4 + z)
+            for z in range(2):
+                copy_dz1_t(0, 0, z, "S")
+            both(make_dz2, 0, 1)
+            for u in range(2):
+                square_y(1, 1, u)
+                park_grad(1, 1, u, 6 + u)
+            for z in range(2):
+                copy_dz1_t(1, 0, z, "S")
+            interleave_dz1(0, 0, "V")
+            quantize_dz2(0, 1)
+            both(make_dz2, 1, 1)
+            quantize_dz1_t(0, 0)
+            quantize_dz2(1, 1)
+            for t in range(4):
+                hidden_pass(0, 0, 1, t, t)
+            for z in range(2):
+                transpose_x(0, 0, z, 4 + z)
+                copy_x_t(0, 0, z, "S")
+            for t in range(2):
+                hidden_pass(0, 1, 1, t, 6 + t)
+            for t in range(4):
+                hidden_pass(1, 0, 1, t, None)
+            for z in range(2):
+                transpose_x(0, 1, z, 4 + z)
+            interleave_dz1(1, 0, "V")
+            both(square_mem, 0, 1)
+            dz1_quarter(0, 1)
+            for z in range(2):
+                copy_x_t(0, 1, z, "S")
+            for t in range(2):
+                hidden_pass(1, 1, 1, t, None)
+            for z in range(2):
+                transpose_x(1, 0, z, z)
+                copy_x_t(1, 0, z, "S")
+            for z in range(2):
+                transpose_dz1(0, 1, z, 2 + z)
+            for z in range(2):
+                transpose_x(1, 1, z, 4 + z)
+            for t in range(2, 4):
+                for k in range(2):
+                    hidden_pass(k, 1, 1, t, t - 2)
+            quantize_x_t(0, 0)
+            quantize_x_t(0, 1)
+            for z in range(2):
+                copy_dz1_t(0, 1, z, "V")
+            quantize_x_t(1, 0)
+            quantize_dz1_t(0, 1)
+            square_mem(1, 1, 0)
+            for z in range(2):
+                copy_x_t(1, 1, z, "S")
+            square_mem(1, 1, 1)
+            for t in range(2):
+                out_1_product(0, t, 0, 2 + t)
+            for t in range(2):
+                make_dz1(1, 1, t)
+            quantize_x_t(1, 1)
+            for t in range(2, 4):
+                make_dz1(1, 1, t)
+            for t in range(2):
+                out_1_product(0, t, 1, 4 + t)
+            for t in range(2):
+                for n in range(2):
+                    out_1_copy(0, t, n, "S")
+                store("stage_1", out_1_hbm, 0, t, 1)
+            for n in range(2):
+                out_1_product(0, 2, n, 6 + n)
+            for z in range(2):
+                transpose_dz1(1, 1, z, z)
+            for n in range(2):
+                out_1_product(0, 3, n, 2 + n)
+            quantize_dz1(0, 0)
+            quantize_dz1_t(1, 0)
+            for z in range(2):
+                copy_dz1_t(1, 1, z, "V")
+            quantize_dz1(1, 0)
+            for t in range(2, 4):
+                for n in range(2):
+                    out_1_copy(0, t, n, "S")
+                store("stage_1", out_1_hbm, 0, t, 1)
+            quantize_dz1_t(1, 1)
+            for t in range(4):
+                for n in range(2):
+                    out_1_product(1, t, n, (4 + 2 * t + n) % 8)
+                    out_1_copy(1, t, n, "S")
+                store("stage_1", out_1_hbm, 1, t, 1)
+            for g in range(2):
+                interleave_dz1(g, 1, "V")
+            for g in range(2):
+                quantize_dz1(g, 1)
+            for c in range(2):
+                for z in range(2):
+                    for k in range(2):
+                        interleave_w_rg_pair(k, c, z)
+
+                    for k in range(2):
+                        quantize_w_rg_pair(k, c, z)
+            for c in range(2):
+                for t in range(4):
+                    for h in range(2):
+                        out_0_product(c, t, h, (4 + 2 * t + h) % 8)
+                        out_0_copy(c, t, h, "V" if h and 4 * c + t >= 6 else "S")
+                    store("stage_0", out_0_hbm, c, t, 1)

@@ -19,7 +19,7 @@ HALF = 512
 QUARTER = 256
 SLABS = 7
 GROUPED = 4
-TURNED = 4
+TURNED = 3
 MEMSQ = 4
 HALVES = 2
 
@@ -90,8 +90,6 @@ def tile_pt_grumb_pb_v_kernel(
         def move(engine, out, in_):
             if engine == "S":
                 nc.scalar.copy(out=out, in_=in_)
-            elif engine == "G":
-                nc.gpsimd.tensor_scalar(out=out, in0=in_, scalar1=1.0, scalar2=-0.0, op0=ALU.mult, op1=ALU.add)
             else:
                 nc.vector.tensor_copy(out=out, in_=in_)
 
@@ -212,6 +210,18 @@ def tile_pt_grumb_pb_v_kernel(
             )
             held["dz1", g, h] = grouped
 
+        def interleave_dz1_on_gpsimd(g, h, tag, bufs):
+            grouped = work_tile([P, HALF, PACK], BF16, tag, bufs)
+            nc.gpsimd.tensor_scalar(
+                out=grouped[:],
+                in0=dz1[g][h][:].rearrange("p j c -> p c j"),
+                scalar1=1.0,
+                scalar2=-0.0,
+                op0=ALU.mult,
+                op1=ALU.add,
+            )
+            held["dz1", g, h] = grouped
+
         def hidden_pass(k, g, h, t, side):
             if k == 0:
                 held["dh", g, h, t] = bank(side, [P, HALF])
@@ -247,7 +257,8 @@ def tile_pt_grumb_pb_v_kernel(
 
         def grouped_words(key, z):
             if z == 0:
-                tag, bufs = ("turned_kept", 1) if key == ("dz1_t", 1, 0) else ("turned", TURNED)
+                own_tags = {("dz1_t", 1, 0): "turned_kept", ("x_t", 1, 1): "handed_on"}
+                tag, bufs = (own_tags[key], 1) if key in own_tags else ("turned", TURNED)
                 held[key] = work_tile([P, HALF, PACK], BF16, tag, bufs)
             return held[key][:].rearrange("p n j -> p (n j)").bitcast(F32)
 
@@ -391,6 +402,7 @@ def tile_pt_grumb_pb_v_kernel(
             for g in range(2):
                 both(square_mem, g, 0)
                 dz1_quarter(g, 0)
+                interleave_dz1_on_gpsimd(g, 0, "grouped", GROUPED)
             for z in range(2):
                 transpose_dz1(0, 0, z, z)
             for u in range(2):
@@ -406,58 +418,56 @@ def tile_pt_grumb_pb_v_kernel(
                 park_grad(1, 1, u, 6 + u)
             for z in range(2):
                 copy_dz1_t(1, 0, z, "S")
-            interleave_dz1(0, 0, "V")
             quantize_dz2(0, 1)
             both(make_dz2, 1, 1)
             quantize_dz1_t(0, 0)
             quantize_dz2(1, 1)
-            for t in range(4):
+            for t in range(2):
                 hidden_pass(0, 0, 1, t, t)
             for z in range(2):
                 transpose_x(0, 0, z, 4 + z)
                 copy_x_t(0, 0, z, "S")
-            for t in range(2):
-                hidden_pass(0, 1, 1, t, 6 + t)
+            for t in range(2, 4):
+                hidden_pass(0, 0, 1, t, t)
+            for z in range(2):
+                transpose_x(0, 1, z, 6 + z)
+                copy_x_t(0, 1, z, "SS"[z])
             for t in range(4):
                 hidden_pass(1, 0, 1, t, None)
-            for z in range(2):
-                transpose_x(0, 1, z, 4 + z)
-            interleave_dz1(1, 0, "V")
+            for t in range(2):
+                hidden_pass(0, 1, 1, t, 6 + t)
+            for g in range(2):
+                quantize_dz1(g, 0)
+            for h in range(2):
+                quantize_x_t(0, h)
             both(square_mem, 0, 1)
             dz1_quarter(0, 1)
             for z in range(2):
-                copy_x_t(0, 1, z, "S")
+                transpose_x(1, 0, z, 4 + z)
+                copy_x_t(1, 0, z, "S")
             for t in range(2):
                 hidden_pass(1, 1, 1, t, None)
             for z in range(2):
-                transpose_x(1, 0, z, z)
-                copy_x_t(1, 0, z, "S")
-            for z in range(2):
-                transpose_dz1(0, 1, z, 2 + z)
-            for z in range(2):
-                transpose_x(1, 1, z, 4 + z)
-            for t in range(2, 4):
-                for k in range(2):
-                    hidden_pass(k, 1, 1, t, t - 2)
-            quantize_x_t(0, 0)
-            quantize_x_t(0, 1)
-            for z in range(2):
-                copy_dz1_t(0, 1, z, "V")
+                transpose_x(1, 1, z, z)
             quantize_x_t(1, 0)
-            quantize_dz1_t(0, 1)
+            for z in range(2):
+                copy_x_t(1, 1, z, "V")
             square_mem(1, 1, 0)
             for z in range(2):
-                copy_x_t(1, 1, z, "S")
+                transpose_dz1(0, 1, z, 2 + z)
+                copy_dz1_t(0, 1, z, "S")
             square_mem(1, 1, 1)
-            for t in range(2):
-                out_1_product(0, t, 0, 2 + t)
-            for t in range(2):
-                make_dz1(1, 1, t)
-            quantize_x_t(1, 1)
             for t in range(2, 4):
-                make_dz1(1, 1, t)
+                for k in range(2):
+                    hidden_pass(k, 1, 1, t, 2 + t)
+            quantize_dz1_t(1, 0)
+            quantize_dz1_t(0, 1)
+            quantize_x_t(1, 1)
+
             for t in range(2):
-                out_1_product(0, t, 1, 4 + t)
+                for n in range(2):
+                    out_1_product(0, t, n, 2 * t + n)
+            dz1_quarter(1, 1)
             for t in range(2):
                 for n in range(2):
                     out_1_copy(0, t, n, "S")
@@ -465,38 +475,37 @@ def tile_pt_grumb_pb_v_kernel(
             for n in range(2):
                 out_1_product(0, 2, n, 6 + n)
             for z in range(2):
-                transpose_dz1(1, 1, z, z)
+                transpose_dz1(1, 1, z, 4 + z)
             for n in range(2):
-                out_1_product(0, 3, n, 2 + n)
-            quantize_dz1(0, 0)
-            quantize_dz1_t(1, 0)
+                out_1_product(0, 3, n, n)
+            interleave_dz1(0, 1, "V")
+            for n in range(2):
+                out_1_copy(0, 2, n, "S")
+            store("stage_1", out_1_hbm, 0, 2, 1)
             for z in range(2):
-                copy_dz1_t(1, 1, z, "V")
-            quantize_dz1(1, 0)
-            for t in range(2, 4):
-                for n in range(2):
-                    out_1_copy(0, t, n, "S")
-                store("stage_1", out_1_hbm, 0, t, 1)
+                copy_dz1_t(1, 1, z, "VS"[z])
+            for n in range(2):
+                out_1_copy(0, 3, n, "S")
+            store("stage_1", out_1_hbm, 0, 3, 1)
             quantize_dz1_t(1, 1)
+            interleave_dz1(1, 1, "V")
+            quantize_dz1(0, 1)
             for t in range(4):
                 for n in range(2):
-                    out_1_product(1, t, n, (4 + 2 * t + n) % 8)
+                    out_1_product(1, t, n, (2, 6, 4, 0)[t] + n)
                     out_1_copy(1, t, n, "S")
                 store("stage_1", out_1_hbm, 1, t, 1)
-            for g in range(2):
-                interleave_dz1(g, 1, "V")
-            for g in range(2):
-                quantize_dz1(g, 1)
             for c in range(2):
                 for z in range(2):
                     for k in range(2):
                         interleave_w_rg_pair(k, c, z)
-
+                    if c == 0 and z == 0:
+                        quantize_dz1(1, 1)
                     for k in range(2):
                         quantize_w_rg_pair(k, c, z)
             for c in range(2):
                 for t in range(4):
                     for h in range(2):
-                        out_0_product(c, t, h, (4 + 2 * t + h) % 8)
-                        out_0_copy(c, t, h, "V" if h and 4 * c + t >= 6 else "S")
+                        out_0_product(c, t, h, (2, 6, 4, 0)[t] + h)
+                        out_0_copy(c, t, h, "V" if h and 4 * c + t >= 4 else "S")
                     store("stage_0", out_0_hbm, c, t, 1)

@@ -17,7 +17,7 @@ P = 128
 PACK = 4
 HALF = 512
 QUARTER = 256
-SLABS = 7
+SLABS = 6
 GROUPED = 4
 TURNED = 3
 MEMSQ = 4
@@ -72,8 +72,11 @@ def tile_pt_grumb_pb_v_kernel(
         def work_tile(shape, dtype, tag, bufs):
             return work.tile(shape, dtype, name=tag, tag=tag, align_bytes=64, bufs=bufs)
 
+        def dma_tile(shape, dtype, tag, bufs):
+            return work.tile(shape, dtype, name=tag, tag=tag, align_bytes=256, bufs=bufs)
+
         def slab(shape):
-            return work_tile(shape, F32, "slab", SLABS)
+            return dma_tile(shape, F32, "slab", SLABS)
 
         def grouped_tile():
             return work_tile([P, HALF, PACK], BF16, "grouped", GROUPED)
@@ -114,11 +117,11 @@ def tile_pt_grumb_pb_v_kernel(
             )
 
         def load_rows(key, hbm, k, tag, bufs):
-            held[key, k] = work_tile([P, PACK, SIZE], BF16, tag, bufs)
+            held[key, k] = dma_tile([P, PACK, SIZE], BF16, tag, bufs)
             nc.sync.dma_start(out=held[key, k][:], in_=hbm[k])
 
         def load_halves(key, hbm, k, c, tag, bufs):
-            held[key, k, c] = work_tile([P, PACK, HALF], BF16, tag, bufs)
+            held[key, k, c] = dma_tile([P, PACK, HALF], BF16, tag, bufs)
             nc.sync.dma_start(out=held[key, k, c][:], in_=hbm[k][:, :, half(c)])
 
         def whole(key, k):

@@ -50,7 +50,7 @@ def tile_pt_grumb_pb_v_kernel(
         psum = ctx.enter_context(tc.psum_pool(name="psum", bufs=1))
 
         def keep_tile(shape, dtype, name):
-            return keep.tile(shape, dtype, name=name, tag=name, align_bytes=64)
+            return keep.tile(shape, dtype, name=name, tag=name, align_bytes=256)
 
         def codes_pair(name):
             codes = [keep_tile([P, SIZE], U32, "%s_codes_%d" % (name, k)) for k in range(2)]
@@ -70,13 +70,10 @@ def tile_pt_grumb_pb_v_kernel(
         held = {}
 
         def work_tile(shape, dtype, tag, bufs):
-            return work.tile(shape, dtype, name=tag, tag=tag, align_bytes=64, bufs=bufs)
-
-        def dma_tile(shape, dtype, tag, bufs):
             return work.tile(shape, dtype, name=tag, tag=tag, align_bytes=256, bufs=bufs)
 
         def slab(shape):
-            return dma_tile(shape, F32, "slab", SLABS)
+            return work_tile(shape, F32, "slab", SLABS)
 
         def grouped_tile():
             return work_tile([P, HALF, PACK], BF16, "grouped", GROUPED)
@@ -117,11 +114,11 @@ def tile_pt_grumb_pb_v_kernel(
             )
 
         def load_rows(key, hbm, k, tag, bufs):
-            held[key, k] = dma_tile([P, PACK, SIZE], BF16, tag, bufs)
+            held[key, k] = work_tile([P, PACK, SIZE], BF16, tag, bufs)
             nc.sync.dma_start(out=held[key, k][:], in_=hbm[k])
 
         def load_halves(key, hbm, k, c, tag, bufs):
-            held[key, k, c] = dma_tile([P, PACK, HALF], BF16, tag, bufs)
+            held[key, k, c] = work_tile([P, PACK, HALF], BF16, tag, bufs)
             nc.sync.dma_start(out=held[key, k, c][:], in_=hbm[k][:, :, half(c)])
 
         def whole(key, k):
@@ -132,19 +129,12 @@ def tile_pt_grumb_pb_v_kernel(
             load_rows("w_hid_raw", w_hid_hbm, k, "w_raw", 2)
             whole("w_hid_raw", k)
 
-        def load_w_hid_half(k, c):
-            load_halves("w_hid_raw", w_hid_hbm, k, c, "half_raw", HALVES)
-
         def load_grad_half(k, h):
             load_halves("grad_raw", grad_hbm, k, h, "half_raw", HALVES)
 
         def load_w_rg(k):
             load_rows("w_rg_raw", w_rg_hbm, k, "w_raw", 2)
             whole("w_rg_raw", k)
-
-        def load_grad(k):
-            load_rows("grad_raw", grad_hbm, k, "grad_x_raw", 3)
-            whole("grad_raw", k)
 
         def load_x(n):
             load_rows("x_raw", x_hbm, n, "x_raw", 2)
@@ -284,9 +274,6 @@ def tile_pt_grumb_pb_v_kernel(
         def quantize_w_hid(k, c):
             quantize(w_hid_q, E4M3, k, c, held["w_hid", k, c])
 
-        def quantize_w_rg(k, c):
-            quantize(w_rg_q, E4M3, k, c, held["w_rg", k, c])
-
         def interleave_w_rg_pair(k, c, z):
             grouped = work_tile([P, QUARTER, PACK], BF16, "grouped", GROUPED)
             nc.vector.tensor_copy(
@@ -405,7 +392,8 @@ def tile_pt_grumb_pb_v_kernel(
             for g in range(2):
                 both(square_mem, g, 0)
                 dz1_quarter(g, 0)
-                interleave_dz1_on_gpsimd(g, 0, "grouped", GROUPED)
+                if g == 0:
+                    interleave_dz1_on_gpsimd(0, 0, "grouped", GROUPED)
             for z in range(2):
                 transpose_dz1(0, 0, z, z)
             for u in range(2):
@@ -421,6 +409,7 @@ def tile_pt_grumb_pb_v_kernel(
                 park_grad(1, 1, u, 6 + u)
             for z in range(2):
                 copy_dz1_t(1, 0, z, "S")
+            interleave_dz1(1, 0, "V")
             quantize_dz2(0, 1)
             both(make_dz2, 1, 1)
             quantize_dz1_t(0, 0)

@@ -22,6 +22,8 @@ GROUPED = 4
 TURNED = 3
 MEMSQ = 4
 HALVES = 2
+SLAB_BYTES = 8192
+MOVED_AT = {"slab": 0, "w_raw": SLABS * SLAB_BYTES, "x_raw": (SLABS + 2) * SLAB_BYTES, "half_raw": (SLABS + 4) * SLAB_BYTES}
 
 FLOPS = 3 * 2 * SIZE * SIZE * SIZE
 BYTES = 4 * SIZE * SIZE * 2 + 2 * SIZE * SIZE * 4 + 2 * SIZE * SIZE * 4
@@ -47,6 +49,7 @@ def tile_pt_grumb_pb_v_kernel(
     with ExitStack() as ctx:
         keep = ctx.enter_context(tc.tile_pool(name="keep", bufs=1))
         work = ctx.enter_context(tc.tile_pool(name="work", bufs=1))
+        moved = ctx.enter_context(tc.tile_pool(name="moved", bufs=1))
         psum = ctx.enter_context(tc.psum_pool(name="psum", bufs=1))
 
         def keep_tile(shape, dtype, name):
@@ -72,8 +75,11 @@ def tile_pt_grumb_pb_v_kernel(
         def work_tile(shape, dtype, tag, bufs):
             return work.tile(shape, dtype, name=tag, tag=tag, align_bytes=256, bufs=bufs)
 
+        def dma_tile(shape, dtype, tag, bufs):
+            return moved.tile(shape, dtype, name=tag, tag=tag, align_bytes=2048, bufs=bufs, offset=MOVED_AT[tag])
+
         def slab(shape):
-            return work_tile(shape, F32, "slab", SLABS)
+            return dma_tile(shape, F32, "slab", SLABS)
 
         def grouped_tile():
             return work_tile([P, HALF, PACK], BF16, "grouped", GROUPED)
@@ -114,11 +120,11 @@ def tile_pt_grumb_pb_v_kernel(
             )
 
         def load_rows(key, hbm, k, tag, bufs):
-            held[key, k] = work_tile([P, PACK, SIZE], BF16, tag, bufs)
+            held[key, k] = dma_tile([P, PACK, SIZE], BF16, tag, bufs)
             nc.sync.dma_start(out=held[key, k][:], in_=hbm[k])
 
         def load_halves(key, hbm, k, c, tag, bufs):
-            held[key, k, c] = work_tile([P, PACK, HALF], BF16, tag, bufs)
+            held[key, k, c] = dma_tile([P, PACK, HALF], BF16, tag, bufs)
             nc.sync.dma_start(out=held[key, k, c][:], in_=hbm[k][:, :, half(c)])
 
         def whole(key, k):

@@ -17,13 +17,16 @@ P = 128
 PACK = 4
 HALF = 512
 QUARTER = 256
-SLABS = 6
-GROUPED = 4
-TURNED = 3
-MEMSQ = 4
-HALVES = 2
+SLABS = 9
+HALF_SLABS = 4
+GROUPED = 3
+TURNED = 4
+Y_SQUARED = 3
+MEM_SQUARED = 4
 SLAB_BYTES = 8192
-MOVED_AT = {"slab": 0, "w_raw": SLABS * SLAB_BYTES, "x_raw": (SLABS + 2) * SLAB_BYTES, "half_raw": (SLABS + 4) * SLAB_BYTES}
+MOVED_AT = {"slab": 0, "half_slab": SLABS * SLAB_BYTES}
+
+BY_COLUMNS = (("out_1", 0, 0),)
 
 FLOPS = 3 * 2 * SIZE * SIZE * SIZE
 BYTES = 4 * SIZE * SIZE * 2 + 2 * SIZE * SIZE * 4 + 2 * SIZE * SIZE * 4
@@ -37,14 +40,16 @@ def tile_pt_grumb_pb_v_kernel(
     def rows_by_four(hbm):
         return hbm.rearrange("(k p j) c -> k p j c", p=P, j=PACK)
 
-    w_hid_hbm = rows_by_four(w_hid_out)
-    w_rg_hbm = rows_by_four(w_readgate)
-    y_hbm = rows_by_four(y)
-    grad_hbm = rows_by_four(grad_out)
-    mem_hbm = rows_by_four(mem_out)
-    x_hbm = rows_by_four(x)
-    out_0_hbm = rows_by_four(out_0)
-    out_1_hbm = rows_by_four(out_1)
+    hbm = {
+        "w_hid": rows_by_four(w_hid_out),
+        "w_rg": rows_by_four(w_readgate),
+        "y": rows_by_four(y),
+        "grad": rows_by_four(grad_out),
+        "mem": rows_by_four(mem_out),
+        "x": rows_by_four(x),
+        "out_0": rows_by_four(out_0),
+        "out_1": rows_by_four(out_1),
+    }
 
     with ExitStack() as ctx:
         keep = ctx.enter_context(tc.tile_pool(name="keep", bufs=1))
@@ -60,12 +65,8 @@ def tile_pt_grumb_pb_v_kernel(
             scales = [keep_tile([P, SIZE], U8, "%s_scales_%d" % (name, k)) for k in range(2)]
             return codes, scales
 
-        w_hid_q = codes_pair("w_hid")
-        w_rg_q = codes_pair("w_rg")
-        dz2_q = codes_pair("dz2")
-        dz1_q = codes_pair("dz1")
-        dz1_t_q = codes_pair("dz1_t")
-        x_t_q = codes_pair("x_t")
+        operand = {name: codes_pair(name) for name in ("w_hid", "dz2", "dz1", "dz1_t", "x_t")}
+        fp8 = {"w_hid": E4M3, "w_rg": E4M3, "x_t": E4M3, "dz2": E5M2, "dz1": E5M2, "dz1_t": E5M2}
         dz1 = [[keep_tile([P, PACK, HALF], BF16, "dz1_%d_%d" % (g, h)) for h in range(2)] for g in range(2)]
         ident = keep_tile([P, P], F32, "ident")
         ident_bf16 = keep_tile([P, P], BF16, "ident_bf16")
@@ -75,14 +76,12 @@ def tile_pt_grumb_pb_v_kernel(
         def work_tile(shape, dtype, tag, bufs):
             return work.tile(shape, dtype, name=tag, tag=tag, align_bytes=256, bufs=bufs)
 
-        def dma_tile(shape, dtype, tag, bufs):
+        def dma_tile(shape, dtype, tag):
+            bufs = {"slab": SLABS, "half_slab": HALF_SLABS}[tag]
             return moved.tile(shape, dtype, name=tag, tag=tag, align_bytes=2048, bufs=bufs, offset=MOVED_AT[tag])
 
-        def slab(shape):
-            return dma_tile(shape, F32, "slab", SLABS)
-
-        def grouped_tile():
-            return work_tile([P, HALF, PACK], BF16, "grouped", GROUPED)
+        def grouped_tile(columns, tag="grouped", bufs=GROUPED):
+            return work_tile([P, columns, PACK], BF16, tag, bufs)
 
         def bank(side, shape, dtype=F32):
             return psum.tile(shape, dtype, name="bank_%d" % side, tag="bank_%d" % side)
@@ -96,84 +95,73 @@ def tile_pt_grumb_pb_v_kernel(
         def move(engine, out, in_):
             if engine == "S":
                 nc.scalar.copy(out=out, in_=in_)
-            else:
+            elif engine == "V":
                 nc.vector.tensor_copy(out=out, in_=in_)
+            else:
+                nc.gpsimd.tensor_scalar(out=out, in0=in_, scalar1=1.0, scalar2=-0.0, op0=ALU.mult, op1=ALU.add)
 
-        def quantize(operand, dtype, k, col, grouped):
-            codes, scales = operand
+        def quantize(name, k, first, columns):
+            codes, scales = operand[name]
+            cols = slice(first, first + columns)
             nc.vector.quantize_mx(
-                out=codes[k][:, half(col)].bitcast(dtype),
-                scales=scales[k][:, half(col)],
-                in_=grouped[:].rearrange("p n j -> p (n j)"),
+                out=codes[k][:, cols].bitcast(fp8[name]),
+                scales=scales[k][:, cols],
+                in_=held[name, k, first][:].rearrange("p n j -> p (n j)"),
             )
 
-        def product_pass(k, out, lhs, lhs_dtype, lhs_first, rhs, rhs_dtype, rhs_half):
+        def product_pass(k, out, lhs, lhs_first, rhs, rhs_half):
             lhs_cols = slice(lhs_first, lhs_first + P)
             nc.tensor.matmul_mx(
                 out=out,
-                lhsT=lhs[0][k][:, lhs_cols].bitcast(lhs_dtype),
-                lhsT_scale=lhs[1][k][:, lhs_cols],
-                rhs=rhs[0][k][:, half(rhs_half)].bitcast(rhs_dtype),
-                rhs_scale=rhs[1][k][:, half(rhs_half)],
+                lhsT=operand[lhs][0][k][:, lhs_cols].bitcast(fp8[lhs]),
+                lhsT_scale=operand[lhs][1][k][:, lhs_cols],
+                rhs=operand[rhs][0][k][:, half(rhs_half)].bitcast(fp8[rhs]),
+                rhs_scale=operand[rhs][1][k][:, half(rhs_half)],
                 start=(k == 0),
                 stop=(k == 1),
             )
 
-        def load_rows(key, hbm, k, tag, bufs):
-            held[key, k] = dma_tile([P, PACK, SIZE], BF16, tag, bufs)
-            nc.sync.dma_start(out=held[key, k][:], in_=hbm[k])
-
-        def load_halves(key, hbm, k, c, tag, bufs):
-            held[key, k, c] = dma_tile([P, PACK, HALF], BF16, tag, bufs)
-            nc.sync.dma_start(out=held[key, k, c][:], in_=hbm[k][:, :, half(c)])
-
-        def whole(key, k):
+        def load_rows(name, k):
+            tile = dma_tile([P, PACK, SIZE], BF16, "slab")
+            nc.sync.dma_start(out=tile[:], in_=hbm[name][k])
+            held["raw", name, k] = tile
             for c in range(2):
-                held[key, k, c] = held[key, k][:, :, half(c)]
+                held["raw", name, k, c] = tile[:, :, half(c)]
 
-        def load_w_hid(k):
-            load_rows("w_hid_raw", w_hid_hbm, k, "w_raw", 2)
-            whole("w_hid_raw", k)
+        def load_half(name, k, c):
+            if name in ("y", "mem"):
+                tile = dma_tile([P, PACK, HALF], F32, "slab")
+            else:
+                tile = dma_tile([P, PACK, HALF], BF16, "half_slab")
+            nc.sync.dma_start(out=tile[:], in_=hbm[name][k][:, :, half(c)])
+            held["raw", name, k, c] = tile[:]
 
-        def load_grad_half(k, h):
-            load_halves("grad_raw", grad_hbm, k, h, "half_raw", HALVES)
-
-        def load_w_rg(k):
-            load_rows("w_rg_raw", w_rg_hbm, k, "w_raw", 2)
-            whole("w_rg_raw", k)
-
-        def load_x(n):
-            load_rows("x_raw", x_hbm, n, "x_raw", 2)
-
-        def load_y(k, h):
-            held["y_raw", k, h] = slab([P, PACK, HALF])
-            nc.sync.dma_start(out=held["y_raw", k, h][:], in_=y_hbm[k][:, :, half(h)])
-
-        def load_mem(g, h):
-            held["mem_raw", g, h] = slab([P, PACK, HALF])
-            nc.sync.dma_start(out=held["mem_raw", g, h][:], in_=mem_hbm[g][:, :, half(h)])
+        def load_mem_rows(g, z):
+            tile = dma_tile([P, 2, SIZE], F32, "slab")
+            nc.sync.dma_start(out=tile[:], in_=hbm["mem"][g][:, pair(z), :])
+            held["mem_rows", g, z] = tile
 
         def square_y(k, h, u):
-            t = work_tile([P, P, 2, PACK], F32, "y_squared", 3)
+            t = work_tile([P, P, 2, PACK], F32, "y_squared", Y_SQUARED)
             nc.scalar.activation(
                 out=t[:].rearrange("p w e j -> p w j e"),
-                in_=held["y_raw", k, h][:].rearrange("p j (w u e) -> p u w j e", u=2, e=2)[:, u],
+                in_=held["raw", "y", k, h].rearrange("p j (w u e) -> p u w j e", u=2, e=2)[:, u],
                 func=ACT.Square,
             )
             held["y_squared", k, h, u] = t
 
         def park_grad(k, h, u, side):
             ps = bank(side, [P, PACK, P, 2], BF16)
-            source = held["grad_raw", k, h][:].rearrange("p j (w u e) -> p u j w e", u=2, e=2)[:, u]
+            source = held["raw", "grad", k, h].rearrange("p j (w u e) -> p u j w e", u=2, e=2)[:, u]
             for z in range(2):
                 nc.tensor.matmul(out=ps[:, pair(z)], lhsT=ident_bf16[:], rhs=source[:, pair(z)], start=True, stop=True)
             held["grad_ps", k, h, u] = ps
 
         def make_dz2(k, h, u):
             if u == 0:
-                held["dz2", k, h] = grouped_tile()
+                held["dz2", k, h * HALF] = grouped_tile(HALF)
             nc.vector.scalar_tensor_tensor(
-                out=held["dz2", k, h][:, u * QUARTER : (u + 1) * QUARTER, :],
+                out=held["dz2", k, h * HALF][:, u * QUARTER : (u + 1) * QUARTER, :],
                 in0=held["y_squared", k, h, u][:].rearrange("p w e j -> p (w e) j"),
                 scalar=1.0,
                 in1=held["grad_ps", k, h, u][:].rearrange("p j w e -> p (w e) j"),
@@ -182,54 +170,80 @@ def tile_pt_grumb_pb_v_kernel(
             )
 
         def square_mem(g, h, z):
-            sq = work_tile([P, 2, 2, QUARTER], F32, "mem_squared", MEMSQ)
+            sq = work_tile([P, 2, 2, QUARTER], F32, "mem_squared", MEM_SQUARED)
             nc.scalar.activation(
                 out=sq[:].rearrange("p u a (w e) -> p u (a w) e", e=2),
-                in_=held["mem_raw", g, h][:, pair(z), :].rearrange("p a (w u e) -> p u (a w) e", u=2, e=2),
+                in_=held["raw", "mem", g, h][:, pair(z), :].rearrange("p a (w u e) -> p u (a w) e", u=2, e=2),
                 func=ACT.Square,
                 bias=minus_half[:],
             )
-            held["mem_squared", g, h, z] = sq
+            for a in range(2):
+                held["mem_squared", g, h, 2 * z + a] = sq[:, :, a, :]
 
-        def interleave_weight(key, k, c, engine):
-            grouped = grouped_tile()
+        def square_mem_row(g, t):
+            sq = work_tile([P, 2, 2, QUARTER], F32, "mem_squared", MEM_SQUARED)
+            nc.scalar.activation(
+                out=sq[:].rearrange("p u h (w e) -> p u (h w) e", e=2),
+                in_=held["mem_rows", g, t // 2][:, t % 2, :].rearrange("p (w u e) -> p u w e", u=2, e=2),
+                func=ACT.Square,
+                bias=minus_half[:],
+            )
+            for h in range(2):
+                held["mem_squared", g, h, t] = sq[:, :, h, :]
+
+        def interleave_weight(name, k, c, engine):
+            grouped = grouped_tile(HALF)
             move(
                 engine,
                 grouped[:].rearrange("p (t m) j -> p m j t", t=PACK),
-                held[key + "_raw", k, c][:].rearrange("p j (m t) -> p m j t", t=PACK),
+                held["raw", name, k, c].rearrange("p j (m t) -> p m j t", t=PACK),
             )
-            held[key, k, c] = grouped
+            held[name, k, c * HALF] = grouped
 
-        def interleave_dz1(g, h, engine):
-            grouped = grouped_tile()
+        def interleave_weight_pair(name, k, c, z, engine, tag="grouped", bufs=GROUPED):
+            grouped = grouped_tile(QUARTER, tag, bufs)
             move(
                 engine,
-                grouped[:].rearrange("p (c i) j -> p c j i", i=4),
-                dz1[g][h][:].rearrange("p j (c i) -> p c j i", i=4),
+                grouped[:].rearrange("p (a m) j -> p m j a", a=2),
+                held["raw", name, k, c].rearrange("p j (m t) -> p m j t", t=PACK)[:, :, :, pair(z)],
             )
-            held["dz1", g, h] = grouped
+            held[name, k, c * HALF + z * QUARTER] = grouped
 
-        def interleave_dz1_on_gpsimd(g, h, tag, bufs):
-            grouped = work_tile([P, HALF, PACK], BF16, tag, bufs)
-            nc.gpsimd.tensor_scalar(
-                out=grouped[:],
-                in0=dz1[g][h][:].rearrange("p j c -> p c j"),
-                scalar1=1.0,
-                scalar2=-0.0,
-                op0=ALU.mult,
-                op1=ALU.add,
-            )
-            held["dz1", g, h] = grouped
+        def interleave_dz1(g, h, engine, tag="grouped", bufs=GROUPED):
+            grouped = grouped_tile(HALF, tag, bufs)
+            if engine == "G":
+                move(engine, grouped[:], dz1[g][h][:].rearrange("p j c -> p c j"))
+            else:
+                move(
+                    engine,
+                    grouped[:].rearrange("p (c i) j -> p c j i", i=4),
+                    dz1[g][h][:].rearrange("p j (c i) -> p c j i", i=4),
+                )
+            held["dz1", g, h * HALF] = grouped
 
-        def hidden_pass(k, g, h, t, side):
+        def interleave_dz1_half(g, h, u, engine, tag="grouped", bufs=GROUPED):
+            if u == 0:
+                held["dz1", g, h * HALF] = grouped_tile(HALF, tag, bufs)
+            cols = slice(u * QUARTER, (u + 1) * QUARTER)
+            grouped = held["dz1", g, h * HALF][:, cols, :]
+            if engine == "G":
+                move(engine, grouped, dz1[g][h][:, :, cols].rearrange("p j c -> p c j"))
+            else:
+                move(
+                    engine,
+                    grouped.rearrange("p (c i) j -> p c j i", i=4),
+                    dz1[g][h][:, :, cols].rearrange("p j (c i) -> p c j i", i=4),
+                )
+
+        def hidden_pass(k, g, h, t, side=None):
             if k == 0:
                 held["dh", g, h, t] = bank(side, [P, HALF])
-            product_pass(k, held["dh", g, h, t][:], w_hid_q, E4M3, g * HALF + t * P, dz2_q, E5M2, h)
+            product_pass(k, held["dh", g, h, t][:], "w_hid", g * HALF + t * P, "dz2", h)
 
         def make_dz1(g, h, t):
             nc.vector.scalar_tensor_tensor(
                 out=dz1[g][h][:, t, :].rearrange("p (u n) -> p u n", u=2),
-                in0=held["mem_squared", g, h, t // 2][:, :, t % 2, :],
+                in0=held["mem_squared", g, h, t],
                 scalar=0.25,
                 in1=held["dh", g, h, t][:].rearrange("p (u n) -> p u n", u=2),
                 op0=ALU.subtract,
@@ -246,7 +260,7 @@ def tile_pt_grumb_pb_v_kernel(
             held["dz1_t_ps", g, h, z] = ps
 
         def transpose_x(n, h, z, side):
-            words = held["x_raw", n][:].rearrange("p a b -> p (a b)").bitcast(F32)
+            words = held["raw", "x", n][:].rearrange("p a b -> p (a b)").bitcast(F32)
             ps = bank(side, [P, 2, 2, P])
             for a in range(2):
                 for u in range(2):
@@ -254,172 +268,149 @@ def tile_pt_grumb_pb_v_kernel(
                     nc.tensor.transpose(ps[:, a, u, :], words[:, first : first + QUARTER - 1 : 2], ident[:])
             held["x_t_ps", n, h, z] = ps
 
-        def grouped_words(key, z):
-            if z == 0:
-                own_tags = {("dz1_t", 1, 0): "turned_kept", ("x_t", 1, 1): "handed_on"}
-                tag, bufs = (own_tags[key], 1) if key in own_tags else ("turned", TURNED)
-                held[key] = work_tile([P, HALF, PACK], BF16, tag, bufs)
-            return held[key][:].rearrange("p n j -> p (n j)").bitcast(F32)
+        def as_words(tile):
+            return tile[:].rearrange("p n j -> p (n j)").bitcast(F32)
 
         def copy_dz1_t(g, h, z, engine):
-            words = grouped_words(("dz1_t", g, h), z)
+            if z == 0:
+                held["dz1_t", h, g * HALF] = grouped_tile(HALF, "turned", TURNED)
             move(
                 engine,
-                words[:, half(z)].rearrange("p (a r u) -> p a r u", a=2, u=2),
+                as_words(held["dz1_t", h, g * HALF])[:, half(z)].rearrange("p (a r u) -> p a r u", a=2, u=2),
                 held["dz1_t_ps", g, h, z][:].rearrange("p a u r -> p a r u"),
             )
 
-        def copy_x_t(n, h, z, engine):
-            words = grouped_words(("x_t", n, h), z)
+        def copy_dz1_t_pair(g, h, z, engine):
+            tile = grouped_tile(QUARTER, "turned", TURNED)
+            held["dz1_t", h, g * HALF + z * QUARTER] = tile
             move(
                 engine,
-                words.rearrange("p (r z a u) -> p z r a u", z=2, a=2, u=2)[:, z],
+                as_words(tile).rearrange("p (a r u) -> p a r u", a=2, u=2),
+                held["dz1_t_ps", g, h, z][:].rearrange("p a u r -> p a r u"),
+            )
+
+        def copy_x_t(n, h, z, engine, tag="turned", bufs=TURNED):
+            if z == 0:
+                held["x_t", h, n * HALF] = grouped_tile(HALF, tag, bufs)
+            move(
+                engine,
+                as_words(held["x_t", h, n * HALF]).rearrange("p (r z a u) -> p z r a u", z=2, a=2, u=2)[:, z],
                 held["x_t_ps", n, h, z][:].rearrange("p a u r -> p r a u"),
             )
 
-        def quantize_w_hid(k, c):
-            quantize(w_hid_q, E4M3, k, c, held["w_hid", k, c])
-
-        def interleave_w_rg_pair(k, c, z):
-            grouped = work_tile([P, QUARTER, PACK], BF16, "grouped", GROUPED)
-            nc.vector.tensor_copy(
-                out=grouped[:].rearrange("p (a m) j -> p m j a", a=2),
-                in_=held["w_rg_raw", k, c][:].rearrange("p j (m t) -> p m j t", t=PACK)[:, :, :, pair(z)],
-            )
-            held["w_rg", k, c, z] = grouped
-
-        def quantize_w_rg_pair(k, c, z):
-            cols = slice(c * HALF + z * QUARTER, c * HALF + (z + 1) * QUARTER)
-            nc.vector.quantize_mx(
-                out=w_rg_q[0][k][:, cols].bitcast(E4M3),
-                scales=w_rg_q[1][k][:, cols],
-                in_=held["w_rg", k, c, z][:].rearrange("p n j -> p (n j)"),
-            )
-
-        def quantize_dz2(k, h):
-            quantize(dz2_q, E5M2, k, h, held["dz2", k, h])
-
-        def quantize_dz1(g, h):
-            quantize(dz1_q, E5M2, g, h, held["dz1", g, h])
-
-        def quantize_dz1_t(g, h):
-            quantize(dz1_t_q, E5M2, h, g, held["dz1_t", g, h])
-
-        def quantize_x_t(n, h):
-            quantize(x_t_q, E4M3, h, n, held["x_t", n, h])
-
-        def stage_for(key, shape):
-            if key not in held:
-                held[key] = slab(shape)
-            return held[key]
+        def stage_for(name, c, t, n):
+            if (name, c, t // 2) not in held:
+                held[name, c, t // 2] = dma_tile([P, 2, 2, HALF], F32, "slab")
+            if (name, c, t // 2) in BY_COLUMNS:
+                return held[name, c, t // 2][:, n, t % 2, :]
+            return held[name, c, t // 2][:, t % 2, n, :]
 
         def out_0_product(c, t, h, side):
             held["ps_0", c, t, h] = bank(side, [P, HALF])
             for k in range(2):
-                product_pass(k, held["ps_0", c, t, h][:], w_rg_q, E4M3, c * HALF + t * P, dz1_q, E5M2, h)
+                product_pass(k, held["ps_0", c, t, h][:], "w_rg", c * HALF + t * P, "dz1", h)
 
         def out_0_copy(c, t, h, engine):
             move(
                 engine,
-                stage_for(("stage_0", c, t // 2), [P, 2, SIZE])[:, t % 2, half(h)].rearrange("p (w u e) -> p w u e", u=2, e=2),
+                stage_for("out_0", c, t, h).rearrange("p (w u e) -> p w u e", u=2, e=2),
                 held["ps_0", c, t, h][:].rearrange("p (u w e) -> p w u e", u=2, e=2),
             )
 
         def out_1_product(g, t, n, side):
             held["ps_1", g, t, n] = bank(side, [P, HALF])
             for k in range(2):
-                product_pass(k, held["ps_1", g, t, n][:], dz1_t_q, E5M2, g * HALF + t * P, x_t_q, E4M3, n)
+                product_pass(k, held["ps_1", g, t, n][:], "dz1_t", g * HALF + t * P, "x_t", n)
 
         def out_1_copy(g, t, n, engine):
-            move(engine, stage_for(("stage_1", g, t // 2), [P, 2, SIZE])[:, t % 2, half(n)], held["ps_1", g, t, n][:])
+            move(engine, stage_for("out_1", g, t, n), held["ps_1", g, t, n][:])
 
-        def store(key, hbm, c, first, count):
-            rows = slice(first % 2, first % 2 + count)
-            nc.sync.dma_start(out=hbm[c][:, first : first + count, :], in_=held[key, c, first // 2][:, rows, :])
+        def store(name, c, t):
+            rows = held[name, c, t // 2][:, t % 2].rearrange("p n w -> p (n w)")
+            nc.sync.dma_start(out=hbm[name][c][:, t, :], in_=rows)
+
+        def store_columns(name, c, z, n):
+            nc.sync.dma_start(out=hbm[name][c][:, pair(z), half(n)], in_=held[name, c, z][:, n])
+
+        def store_piece(name, c, t, n):
+            nc.sync.dma_start(out=hbm[name][c][:, t, half(n)], in_=stage_for(name, c, t, n))
+
+        def both(step, *args):
+            for u in range(2):
+                step(*args, u)
 
         nc.vector.memset(minus_half[:], -0.5)
         make_identity(nc, ident_bf16[:])
         make_identity(nc, ident[:])
 
         with tc.manual_schedule():
-            def both(fn, *args):
-                for u in range(2):
-                    fn(*args, u)
-
-            def hidden(g, h, side):
-                for t in range(4):
-                    for k in range(2):
-                        hidden_pass(k, g, h, t, side)
-
-            def dz1_quarter(g, h):
-                for t in range(4):
-                    make_dz1(g, h, t)
-
-            load_w_hid(0)
-            load_y(0, 0)
-            load_grad_half(0, 0)
-            load_y(1, 0)
-            load_grad_half(1, 0)
-            load_w_hid(1)
-            load_mem(0, 0)
-            load_mem(1, 0)
-
+            load_rows("w_hid", 0)
+            load_half("y", 0, 0)
+            load_half("grad", 0, 0)
+            load_half("y", 1, 0)
+            load_half("grad", 1, 0)
+            load_rows("w_hid", 1)
+            load_half("mem", 0, 0)
+            load_half("mem", 1, 0)
+            load_half("y", 0, 1)
+            load_half("grad", 0, 1)
+            load_half("y", 1, 1)
+            load_half("grad", 1, 1)
+            load_rows("x", 0)
             for c in range(2):
                 interleave_weight("w_hid", 0, c, "V")
             for c in range(2):
-                quantize_w_hid(0, c)
+                quantize("w_hid", 0, c * HALF, HALF)
+            load_half("mem", 0, 1)
             for k in range(2):
                 for u in range(2):
                     square_y(k, 0, u)
                     park_grad(k, 0, u, 4 + 2 * k + u)
                 both(make_dz2, k, 0)
                 if k == 0:
-                    quantize_dz2(0, 0)
-            for k in range(2):
-                load_y(k, 1)
-                load_grad_half(k, 1)
-            load_x(0)
-            load_mem(0, 1)
-            load_x(1)
+                    quantize("dz2", 0, 0, HALF)
+            load_rows("x", 1)
+            load_half("mem", 1, 1)
             for g in range(2):
                 for t in range(4):
                     hidden_pass(0, g, 0, t, 4 * g + t)
             interleave_weight("w_hid", 1, 0, "V")
             interleave_weight("w_hid", 1, 1, "S")
-            load_mem(1, 1)
-            load_w_rg(0)
-            load_w_rg(1)
-            quantize_dz2(1, 0)
-            for g in range(2):
-                quantize_w_hid(1, g)
+            load_rows("w_rg", 0)
+            quantize("dz2", 1, 0, HALF)
+            for c in range(2):
+                quantize("w_hid", 1, c * HALF, HALF)
             for g in range(2):
                 for t in range(4):
-                    hidden_pass(1, g, 0, t, None)
+                    hidden_pass(1, g, 0, t)
             for g in range(2):
                 both(square_mem, g, 0)
-                dz1_quarter(g, 0)
+                for t in range(4):
+                    make_dz1(g, 0, t)
                 if g == 0:
-                    interleave_dz1_on_gpsimd(0, 0, "grouped", GROUPED)
+                    interleave_dz1(0, 0, "G", "by_gpsimd", 2)
+                    load_rows("w_rg", 1)
+            interleave_dz1_half(1, 0, 0, "G", "by_gpsimd", 2)
             for z in range(2):
                 transpose_dz1(0, 0, z, z)
-            for u in range(2):
-                square_y(0, 1, u)
-                park_grad(0, 1, u, 2 + u)
+            both(square_y, 0, 1)
+            park_grad(0, 1, 0, 2)
             for z in range(2):
                 transpose_dz1(1, 0, z, 4 + z)
-            for z in range(2):
-                copy_dz1_t(0, 0, z, "S")
-            both(make_dz2, 0, 1)
+            park_grad(0, 1, 1, 3)
+            make_dz2(0, 1, 0)
+            copy_dz1_t(0, 0, 0, "S")
+            make_dz2(0, 1, 1)
+            copy_dz1_t(0, 0, 1, "V")
             for u in range(2):
                 square_y(1, 1, u)
                 park_grad(1, 1, u, 6 + u)
             for z in range(2):
                 copy_dz1_t(1, 0, z, "S")
-            interleave_dz1(1, 0, "V")
-            quantize_dz2(0, 1)
+            quantize("dz2", 0, HALF, HALF)
             both(make_dz2, 1, 1)
-            quantize_dz1_t(0, 0)
-            quantize_dz2(1, 1)
+            quantize("dz1_t", 0, 0, HALF)
+            quantize("dz2", 1, HALF, HALF)
             for t in range(2):
                 hidden_pass(0, 0, 1, t, t)
             for z in range(2):
@@ -429,81 +420,93 @@ def tile_pt_grumb_pb_v_kernel(
                 hidden_pass(0, 0, 1, t, t)
             for z in range(2):
                 transpose_x(0, 1, z, 6 + z)
-                copy_x_t(0, 1, z, "SS"[z])
             for t in range(4):
-                hidden_pass(1, 0, 1, t, None)
-            for t in range(2):
-                hidden_pass(0, 1, 1, t, 6 + t)
-            for g in range(2):
-                quantize_dz1(g, 0)
-            for h in range(2):
-                quantize_x_t(0, h)
+                hidden_pass(1, 0, 1, t)
             both(square_mem, 0, 1)
-            dz1_quarter(0, 1)
+            quantize("dz1_t", 0, HALF, HALF)
+            quantize("x_t", 0, 0, HALF)
+            for t in range(4):
+                make_dz1(0, 1, t)
+            for z in range(2):
+                copy_x_t(0, 1, z, "S")
             for z in range(2):
                 transpose_x(1, 0, z, 4 + z)
                 copy_x_t(1, 0, z, "S")
-            for t in range(2):
-                hidden_pass(1, 1, 1, t, None)
-            for z in range(2):
-                transpose_x(1, 1, z, z)
-            quantize_x_t(1, 0)
-            for z in range(2):
-                copy_x_t(1, 1, z, "V")
-            square_mem(1, 1, 0)
+            for k in range(2):
+                hidden_pass(k, 1, 1, 0, 0)
             for z in range(2):
                 transpose_dz1(0, 1, z, 2 + z)
-                copy_dz1_t(0, 1, z, "S")
+            transpose_x(1, 1, 0, 6)
+            for k in range(2):
+                hidden_pass(k, 1, 1, 1, 1)
+            transpose_x(1, 1, 1, 7)
+            quantize("dz1", 0, 0, HALF)
+            quantize("x_t", 1, 0, HALF)
+            for z in range(2):
+                copy_dz1_t(0, 1, z, "V")
+            square_mem(1, 1, 0)
+            quantize("x_t", 0, HALF, HALF)
+            quantize("dz1_t", 1, 0, HALF)
+            for z in range(2):
+                copy_x_t(1, 1, z, "S", "handed_on", 1)
             square_mem(1, 1, 1)
-            for t in range(2, 4):
-                for k in range(2):
-                    hidden_pass(k, 1, 1, t, 2 + t)
-            quantize_dz1_t(1, 0)
-            quantize_dz1_t(0, 1)
-            quantize_x_t(1, 1)
-
+            interleave_dz1_half(1, 0, 1, "V")
+            quantize("x_t", 1, HALF, HALF)
+            interleave_dz1(0, 1, "G", "handed_on", 1)
+            for k in range(2):
+                hidden_pass(k, 1, 1, 2, 4)
             for t in range(2):
-                for n in range(2):
-                    out_1_product(0, t, n, 2 * t + n)
-            dz1_quarter(1, 1)
+                out_1_product(0, t, 0, 2 + t)
+            for k in range(2):
+                hidden_pass(k, 1, 1, 3, 5)
             for t in range(2):
-                for n in range(2):
-                    out_1_copy(0, t, n, "S")
-                store("stage_1", out_1_hbm, 0, t, 1)
+                out_1_product(0, t, 1, 6 + t)
+            for t in range(4):
+                make_dz1(1, 1, t)
             for n in range(2):
-                out_1_product(0, 2, n, 6 + n)
+                for t in range(2):
+                    out_1_copy(0, t, n, "S")
+                store_columns("out_1", 0, 0, n)
+            out_1_product(0, 2, 0, 0)
             for z in range(2):
                 transpose_dz1(1, 1, z, 4 + z)
+            out_1_product(0, 2, 1, 1)
             for n in range(2):
-                out_1_product(0, 3, n, n)
-            interleave_dz1(0, 1, "V")
-            for n in range(2):
-                out_1_copy(0, 2, n, "S")
-            store("stage_1", out_1_hbm, 0, 2, 1)
+                out_1_product(0, 3, n, 2 + n)
+            out_1_copy(0, 2, 0, "V")
             for z in range(2):
                 copy_dz1_t(1, 1, z, "VS"[z])
+            out_1_copy(0, 2, 1, "S")
+            store("out_1", 0, 2)
             for n in range(2):
                 out_1_copy(0, 3, n, "S")
-            store("stage_1", out_1_hbm, 0, 3, 1)
-            quantize_dz1_t(1, 1)
+            store("out_1", 0, 3)
+            operand["w_rg"] = codes_pair("w_hid")
+            quantize("dz1", 1, 0, HALF)
+            quantize("dz1_t", 1, HALF, HALF)
             interleave_dz1(1, 1, "V")
-            quantize_dz1(0, 1)
+            quantize("dz1", 0, HALF, HALF)
+            interleave_weight_pair("w_rg", 0, 0, 0, "V")
+            quantize("dz1", 1, HALF, HALF)
+            interleave_weight_pair("w_rg", 1, 0, 0, "V")
+            for k in range(2):
+                quantize("w_rg", k, 0, QUARTER)
             for t in range(4):
                 for n in range(2):
-                    out_1_product(1, t, n, (2, 6, 4, 0)[t] + n)
+                    out_1_product(1, t, n, (6, 0, 4, 2)[t] + n)
                     out_1_copy(1, t, n, "S")
-                store("stage_1", out_1_hbm, 1, t, 1)
-            for c in range(2):
-                for z in range(2):
-                    for k in range(2):
-                        interleave_w_rg_pair(k, c, z)
-                    if c == 0 and z == 0:
-                        quantize_dz1(1, 1)
-                    for k in range(2):
-                        quantize_w_rg_pair(k, c, z)
+                store("out_1", 1, t)
+            for c, z in ((0, 1), (1, 0), (1, 1)):
+                for k in range(2):
+                    interleave_weight_pair("w_rg", k, c, z, "V")
+                for k in range(2):
+                    quantize("w_rg", k, c * HALF + z * QUARTER, QUARTER)
             for c in range(2):
                 for t in range(4):
                     for h in range(2):
-                        out_0_product(c, t, h, (2, 6, 4, 0)[t] + h)
+                        out_0_product(c, t, h, (6, 0, 4, 2)[t] + h)
                         out_0_copy(c, t, h, "V" if h and 4 * c + t >= 4 else "S")
-                    store("stage_0", out_0_hbm, c, t, 1)
+                        if c == 1 and t == 3:
+                            store_piece("out_0", c, t, h)
+                    if c == 0 or t < 3:
+                        store("out_0", c, t)

@@ -17,16 +17,13 @@ P = 128
 PACK = 4
 HALF = 512
 QUARTER = 256
-SLABS = 9
-HALF_SLABS = 4
-GROUPED = 3
-TURNED = 4
-Y_SQUARED = 3
+PIECES = 16
+GROUPED = 5
+TURNED = 5
+Y_SQUARED = 5
 MEM_SQUARED = 4
-SLAB_BYTES = 8192
-MOVED_AT = {"slab": 0, "half_slab": SLABS * SLAB_BYTES}
-
-BY_COLUMNS = (("out_1", 0, 0),)
+PIECE_BYTES = 4096
+HANDED_ON = None
 
 FLOPS = 3 * 2 * SIZE * SIZE * SIZE
 BYTES = 4 * SIZE * SIZE * 2 + 2 * SIZE * SIZE * 4 + 2 * SIZE * SIZE * 4
@@ -47,7 +44,7 @@ def tile_pt_grumb_pb_v_kernel(
         "grad": rows_by_four(grad_out),
         "mem": rows_by_four(mem_out),
         "x": rows_by_four(x),
-        "out_0": rows_by_four(out_0),
+        "out_0": out_0.rearrange("(c t p) b -> c p t b", p=P, t=PACK),
         "out_1": rows_by_four(out_1),
     }
 
@@ -76,9 +73,8 @@ def tile_pt_grumb_pb_v_kernel(
         def work_tile(shape, dtype, tag, bufs):
             return work.tile(shape, dtype, name=tag, tag=tag, align_bytes=256, bufs=bufs)
 
-        def dma_tile(shape, dtype, tag):
-            bufs = {"slab": SLABS, "half_slab": HALF_SLABS}[tag]
-            return moved.tile(shape, dtype, name=tag, tag=tag, align_bytes=2048, bufs=bufs, offset=MOVED_AT[tag])
+        def piece(shape, dtype):
+            return moved.tile(shape, dtype, name="piece", tag="piece", align_bytes=2048, bufs=PIECES, offset=0)
 
         def grouped_tile(columns, tag="grouped", bufs=GROUPED):
             return work_tile([P, columns, PACK], BF16, tag, bufs)
@@ -88,6 +84,9 @@ def tile_pt_grumb_pb_v_kernel(
 
         def half(n):
             return slice(n * HALF, (n + 1) * HALF)
+
+        def quarter(n):
+            return slice(n * QUARTER, (n + 1) * QUARTER)
 
         def pair(z):
             return slice(2 * z, 2 * z + 2)
@@ -100,13 +99,14 @@ def tile_pt_grumb_pb_v_kernel(
             else:
                 nc.gpsimd.tensor_scalar(out=out, in0=in_, scalar1=1.0, scalar2=-0.0, op0=ALU.mult, op1=ALU.add)
 
-        def quantize(name, k, first, columns):
+        def quantize(name, k, c, part=None):
             codes, scales = operand[name]
-            cols = slice(first, first + columns)
+            grouped = held[name, k, c][:] if part is None else held[name, k, c][:, quarter(part), :]
+            cols = half(c) if part is None else quarter(2 * c + part)
             nc.vector.quantize_mx(
                 out=codes[k][:, cols].bitcast(fp8[name]),
                 scales=scales[k][:, cols],
-                in_=held[name, k, first][:].rearrange("p n j -> p (n j)"),
+                in_=grouped.rearrange("p n j -> p (n j)"),
             )
 
         def product_pass(k, out, lhs, lhs_first, rhs, rhs_half):
@@ -121,50 +121,50 @@ def tile_pt_grumb_pb_v_kernel(
                 stop=(k == 1),
             )
 
-        def load_rows(name, k):
-            tile = dma_tile([P, PACK, SIZE], BF16, "slab")
-            nc.sync.dma_start(out=tile[:], in_=hbm[name][k])
-            held["raw", name, k] = tile
-            for c in range(2):
-                held["raw", name, k, c] = tile[:, :, half(c)]
-
         def load_half(name, k, c):
-            if name in ("y", "mem"):
-                tile = dma_tile([P, PACK, HALF], F32, "slab")
-            else:
-                tile = dma_tile([P, PACK, HALF], BF16, "half_slab")
-            nc.sync.dma_start(out=tile[:], in_=hbm[name][k][:, :, half(c)])
-            held["raw", name, k, c] = tile[:]
+            held["raw", name, k, c] = piece([P, PACK, HALF], BF16)
+            nc.sync.dma_start(out=held["raw", name, k, c][:], in_=hbm[name][k][:, :, half(c)])
 
-        def load_mem_rows(g, z):
-            tile = dma_tile([P, 2, SIZE], F32, "slab")
-            nc.sync.dma_start(out=tile[:], in_=hbm["mem"][g][:, pair(z), :])
-            held["mem_rows", g, z] = tile
+        def load_y(k, h, v):
+            held["raw", "y", k, h, v] = piece([P, PACK, QUARTER], F32)
+            nc.sync.dma_start(out=held["raw", "y", k, h, v][:], in_=hbm["y"][k][:, :, quarter(2 * h + v)])
 
-        def square_y(k, h, u):
-            t = work_tile([P, P, 2, PACK], F32, "y_squared", Y_SQUARED)
+        def load_mem(g, h, z):
+            held["raw", "mem", g, h, z] = piece([P, 2, HALF], F32)
+            nc.sync.dma_start(out=held["raw", "mem", g, h, z][:], in_=hbm["mem"][g][:, pair(z), half(h)])
+
+        def load_w_rg(k):
+            tile = moved.tile(
+                [P, PACK, SIZE], BF16, name="w_rg_raw", tag="w_rg_raw", align_bytes=2048, bufs=2, offset=PIECES * PIECE_BYTES
+            )
+            nc.sync.dma_start(out=tile[:], in_=hbm["w_rg"][k])
+            held["raw", "w_rg", k] = tile
+
+        def square_y(k, h, v, u):
+            t = work_tile([P, P // 2, 2, PACK], F32, "y_squared", Y_SQUARED)
             nc.scalar.activation(
                 out=t[:].rearrange("p w e j -> p w j e"),
-                in_=held["raw", "y", k, h].rearrange("p j (w u e) -> p u w j e", u=2, e=2)[:, u],
+                in_=held["raw", "y", k, h, v][:].rearrange("p j (w u e) -> p u w j e", u=2, e=2)[:, u],
                 func=ACT.Square,
             )
-            held["y_squared", k, h, u] = t
+            held["y_squared", k, h, v, u] = t
 
         def park_grad(k, h, u, side):
             ps = bank(side, [P, PACK, P, 2], BF16)
-            source = held["raw", "grad", k, h].rearrange("p j (w u e) -> p u j w e", u=2, e=2)[:, u]
+            source = held["raw", "grad", k, h][:].rearrange("p j (w u e) -> p u j w e", u=2, e=2)[:, u]
             for z in range(2):
                 nc.tensor.matmul(out=ps[:, pair(z)], lhsT=ident_bf16[:], rhs=source[:, pair(z)], start=True, stop=True)
             held["grad_ps", k, h, u] = ps
 
-        def make_dz2(k, h, u):
-            if u == 0:
-                held["dz2", k, h * HALF] = grouped_tile(HALF)
+        def make_dz2(k, h, v, u):
+            if ("dz2", k, h) not in held:
+                held["dz2", k, h] = grouped_tile(HALF)
+            first = u * QUARTER + v * P
             nc.vector.scalar_tensor_tensor(
-                out=held["dz2", k, h * HALF][:, u * QUARTER : (u + 1) * QUARTER, :],
-                in0=held["y_squared", k, h, u][:].rearrange("p w e j -> p (w e) j"),
+                out=held["dz2", k, h][:, first : first + P, :],
+                in0=held["y_squared", k, h, v, u][:].rearrange("p w e j -> p (w e) j"),
                 scalar=1.0,
-                in1=held["grad_ps", k, h, u][:].rearrange("p j w e -> p (w e) j"),
+                in1=held["grad_ps", k, h, u][:].rearrange("p j w e -> p (w e) j")[:, v * P : (v + 1) * P, :],
                 op0=ALU.subtract,
                 op1=ALU.mult,
             )
@@ -173,67 +173,60 @@ def tile_pt_grumb_pb_v_kernel(
             sq = work_tile([P, 2, 2, QUARTER], F32, "mem_squared", MEM_SQUARED)
             nc.scalar.activation(
                 out=sq[:].rearrange("p u a (w e) -> p u (a w) e", e=2),
-                in_=held["raw", "mem", g, h][:, pair(z), :].rearrange("p a (w u e) -> p u (a w) e", u=2, e=2),
+                in_=held["raw", "mem", g, h, z][:].rearrange("p a (w u e) -> p u (a w) e", u=2, e=2),
                 func=ACT.Square,
                 bias=minus_half[:],
             )
-            for a in range(2):
-                held["mem_squared", g, h, 2 * z + a] = sq[:, :, a, :]
+            held["mem_squared", g, h, z] = sq
 
-        def square_mem_row(g, t):
-            sq = work_tile([P, 2, 2, QUARTER], F32, "mem_squared", MEM_SQUARED)
-            nc.scalar.activation(
-                out=sq[:].rearrange("p u h (w e) -> p u (h w) e", e=2),
-                in_=held["mem_rows", g, t // 2][:, t % 2, :].rearrange("p (w u e) -> p u w e", u=2, e=2),
-                func=ACT.Square,
-                bias=minus_half[:],
-            )
-            for h in range(2):
-                held["mem_squared", g, h, t] = sq[:, :, h, :]
-
-        def interleave_weight(name, k, c, engine):
-            grouped = grouped_tile(HALF)
+        def interleave_w_hid(k, g, engine, part=None):
+            if ("w_hid", k, g) not in held:
+                held["w_hid", k, g] = grouped_tile(HALF)
+            rows = slice(0, P) if part is None else slice(part * P // 2, (part + 1) * P // 2)
             move(
                 engine,
-                grouped[:].rearrange("p (t m) j -> p m j t", t=PACK),
-                held["raw", name, k, c].rearrange("p j (m t) -> p m j t", t=PACK),
+                held["w_hid", k, g][:].rearrange("p (t m) j -> p m j t", t=PACK)[:, rows],
+                held["raw", "w_hid", k, g][:].rearrange("p j (m t) -> p m j t", t=PACK)[:, rows],
             )
-            held[name, k, c * HALF] = grouped
 
-        def interleave_weight_pair(name, k, c, z, engine, tag="grouped", bufs=GROUPED):
-            grouped = grouped_tile(QUARTER, tag, bufs)
+        def interleave(engine, grouped, rows):
+            if engine == "G":
+                move(engine, grouped, rows.rearrange("p j c -> p c j"))
+            else:
+                move(engine, grouped.rearrange("p (c i) j -> p c j i", i=4), rows.rearrange("p j (c i) -> p c j i", i=4))
+
+        def interleave_w_rg(k, c, z, engine):
+            if ("w_rg", k, c) not in held:
+                held["w_rg", k, c] = grouped_tile(HALF)
+            interleave(engine, held["w_rg", k, c][:, quarter(z), :], held["raw", "w_rg", k][:, :, quarter(2 * c + z)])
+
+        def interleave_dz1(g, h, engine, part=None, tag="grouped", bufs=GROUPED):
+            if ("dz1", g, h) not in held:
+                held["dz1", g, h] = grouped_tile(HALF, tag, bufs)
+            cols = slice(0, HALF) if part is None else quarter(part)
+            interleave(engine, held["dz1", g, h][:, cols, :], dz1[g][h][:, :, cols])
+
+        def interleave_on_tensor(g, h, part, side):
+            ps = bank(side, [P, QUARTER, PACK], BF16)
+            for s in range(2):
+                first = part * QUARTER + s * P
+                nc.tensor.matmul(
+                    out=ps[:, s * P : (s + 1) * P, :].rearrange("p c j -> p j c"),
+                    lhsT=ident_bf16[:],
+                    rhs=dz1[g][h][:, :, first : first + P],
+                    start=True,
+                    stop=True,
+                )
+            held["dz1_ps", g, h, part] = ps
+
+        def copy_interleaved(g, h, part, engine):
+            if ("dz1", g, h) not in held:
+                held["dz1", g, h] = grouped_tile(HALF)
             move(
                 engine,
-                grouped[:].rearrange("p (a m) j -> p m j a", a=2),
-                held["raw", name, k, c].rearrange("p j (m t) -> p m j t", t=PACK)[:, :, :, pair(z)],
+                held["dz1", g, h][:, quarter(part), :].rearrange("p c j -> p (c j)").bitcast(F32),
+                held["dz1_ps", g, h, part][:].rearrange("p c j -> p (c j)").bitcast(F32),
             )
-            held[name, k, c * HALF + z * QUARTER] = grouped
-
-        def interleave_dz1(g, h, engine, tag="grouped", bufs=GROUPED):
-            grouped = grouped_tile(HALF, tag, bufs)
-            if engine == "G":
-                move(engine, grouped[:], dz1[g][h][:].rearrange("p j c -> p c j"))
-            else:
-                move(
-                    engine,
-                    grouped[:].rearrange("p (c i) j -> p c j i", i=4),
-                    dz1[g][h][:].rearrange("p j (c i) -> p c j i", i=4),
-                )
-            held["dz1", g, h * HALF] = grouped
-
-        def interleave_dz1_half(g, h, u, engine, tag="grouped", bufs=GROUPED):
-            if u == 0:
-                held["dz1", g, h * HALF] = grouped_tile(HALF, tag, bufs)
-            cols = slice(u * QUARTER, (u + 1) * QUARTER)
-            grouped = held["dz1", g, h * HALF][:, cols, :]
-            if engine == "G":
-                move(engine, grouped, dz1[g][h][:, :, cols].rearrange("p j c -> p c j"))
-            else:
-                move(
-                    engine,
-                    grouped.rearrange("p (c i) j -> p c j i", i=4),
-                    dz1[g][h][:, :, cols].rearrange("p j (c i) -> p c j i", i=4),
-                )
 
         def hidden_pass(k, g, h, t, side=None):
             if k == 0:
@@ -243,7 +236,7 @@ def tile_pt_grumb_pb_v_kernel(
         def make_dz1(g, h, t):
             nc.vector.scalar_tensor_tensor(
                 out=dz1[g][h][:, t, :].rearrange("p (u n) -> p u n", u=2),
-                in0=held["mem_squared", g, h, t],
+                in0=held["mem_squared", g, h, t // 2][:, :, t % 2, :],
                 scalar=0.25,
                 in1=held["dh", g, h, t][:].rearrange("p (u n) -> p u n", u=2),
                 op0=ALU.subtract,
@@ -260,80 +253,65 @@ def tile_pt_grumb_pb_v_kernel(
             held["dz1_t_ps", g, h, z] = ps
 
         def transpose_x(n, h, z, side):
-            words = held["raw", "x", n][:].rearrange("p a b -> p (a b)").bitcast(F32)
+            words = held["raw", "x", n, h][:].rearrange("p a b -> p (a b)").bitcast(F32)
             ps = bank(side, [P, 2, 2, P])
             for a in range(2):
                 for u in range(2):
-                    first = (2 * z + a) * HALF + h * QUARTER + u
+                    first = (2 * z + a) * QUARTER + u
                     nc.tensor.transpose(ps[:, a, u, :], words[:, first : first + QUARTER - 1 : 2], ident[:])
             held["x_t_ps", n, h, z] = ps
 
-        def as_words(tile):
-            return tile[:].rearrange("p n j -> p (n j)").bitcast(F32)
+        def turned_words(name, h, c):
+            if (name, h, c) not in held:
+                tag, bufs = ("handed_on", 1) if (name, h, c) == HANDED_ON else ("turned", TURNED)
+                held[name, h, c] = grouped_tile(HALF, tag, bufs)
+            return held[name, h, c][:].rearrange("p n j -> p (n j)").bitcast(F32)
 
         def copy_dz1_t(g, h, z, engine):
-            if z == 0:
-                held["dz1_t", h, g * HALF] = grouped_tile(HALF, "turned", TURNED)
             move(
                 engine,
-                as_words(held["dz1_t", h, g * HALF])[:, half(z)].rearrange("p (a r u) -> p a r u", a=2, u=2),
+                turned_words("dz1_t", h, g)[:, half(z)].rearrange("p (a r u) -> p a r u", a=2, u=2),
                 held["dz1_t_ps", g, h, z][:].rearrange("p a u r -> p a r u"),
             )
 
-        def copy_dz1_t_pair(g, h, z, engine):
-            tile = grouped_tile(QUARTER, "turned", TURNED)
-            held["dz1_t", h, g * HALF + z * QUARTER] = tile
+        def copy_x_t(n, h, z, engine):
             move(
                 engine,
-                as_words(tile).rearrange("p (a r u) -> p a r u", a=2, u=2),
-                held["dz1_t_ps", g, h, z][:].rearrange("p a u r -> p a r u"),
-            )
-
-        def copy_x_t(n, h, z, engine, tag="turned", bufs=TURNED):
-            if z == 0:
-                held["x_t", h, n * HALF] = grouped_tile(HALF, tag, bufs)
-            move(
-                engine,
-                as_words(held["x_t", h, n * HALF]).rearrange("p (r z a u) -> p z r a u", z=2, a=2, u=2)[:, z],
+                turned_words("x_t", h, n).rearrange("p (r z a u) -> p z r a u", z=2, a=2, u=2)[:, z],
                 held["x_t_ps", n, h, z][:].rearrange("p a u r -> p r a u"),
             )
 
-        def stage_for(name, c, t, n):
-            if (name, c, t // 2) not in held:
-                held[name, c, t // 2] = dma_tile([P, 2, 2, HALF], F32, "slab")
-            if (name, c, t // 2) in BY_COLUMNS:
-                return held[name, c, t // 2][:, n, t % 2, :]
-            return held[name, c, t // 2][:, t % 2, n, :]
+        def out_pass(k, name, c, t, n, side=None):
+            if k == 0:
+                held["ps", name, c, t, n] = bank(side, [P, HALF])
+            lhs, rhs = ("w_rg", "dz1") if name == "out_0" else ("dz1_t", "x_t")
+            product_pass(k, held["ps", name, c, t, n][:], lhs, c * HALF + t * P, rhs, n)
 
-        def out_0_product(c, t, h, side):
-            held["ps_0", c, t, h] = bank(side, [P, HALF])
+        def out_product(name, c, t, n, side):
             for k in range(2):
-                product_pass(k, held["ps_0", c, t, h][:], "w_rg", c * HALF + t * P, "dz1", h)
+                out_pass(k, name, c, t, n, side)
 
-        def out_0_copy(c, t, h, engine):
-            move(
-                engine,
-                stage_for("out_0", c, t, h).rearrange("p (w u e) -> p w u e", u=2, e=2),
-                held["ps_0", c, t, h][:].rearrange("p (u w e) -> p w u e", u=2, e=2),
-            )
+        def by_columns(name, c):
+            return name == "out_1" and c == 0
 
-        def out_1_product(g, t, n, side):
-            held["ps_1", g, t, n] = bank(side, [P, HALF])
-            for k in range(2):
-                product_pass(k, held["ps_1", g, t, n][:], "dz1_t", g * HALF + t * P, "x_t", n)
+        def out_copy(name, c, t, n, engine):
+            key, place = ((name, c, t // 2, n), t % 2) if by_columns(name, c) else ((name, c, t), n)
+            if key not in held:
+                held[key] = piece([P, 2, HALF], F32)
+            staged, ps = held[key][:, place, :], held["ps", name, c, t, n][:]
+            if name == "out_0":
+                staged = staged.rearrange("p (w u e) -> p w u e", u=2, e=2)
+                ps = ps.rearrange("p (u w e) -> p w u e", u=2, e=2)
+            move(engine, staged, ps)
 
-        def out_1_copy(g, t, n, engine):
-            move(engine, stage_for("out_1", g, t, n), held["ps_1", g, t, n][:])
-
-        def store(name, c, t):
-            rows = held[name, c, t // 2][:, t % 2].rearrange("p n w -> p (n w)")
-            nc.sync.dma_start(out=hbm[name][c][:, t, :], in_=rows)
+        def store_row(name, c, t):
+            nc.sync.dma_start(out=hbm[name][c][:, t, :], in_=held[name, c, t][:].rearrange("p n w -> p (n w)"))
 
         def store_columns(name, c, z, n):
-            nc.sync.dma_start(out=hbm[name][c][:, pair(z), half(n)], in_=held[name, c, z][:, n])
+            nc.sync.dma_start(out=hbm[name][c][:, pair(z), half(n)], in_=held[name, c, z, n][:])
 
         def store_piece(name, c, t, n):
-            nc.sync.dma_start(out=hbm[name][c][:, t, half(n)], in_=stage_for(name, c, t, n))
+            nc.sync.dma_start(out=hbm[name][c][:, t, half(n)], in_=held[name, c, t][:, n, :])
 
         def both(step, *args):
             for u in range(2):
@@ -344,169 +322,189 @@ def tile_pt_grumb_pb_v_kernel(
         make_identity(nc, ident[:])
 
         with tc.manual_schedule():
-            load_rows("w_hid", 0)
-            load_half("y", 0, 0)
+            both(load_half, "w_hid", 0)
             load_half("grad", 0, 0)
-            load_half("y", 1, 0)
+            both(load_y, 0, 0)
+            load_half("w_hid", 1, 0)
             load_half("grad", 1, 0)
-            load_rows("w_hid", 1)
-            load_half("mem", 0, 0)
-            load_half("mem", 1, 0)
-            load_half("y", 0, 1)
+            both(load_y, 1, 0)
+            load_mem(0, 0, 0)
+            load_half("w_hid", 1, 1)
+            load_mem(0, 0, 1)
+            both(load_mem, 1, 0)
             load_half("grad", 0, 1)
-            load_half("y", 1, 1)
-            load_half("grad", 1, 1)
-            load_rows("x", 0)
-            for c in range(2):
-                interleave_weight("w_hid", 0, c, "V")
-            for c in range(2):
-                quantize("w_hid", 0, c * HALF, HALF)
-            load_half("mem", 0, 1)
-            for k in range(2):
-                for u in range(2):
-                    square_y(k, 0, u)
-                    park_grad(k, 0, u, 4 + 2 * k + u)
-                both(make_dz2, k, 0)
-                if k == 0:
-                    quantize("dz2", 0, 0, HALF)
-            load_rows("x", 1)
-            load_half("mem", 1, 1)
+            load_y(0, 1, 0)
             for g in range(2):
-                for t in range(4):
-                    hidden_pass(0, g, 0, t, 4 * g + t)
-            interleave_weight("w_hid", 1, 0, "V")
-            interleave_weight("w_hid", 1, 1, "S")
-            load_rows("w_rg", 0)
-            quantize("dz2", 1, 0, HALF)
-            for c in range(2):
-                quantize("w_hid", 1, c * HALF, HALF)
-            for g in range(2):
-                for t in range(4):
-                    hidden_pass(1, g, 0, t)
-            for g in range(2):
-                both(square_mem, g, 0)
-                for t in range(4):
-                    make_dz1(g, 0, t)
-                if g == 0:
-                    interleave_dz1(0, 0, "G", "by_gpsimd", 2)
-                    load_rows("w_rg", 1)
-            interleave_dz1_half(1, 0, 0, "G", "by_gpsimd", 2)
-            for z in range(2):
-                transpose_dz1(0, 0, z, z)
-            both(square_y, 0, 1)
-            park_grad(0, 1, 0, 2)
-            for z in range(2):
-                transpose_dz1(1, 0, z, 4 + z)
-            park_grad(0, 1, 1, 3)
-            make_dz2(0, 1, 0)
-            copy_dz1_t(0, 0, 0, "S")
-            make_dz2(0, 1, 1)
-            copy_dz1_t(0, 0, 1, "V")
+                interleave_w_hid(0, g, "V")
+            both(quantize, "w_hid", 0)
             for u in range(2):
-                square_y(1, 1, u)
-                park_grad(1, 1, u, 6 + u)
-            for z in range(2):
-                copy_dz1_t(1, 0, z, "S")
-            quantize("dz2", 0, HALF, HALF)
-            both(make_dz2, 1, 1)
-            quantize("dz1_t", 0, 0, HALF)
-            quantize("dz2", 1, HALF, HALF)
+                park_grad(0, 0, u, 4 + u)
+            for v in range(2):
+                both(square_y, 0, 0, v)
+                both(make_dz2, 0, 0, v)
+            load_y(0, 1, 1)
+            load_half("grad", 1, 1)
+            load_half("x", 0, 0)
+            both(load_y, 1, 1)
+            interleave_w_hid(1, 0, "V")
+            quantize("dz2", 0, 0)
+            quantize("w_hid", 1, 0)
+            load_half("x", 0, 1)
+            for u in range(2):
+                park_grad(1, 0, u, 6 + u)
+            for t in range(4):
+                hidden_pass(0, 0, 0, t, t)
+            for v in range(2):
+                both(square_y, 1, 0, v)
+                both(make_dz2, 1, 0, v)
             for t in range(2):
-                hidden_pass(0, 0, 1, t, t)
-            for z in range(2):
-                transpose_x(0, 0, z, 4 + z)
-                copy_x_t(0, 0, z, "S")
+                hidden_pass(0, 1, 0, t, 6 + t)
+            both(load_mem, 0, 1)
+            load_half("x", 1, 0)
+            both(quantize, "dz2", 1, 0)
+            for t in range(4):
+                hidden_pass(1, 0, 0, t)
+            both(square_mem, 0, 0)
+            interleave_w_hid(1, 1, "V")
+            for t in range(2):
+                make_dz1(0, 0, t)
             for t in range(2, 4):
-                hidden_pass(0, 0, 1, t, t)
+                hidden_pass(0, 1, 0, t, 2 + t)
+            transpose_dz1(0, 0, 0, 0)
+            quantize("w_hid", 1, 1)
+            for t in range(2, 4):
+                make_dz1(0, 0, t)
+            interleave_dz1(0, 0, "G", None, "by_gpsimd", 2)
+            for t in range(4):
+                hidden_pass(1, 1, 0, t)
+            both(square_mem, 1, 0)
+            copy_dz1_t(0, 0, 0, "S")
+            load_half("x", 1, 1)
+            both(load_mem, 1, 1)
+            both(load_w_rg)
+            park_grad(0, 1, 0, 2)
+            transpose_dz1(0, 0, 1, 1)
+            park_grad(0, 1, 1, 3)
+            for t in range(4):
+                make_dz1(1, 0, t)
+            interleave_dz1(1, 0, "G", 0, "by_gpsimd", 2)
+            copy_dz1_t(0, 0, 1, "V")
             for z in range(2):
-                transpose_x(0, 1, z, 6 + z)
+                transpose_dz1(1, 0, z, 6 + z)
+            interleave_on_tensor(1, 0, 1, 1)
+            for v in range(2):
+                both(square_y, 0, 1, v)
+                both(make_dz2, 0, 1, v)
+            copy_dz1_t(1, 0, 0, "S")
+            copy_interleaved(1, 0, 1, "S")
+            copy_dz1_t(1, 0, 1, "S")
+            quantize("dz1", 0, 0)
+            for u in range(2):
+                park_grad(1, 1, u, 4 + u)
+                transpose_x(0, 0, u, u)
+            both(quantize, "dz1_t", 0)
+            quantize("dz2", 0, 1)
+            copy_x_t(0, 0, 0, "S")
+            for t in range(4):
+                hidden_pass(0, 0, 1, t, (2, 3, 6, 7)[t])
+            for v in range(2):
+                both(square_y, 1, 1, v)
+                both(make_dz2, 1, 1, v)
+            both(quantize, "dz2", 1, 1)
+            for z in range(2):
+                transpose_x(0, 1, z, 4 * z)
+            copy_x_t(0, 0, 1, "S")
+            for t in range(2):
+                hidden_pass(0, 1, 1, t, 1 + 4 * t)
             for t in range(4):
                 hidden_pass(1, 0, 1, t)
+            for t in range(2):
+                hidden_pass(1, 1, 1, t)
+            copy_x_t(0, 1, 0, "S")
+            quantize("x_t", 0, 0)
+            quantize("dz1", 1, 0)
             both(square_mem, 0, 1)
-            quantize("dz1_t", 0, HALF, HALF)
-            quantize("x_t", 0, 0, HALF)
             for t in range(4):
                 make_dz1(0, 1, t)
+            copy_x_t(0, 1, 1, "S")
+            transpose_x(1, 0, 0, 0)
+            transpose_dz1(0, 1, 0, 2)
+            for t in range(2):
+                out_pass(0, "out_1", 0, t, 0, 3 + 3 * t)
+            transpose_dz1(0, 1, 1, 7)
+            transpose_x(1, 0, 1, 4)
+            copy_dz1_t(0, 1, 0, "S")
+            copy_x_t(1, 0, 0, "S")
+            copy_dz1_t(0, 1, 1, "S")
+            quantize("x_t", 1, 0)
+            quantize("dz1_t", 1, 0, 0)
+            interleave_dz1(0, 1, "V", 0)
+            copy_x_t(1, 0, 1, "V")
+            quantize("dz1_t", 1, 0, 1)
+            for t in range(2):
+                out_pass(1, "out_1", 0, t, 0)
             for z in range(2):
-                copy_x_t(0, 1, z, "S")
-            for z in range(2):
-                transpose_x(1, 0, z, 4 + z)
-                copy_x_t(1, 0, z, "S")
-            for k in range(2):
-                hidden_pass(k, 1, 1, 0, 0)
-            for z in range(2):
-                transpose_dz1(0, 1, z, 2 + z)
-            transpose_x(1, 1, 0, 6)
-            for k in range(2):
-                hidden_pass(k, 1, 1, 1, 1)
-            transpose_x(1, 1, 1, 7)
-            quantize("dz1", 0, 0, HALF)
-            quantize("x_t", 1, 0, HALF)
-            for z in range(2):
-                copy_dz1_t(0, 1, z, "V")
+                transpose_x(1, 1, z, 2 * z)
+            for t in range(2, 4):
+                out_product("out_1", 0, t, 0, (7, 4)[t - 2])
             square_mem(1, 1, 0)
-            quantize("x_t", 0, HALF, HALF)
-            quantize("dz1_t", 1, 0, HALF)
-            for z in range(2):
-                copy_x_t(1, 1, z, "S", "handed_on", 1)
-            square_mem(1, 1, 1)
-            interleave_dz1_half(1, 0, 1, "V")
-            quantize("x_t", 1, HALF, HALF)
-            interleave_dz1(0, 1, "G", "handed_on", 1)
-            for k in range(2):
-                hidden_pass(k, 1, 1, 2, 4)
+            copy_x_t(1, 1, 0, "V")
             for t in range(2):
-                out_1_product(0, t, 0, 2 + t)
-            for k in range(2):
-                hidden_pass(k, 1, 1, 3, 5)
-            for t in range(2):
-                out_1_product(0, t, 1, 6 + t)
-            for t in range(4):
                 make_dz1(1, 1, t)
-            for n in range(2):
-                for t in range(2):
-                    out_1_copy(0, t, n, "S")
-                store_columns("out_1", 0, 0, n)
-            out_1_product(0, 2, 0, 0)
-            for z in range(2):
-                transpose_dz1(1, 1, z, 4 + z)
-            out_1_product(0, 2, 1, 1)
-            for n in range(2):
-                out_1_product(0, 3, n, 2 + n)
-            out_1_copy(0, 2, 0, "V")
-            for z in range(2):
-                copy_dz1_t(1, 1, z, "VS"[z])
-            out_1_copy(0, 2, 1, "S")
-            store("out_1", 0, 2)
-            for n in range(2):
-                out_1_copy(0, 3, n, "S")
-            store("out_1", 0, 3)
+            copy_x_t(1, 1, 1, "V")
+            for h in range(2):
+                quantize("x_t", h, 1)
+            for t in range(2):
+                out_copy("out_1", 0, t, 0, "S")
+            store_columns("out_1", 0, 0, 0)
+            for t in range(2, 4):
+                for k in range(2):
+                    hidden_pass(k, 1, 1, t, (1, 5)[t - 2])
             operand["w_rg"] = codes_pair("w_hid")
-            quantize("dz1", 1, 0, HALF)
-            quantize("dz1_t", 1, HALF, HALF)
+            transpose_dz1(1, 1, 0, 3)
+            square_mem(1, 1, 1)
+            for t in range(2, 4):
+                out_copy("out_1", 0, t, 0, "S")
+            store_columns("out_1", 0, 1, 0)
+            for t in range(2, 4):
+                make_dz1(1, 1, t)
+            copy_dz1_t(1, 1, 0, "S")
+            for z in range(2):
+                for k in range(2):
+                    for t in range(2 * z, 2 * z + 2):
+                        out_pass(k, "out_1", 0, t, 1, (6, 0, 2, 7)[t])
+            transpose_dz1(1, 1, 1, 4)
+            interleave_dz1(0, 1, "V", 1)
+            quantize("dz1_t", 1, 1, 0)
             interleave_dz1(1, 1, "V")
-            quantize("dz1", 0, HALF, HALF)
-            interleave_weight_pair("w_rg", 0, 0, 0, "V")
-            quantize("dz1", 1, HALF, HALF)
-            interleave_weight_pair("w_rg", 1, 0, 0, "V")
+            copy_dz1_t(1, 1, 1, "V")
+            quantize("dz1", 0, 1)
+            quantize("dz1_t", 1, 1, 1)
+            for z in range(2):
+                for t in range(2 * z, 2 * z + 2):
+                    out_copy("out_1", 0, t, 1, "S")
+                store_columns("out_1", 0, z, 1)
+            interleave_w_rg(0, 0, 0, "V")
+            quantize("dz1", 1, 1)
+            interleave_w_rg(1, 0, 0, "V")
             for k in range(2):
-                quantize("w_rg", k, 0, QUARTER)
+                quantize("w_rg", k, 0, 0)
             for t in range(4):
                 for n in range(2):
-                    out_1_product(1, t, n, (6, 0, 4, 2)[t] + n)
-                    out_1_copy(1, t, n, "S")
-                store("out_1", 1, t)
+                    out_product("out_1", 1, t, n, (3, 1, 5, 6, 0, 2, 7, 4)[2 * t + n])
+                    out_copy("out_1", 1, t, n, "S")
+                store_row("out_1", 1, t)
             for c, z in ((0, 1), (1, 0), (1, 1)):
                 for k in range(2):
-                    interleave_weight_pair("w_rg", k, c, z, "V")
+                    interleave_w_rg(k, c, z, "V")
                 for k in range(2):
-                    quantize("w_rg", k, c * HALF + z * QUARTER, QUARTER)
+                    quantize("w_rg", k, c, z)
             for c in range(2):
                 for t in range(4):
                     for h in range(2):
-                        out_0_product(c, t, h, (6, 0, 4, 2)[t] + h)
-                        out_0_copy(c, t, h, "V" if h and 4 * c + t >= 4 else "S")
+                        out_product("out_0", c, t, h, (3, 1, 5, 6, 0, 2, 7, 4)[2 * t + h])
+                        out_copy("out_0", c, t, h, "V" if h and 4 * c + t >= 3 else "S")
                         if c == 1 and t == 3:
                             store_piece("out_0", c, t, h)
                     if c == 0 or t < 3:
-                        store("out_0", c, t)
+                        store_row("out_0", c, t)

@@ -17,13 +17,14 @@ P = 128
 PACK = 4
 HALF = 512
 QUARTER = 256
-PIECES = 16
+PIECES = 14
+SLABS = 1
 GROUPED = 5
 TURNED = 5
 Y_SQUARED = 5
 MEM_SQUARED = 4
 PIECE_BYTES = 4096
-HANDED_ON = None
+HANDED_ON = ("dz1_t", 1, 0)
 
 FLOPS = 3 * 2 * SIZE * SIZE * SIZE
 BYTES = 4 * SIZE * SIZE * 2 + 2 * SIZE * SIZE * 4 + 2 * SIZE * SIZE * 4
@@ -39,7 +40,6 @@ def tile_pt_grumb_pb_v_kernel(
 
     hbm = {
         "w_hid": rows_by_four(w_hid_out),
-        "w_rg": rows_by_four(w_readgate),
         "y": rows_by_four(y),
         "grad": rows_by_four(grad_out),
         "mem": rows_by_four(mem_out),
@@ -125,6 +125,21 @@ def tile_pt_grumb_pb_v_kernel(
             held["raw", name, k, c] = piece([P, PACK, HALF], BF16)
             nc.sync.dma_start(out=held["raw", name, k, c][:], in_=hbm[name][k][:, :, half(c)])
 
+        def slab(shape, dtype):
+            return moved.tile(shape, dtype, name="slab", tag="slab", align_bytes=2048, bufs=SLABS, offset=PIECES * PIECE_BYTES)
+
+        def load_rows(name, k):
+            tile = slab([P, PACK, SIZE], BF16)
+            nc.sync.dma_start(out=tile[:], in_=hbm[name][k])
+            for c in range(2):
+                held["raw", name, k, c] = tile[:, :, half(c)]
+
+        def load_mem_quarter(g, h):
+            tile = slab([P, PACK, HALF], F32)
+            nc.sync.dma_start(out=tile[:], in_=hbm["mem"][g][:, :, half(h)])
+            for z in range(2):
+                held["raw", "mem", g, h, z] = tile[:, pair(z), :]
+
         def load_y(k, h, v):
             held["raw", "y", k, h, v] = piece([P, PACK, QUARTER], F32)
             nc.sync.dma_start(out=held["raw", "y", k, h, v][:], in_=hbm["y"][k][:, :, quarter(2 * h + v)])
@@ -133,25 +148,67 @@ def tile_pt_grumb_pb_v_kernel(
             held["raw", "mem", g, h, z] = piece([P, 2, HALF], F32)
             nc.sync.dma_start(out=held["raw", "mem", g, h, z][:], in_=hbm["mem"][g][:, pair(z), half(h)])
 
-        def load_w_rg(k):
-            tile = moved.tile(
-                [P, PACK, SIZE], BF16, name="w_rg_raw", tag="w_rg_raw", align_bytes=2048, bufs=2, offset=PIECES * PIECE_BYTES
+        def load_w_rg():
+            at = PIECES * PIECE_BYTES + SLABS * 2 * PIECE_BYTES
+            tile = moved.tile([P, 2, PACK, SIZE], BF16, name="w_rg_raw", tag="w_rg_raw", align_bytes=2048, bufs=1, offset=at)
+            nc.sync.dma_start(
+                out=tile[:].rearrange("p k j c -> p k (j c)"), in_=w_readgate.rearrange("(k p j) c -> p k (j c)", p=P, j=PACK)
             )
-            nc.sync.dma_start(out=tile[:], in_=hbm["w_rg"][k])
-            held["raw", "w_rg", k] = tile
+            for k in range(2):
+                held["raw", "w_rg", k] = tile[:, k]
+
+        load_order = [
+            (load_half, "w_hid", 0, 0),
+            (load_half, "w_hid", 0, 1),
+            (load_half, "grad", 0, 0),
+            (load_y, 0, 0, 0),
+            (load_y, 0, 0, 1),
+            (load_half, "w_hid", 1, 0),
+            (load_half, "grad", 1, 0),
+            (load_y, 1, 0, 0),
+            (load_y, 1, 0, 1),
+            (load_mem, 0, 0, 0),
+            (load_half, "w_hid", 1, 1),
+            (load_mem, 0, 0, 1),
+            (load_mem, 1, 0, 0),
+            (load_mem, 1, 0, 1),
+            (load_half, "x", 0, 0),
+            (load_half, "grad", 0, 1),
+            (load_y, 0, 1, 0),
+            (load_y, 0, 1, 1),
+            (load_half, "grad", 1, 1),
+            (load_y, 1, 1, 0),
+            (load_y, 1, 1, 1),
+            (load_half, "x", 0, 1),
+            (load_mem, 0, 1, 0),
+            (load_mem, 0, 1, 1),
+            (load_half, "x", 1, 0),
+            (load_half, "x", 1, 1),
+            (load_mem, 1, 1, 0),
+            (load_mem, 1, 1, 1),
+            (load_w_rg,),
+        ]
+        issued = set()
+
+        def raw(*key):
+            for step in load_order:
+                if ("raw",) + key not in held and step not in issued:
+                    issued.add(step)
+                    step[0](*step[1:])
+            return held[("raw",) + key]
 
         def square_y(k, h, v, u):
             t = work_tile([P, P // 2, 2, PACK], F32, "y_squared", Y_SQUARED)
             nc.scalar.activation(
                 out=t[:].rearrange("p w e j -> p w j e"),
-                in_=held["raw", "y", k, h, v][:].rearrange("p j (w u e) -> p u w j e", u=2, e=2)[:, u],
+                in_=raw("y", k, h, v)[:].rearrange("p j (w u e) -> p u w j e", u=2, e=2)[:, u],
                 func=ACT.Square,
             )
             held["y_squared", k, h, v, u] = t
 
         def park_grad(k, h, u, side):
             ps = bank(side, [P, PACK, P, 2], BF16)
-            source = held["raw", "grad", k, h][:].rearrange("p j (w u e) -> p u j w e", u=2, e=2)[:, u]
+            source = raw("grad", k, h)[:].rearrange("p j (w u e) -> p u j w e", u=2, e=2)[:, u]
             for z in range(2):
                 nc.tensor.matmul(out=ps[:, pair(z)], lhsT=ident_bf16[:], rhs=source[:, pair(z)], start=True, stop=True)
             held["grad_ps", k, h, u] = ps
@@ -173,7 +230,7 @@ def tile_pt_grumb_pb_v_kernel(
             sq = work_tile([P, 2, 2, QUARTER], F32, "mem_squared", MEM_SQUARED)
             nc.scalar.activation(
                 out=sq[:].rearrange("p u a (w e) -> p u (a w) e", e=2),
-                in_=held["raw", "mem", g, h, z][:].rearrange("p a (w u e) -> p u (a w) e", u=2, e=2),
+                in_=raw("mem", g, h, z)[:].rearrange("p a (w u e) -> p u (a w) e", u=2, e=2),
                 func=ACT.Square,
                 bias=minus_half[:],
             )
@@ -186,7 +243,7 @@ def tile_pt_grumb_pb_v_kernel(
             move(
                 engine,
                 held["w_hid", k, g][:].rearrange("p (t m) j -> p m j t", t=PACK)[:, rows],
-                held["raw", "w_hid", k, g][:].rearrange("p j (m t) -> p m j t", t=PACK)[:, rows],
+                raw("w_hid", k, g)[:].rearrange("p j (m t) -> p m j t", t=PACK)[:, rows],
             )
 
         def interleave(engine, grouped, rows):
@@ -198,12 +255,11 @@ def tile_pt_grumb_pb_v_kernel(
         def interleave_w_rg(k, c, z, engine):
             if ("w_rg", k, c) not in held:
                 held["w_rg", k, c] = grouped_tile(HALF)
-            interleave(engine, held["w_rg", k, c][:, quarter(z), :], held["raw", "w_rg", k][:, :, quarter(2 * c + z)])
+            interleave(engine, held["w_rg", k, c][:, quarter(z), :], raw("w_rg", k)[:, :, quarter(2 * c + z)])
 
-        def interleave_dz1(g, h, engine, part=None, tag="grouped", bufs=GROUPED):
+        def interleave_dz1(g, h, engine, cols=slice(0, HALF), tag="grouped", bufs=GROUPED):
             if ("dz1", g, h) not in held:
                 held["dz1", g, h] = grouped_tile(HALF, tag, bufs)
-            cols = slice(0, HALF) if part is None else quarter(part)
             interleave(engine, held["dz1", g, h][:, cols, :], dz1[g][h][:, :, cols])
 
         def interleave_on_tensor(g, h, part, side):
@@ -253,7 +309,7 @@ def tile_pt_grumb_pb_v_kernel(
             held["dz1_t_ps", g, h, z] = ps
 
         def transpose_x(n, h, z, side):
-            words = held["raw", "x", n, h][:].rearrange("p a b -> p (a b)").bitcast(F32)
+            words = raw("x", n, h)[:].rearrange("p a b -> p (a b)").bitcast(F32)
             ps = bank(side, [P, 2, 2, P])
             for a in range(2):
                 for u in range(2):
@@ -322,18 +378,6 @@ def tile_pt_grumb_pb_v_kernel(
         make_identity(nc, ident[:])
 
         with tc.manual_schedule():
-            both(load_half, "w_hid", 0)
-            load_half("grad", 0, 0)
-            both(load_y, 0, 0)
-            load_half("w_hid", 1, 0)
-            load_half("grad", 1, 0)
-            both(load_y, 1, 0)
-            load_mem(0, 0, 0)
-            load_half("w_hid", 1, 1)
-            load_mem(0, 0, 1)
-            both(load_mem, 1, 0)
-            load_half("grad", 0, 1)
-            load_y(0, 1, 0)
             for g in range(2):
                 interleave_w_hid(0, g, "V")
             both(quantize, "w_hid", 0)
@@ -342,14 +386,9 @@ def tile_pt_grumb_pb_v_kernel(
             for v in range(2):
                 both(square_y, 0, 0, v)
                 both(make_dz2, 0, 0, v)
-            load_y(0, 1, 1)
-            load_half("grad", 1, 1)
-            load_half("x", 0, 0)
-            both(load_y, 1, 1)
             interleave_w_hid(1, 0, "V")
             quantize("dz2", 0, 0)
             quantize("w_hid", 1, 0)
-            load_half("x", 0, 1)
             for u in range(2):
                 park_grad(1, 0, u, 6 + u)
             for t in range(4):
@@ -359,8 +398,6 @@ def tile_pt_grumb_pb_v_kernel(
                 both(make_dz2, 1, 0, v)
             for t in range(2):
                 hidden_pass(0, 1, 0, t, 6 + t)
-            both(load_mem, 0, 1)
-            load_half("x", 1, 0)
             both(quantize, "dz2", 1, 0)
             for t in range(4):
                 hidden_pass(1, 0, 0, t)
@@ -374,79 +411,75 @@ def tile_pt_grumb_pb_v_kernel(
             quantize("w_hid", 1, 1)
             for t in range(2, 4):
                 make_dz1(0, 0, t)
-            interleave_dz1(0, 0, "G", None, "by_gpsimd", 2)
+            interleave_dz1(0, 0, "G", slice(0, HALF), "by_gpsimd", 2)
             for t in range(4):
                 hidden_pass(1, 1, 0, t)
             both(square_mem, 1, 0)
             copy_dz1_t(0, 0, 0, "S")
-            load_half("x", 1, 1)
-            both(load_mem, 1, 1)
-            both(load_w_rg)
-            park_grad(0, 1, 0, 2)
+            for z in range(2):
+                transpose_x(0, 0, z, 2 + z)
+                copy_x_t(0, 0, z, "S")
+            park_grad(0, 1, 0, 0)
             transpose_dz1(0, 0, 1, 1)
-            park_grad(0, 1, 1, 3)
             for t in range(4):
                 make_dz1(1, 0, t)
-            interleave_dz1(1, 0, "G", 0, "by_gpsimd", 2)
+            interleave_dz1(1, 0, "G", slice(0, 384), "by_gpsimd", 2)
             copy_dz1_t(0, 0, 1, "V")
             for z in range(2):
-                transpose_dz1(1, 0, z, 6 + z)
-            interleave_on_tensor(1, 0, 1, 1)
+                transpose_dz1(1, 0, z, (7, 4)[z])
+            park_grad(0, 1, 1, 6)
             for v in range(2):
                 both(square_y, 0, 1, v)
                 both(make_dz2, 0, 1, v)
-            copy_dz1_t(1, 0, 0, "S")
-            copy_interleaved(1, 0, 1, "S")
-            copy_dz1_t(1, 0, 1, "S")
-            quantize("dz1", 0, 0)
+            for z in range(2):
+                copy_dz1_t(1, 0, z, "S")
             for u in range(2):
-                park_grad(1, 1, u, 4 + u)
-                transpose_x(0, 0, u, u)
-            both(quantize, "dz1_t", 0)
+                park_grad(1, 1, u, (5, 2)[u])
+            quantize("x_t", 0, 0)
             quantize("dz2", 0, 1)
-            copy_x_t(0, 0, 0, "S")
             for t in range(4):
-                hidden_pass(0, 0, 1, t, (2, 3, 6, 7)[t])
+                hidden_pass(0, 0, 1, t, (3, 1, 7, 4)[t])
             for v in range(2):
                 both(square_y, 1, 1, v)
                 both(make_dz2, 1, 1, v)
             both(quantize, "dz2", 1, 1)
+            interleave_dz1(1, 0, "S", slice(384, HALF))
             for z in range(2):
-                transpose_x(0, 1, z, 4 * z)
-            copy_x_t(0, 0, 1, "S")
+                transpose_x(0, 1, z, 6 * z)
             for t in range(2):
-                hidden_pass(0, 1, 1, t, 1 + 4 * t)
+                hidden_pass(0, 1, 1, t, (5, 2)[t])
             for t in range(4):
                 hidden_pass(1, 0, 1, t)
             for t in range(2):
                 hidden_pass(1, 1, 1, t)
             copy_x_t(0, 1, 0, "S")
-            quantize("x_t", 0, 0)
-            quantize("dz1", 1, 0)
+            quantize("dz1_t", 0, 0)
+            quantize("dz1", 0, 0)
             both(square_mem, 0, 1)
             for t in range(4):
                 make_dz1(0, 1, t)
             copy_x_t(0, 1, 1, "S")
             transpose_x(1, 0, 0, 0)
-            transpose_dz1(0, 1, 0, 2)
+            transpose_dz1(0, 1, 0, 3)
             for t in range(2):
-                out_pass(0, "out_1", 0, t, 0, 3 + 3 * t)
-            transpose_dz1(0, 1, 1, 7)
-            transpose_x(1, 0, 1, 4)
+                out_pass(0, "out_1", 0, t, 0, (1, 7)[t])
+            transpose_dz1(0, 1, 1, 4)
+            transpose_x(1, 0, 1, 6)
             copy_dz1_t(0, 1, 0, "S")
             copy_x_t(1, 0, 0, "S")
             copy_dz1_t(0, 1, 1, "S")
             quantize("x_t", 1, 0)
             quantize("dz1_t", 1, 0, 0)
-            interleave_dz1(0, 1, "V", 0)
+            quantize("dz1_t", 0, 1)
             copy_x_t(1, 0, 1, "V")
             quantize("dz1_t", 1, 0, 1)
+            interleave_dz1(0, 1, "G", slice(0, 384), "handed_on", 1)
             for t in range(2):
                 out_pass(1, "out_1", 0, t, 0)
             for z in range(2):
-                transpose_x(1, 1, z, 2 * z)
+                transpose_x(1, 1, z, 3 * z)
             for t in range(2, 4):
-                out_product("out_1", 0, t, 0, (7, 4)[t - 2])
+                out_product("out_1", 0, t, 0, (4, 6)[t - 2])
             square_mem(1, 1, 0)
             copy_x_t(1, 1, 0, "V")
             for t in range(2):
@@ -454,14 +487,15 @@ def tile_pt_grumb_pb_v_kernel(
             copy_x_t(1, 1, 1, "V")
             for h in range(2):
                 quantize("x_t", h, 1)
+            raw("w_rg", 0)
             for t in range(2):
                 out_copy("out_1", 0, t, 0, "S")
             store_columns("out_1", 0, 0, 0)
             for t in range(2, 4):
                 for k in range(2):
-                    hidden_pass(k, 1, 1, t, (1, 5)[t - 2])
+                    hidden_pass(k, 1, 1, t, (5, 2)[t - 2])
             operand["w_rg"] = codes_pair("w_hid")
-            transpose_dz1(1, 1, 0, 3)
+            transpose_dz1(1, 1, 0, 1)
             square_mem(1, 1, 1)
             for t in range(2, 4):
                 out_copy("out_1", 0, t, 0, "S")
@@ -472,26 +506,27 @@ def tile_pt_grumb_pb_v_kernel(
             for z in range(2):
                 for k in range(2):
                     for t in range(2 * z, 2 * z + 2):
-                        out_pass(k, "out_1", 0, t, 1, (6, 0, 2, 7)[t])
-            transpose_dz1(1, 1, 1, 4)
-            interleave_dz1(0, 1, "V", 1)
+                        out_pass(k, "out_1", 0, t, 1, (7, 0, 3, 4)[t])
+            transpose_dz1(1, 1, 1, 6)
+            interleave_dz1(0, 1, "V", slice(384, HALF))
             quantize("dz1_t", 1, 1, 0)
             interleave_dz1(1, 1, "V")
             copy_dz1_t(1, 1, 1, "V")
-            quantize("dz1", 0, 1)
+            quantize("dz1", 1, 0)
             quantize("dz1_t", 1, 1, 1)
             for z in range(2):
                 for t in range(2 * z, 2 * z + 2):
                     out_copy("out_1", 0, t, 1, "S")
                 store_columns("out_1", 0, z, 1)
-            interleave_w_rg(0, 0, 0, "V")
-            quantize("dz1", 1, 1)
-            interleave_w_rg(1, 0, 0, "V")
+            for k in range(2):
+                interleave_w_rg(k, 0, 0, "V")
             for k in range(2):
                 quantize("w_rg", k, 0, 0)
+            for g in range(2):
+                quantize("dz1", g, 1)
             for t in range(4):
                 for n in range(2):
-                    out_product("out_1", 1, t, n, (3, 1, 5, 6, 0, 2, 7, 4)[2 * t + n])
+                    out_product("out_1", 1, t, n, (1, 5, 2, 7, 0, 3, 4, 6)[2 * t + n])
                     out_copy("out_1", 1, t, n, "S")
                 store_row("out_1", 1, t)
             for c, z in ((0, 1), (1, 0), (1, 1)):
@@ -502,8 +537,8 @@ def tile_pt_grumb_pb_v_kernel(
             for c in range(2):
                 for t in range(4):
                     for h in range(2):
-                        out_product("out_0", c, t, h, (3, 1, 5, 6, 0, 2, 7, 4)[2 * t + h])
-                        out_copy("out_0", c, t, h, "V" if h and 4 * c + t >= 3 else "S")
+                        out_product("out_0", c, t, h, (1, 5, 2, 7, 0, 3, 4, 6)[2 * t + h])
+                        out_copy("out_0", c, t, h, "V" if h and 4 * c + t >= 4 else "S")
                         if c == 1 and t == 3:
                             store_piece("out_0", c, t, h)
                     if c == 0 or t < 3:

@@ -423,7 +423,7 @@ def tile_pt_grumb_pb_v_kernel(
             transpose_dz1(0, 0, 1, 1)
             for t in range(4):
                 make_dz1(1, 0, t)
-            interleave_dz1(1, 0, "G", slice(0, 384), "by_gpsimd", 2)
+            interleave_dz1(1, 0, "G", slice(0, 256), "by_gpsimd", 2)
             copy_dz1_t(0, 0, 1, "V")
             for z in range(2):
                 transpose_dz1(1, 0, z, (7, 4)[z])
@@ -443,7 +443,7 @@ def tile_pt_grumb_pb_v_kernel(
                 both(square_y, 1, 1, v)
                 both(make_dz2, 1, 1, v)
             both(quantize, "dz2", 1, 1)
-            interleave_dz1(1, 0, "S", slice(384, HALF))
+            interleave_dz1(1, 0, "S", slice(256, HALF))
             for z in range(2):
                 transpose_x(0, 1, z, 6 * z)
             for t in range(2):
@@ -473,7 +473,7 @@ def tile_pt_grumb_pb_v_kernel(
             quantize("dz1_t", 0, 1)
             copy_x_t(1, 0, 1, "V")
             quantize("dz1_t", 1, 0, 1)
-            interleave_dz1(0, 1, "G", slice(0, 384), "handed_on", 1)
+            interleave_dz1(0, 1, "G", slice(0, 256), "handed_on", 1)
             for t in range(2):
                 out_pass(1, "out_1", 0, t, 0)
             for z in range(2):
@@ -508,7 +508,7 @@ def tile_pt_grumb_pb_v_kernel(
                     for t in range(2 * z, 2 * z + 2):
                         out_pass(k, "out_1", 0, t, 1, (7, 0, 3, 4)[t])
             transpose_dz1(1, 1, 1, 6)
-            interleave_dz1(0, 1, "V", slice(384, HALF))
+            interleave_dz1(0, 1, "V", slice(256, HALF))
             quantize("dz1_t", 1, 1, 0)
             interleave_dz1(1, 1, "V")
             copy_dz1_t(1, 1, 1, "V")
@@ -538,7 +538,7 @@ def tile_pt_grumb_pb_v_kernel(
                 for t in range(4):
                     for h in range(2):
                         out_product("out_0", c, t, h, (1, 5, 2, 7, 0, 3, 4, 6)[2 * t + h])
-                        out_copy("out_0", c, t, h, "V" if h and 4 * c + t >= 4 else "S")
+                        out_copy("out_0", c, t, h, "V" if h and 4 * c + t >= 5 else "S")
                         if c == 1 and t == 3:
                             store_piece("out_0", c, t, h)
                     if c == 0 or t < 3:

@@ -101,7 +101,10 @@ def tile_pt_grumb_pb_v_kernel(
 
         def quantize(name, k, c, part=None):
             codes, scales = operand[name]
-            grouped = held[name, k, c][:] if part is None else held[name, k, c][:, quarter(part), :]
+            if (name, k, c, part) in held:
+                grouped = held[name, k, c, part][:]
+            else:
+                grouped = held[name, k, c][:] if part is None else held[name, k, c][:, quarter(part), :]
             cols = half(c) if part is None else quarter(2 * c + part)
             nc.vector.quantize_mx(
                 out=codes[k][:, cols].bitcast(fp8[name]),
@@ -160,10 +163,10 @@ def tile_pt_grumb_pb_v_kernel(
         load_order = [
             (load_half, "w_hid", 0, 0),
             (load_half, "w_hid", 0, 1),
+            (load_half, "w_hid", 1, 0),
             (load_half, "grad", 0, 0),
             (load_y, 0, 0, 0),
             (load_y, 0, 0, 1),
-            (load_half, "w_hid", 1, 0),
             (load_half, "grad", 1, 0),
             (load_y, 1, 0, 0),
             (load_y, 1, 0, 1),
@@ -284,6 +287,10 @@ def tile_pt_grumb_pb_v_kernel(
                 held["dz1_ps", g, h, part][:].rearrange("p c j -> p (c j)").bitcast(F32),
             )
 
+        def interleave_dz1_part(g, h, part, engine, tag, bufs):
+            held["dz1", g, h, part] = grouped_tile(QUARTER, tag, bufs)
+            interleave(engine, held["dz1", g, h, part][:], dz1[g][h][:, :, quarter(part)])
+
         def hidden_pass(k, g, h, t, side=None):
             if k == 0:
                 held["dh", g, h, t] = bank(side, [P, HALF])
@@ -378,17 +385,18 @@ def tile_pt_grumb_pb_v_kernel(
         make_identity(nc, ident[:])
 
         with tc.manual_schedule():
-            for g in range(2):
-                interleave_w_hid(0, g, "V")
-            both(quantize, "w_hid", 0)
+            interleave_w_hid(0, 0, "V")
+            interleave_w_hid(0, 1, "S")
+            quantize("w_hid", 0, 0)
+            interleave_w_hid(1, 0, "V")
+            quantize("w_hid", 1, 0)
+            quantize("w_hid", 0, 1)
             for u in range(2):
                 park_grad(0, 0, u, 4 + u)
             for v in range(2):
                 both(square_y, 0, 0, v)
                 both(make_dz2, 0, 0, v)
-            interleave_w_hid(1, 0, "V")
             quantize("dz2", 0, 0)
-            quantize("w_hid", 1, 0)
             for u in range(2):
                 park_grad(1, 0, u, 6 + u)
             for t in range(4):
@@ -423,7 +431,7 @@ def tile_pt_grumb_pb_v_kernel(
             transpose_dz1(0, 0, 1, 1)
             for t in range(4):
                 make_dz1(1, 0, t)
-            interleave_dz1(1, 0, "G", slice(0, 256), "by_gpsimd", 2)
+            interleave_dz1_part(1, 0, 0, "G", "by_gpsimd", 2)
             copy_dz1_t(0, 0, 1, "V")
             for z in range(2):
                 transpose_dz1(1, 0, z, (7, 4)[z])
@@ -443,7 +451,6 @@ def tile_pt_grumb_pb_v_kernel(
                 both(square_y, 1, 1, v)
                 both(make_dz2, 1, 1, v)
             both(quantize, "dz2", 1, 1)
-            interleave_dz1(1, 0, "S", slice(256, HALF))
             for z in range(2):
                 transpose_x(0, 1, z, 6 * z)
             for t in range(2):
@@ -455,6 +462,7 @@ def tile_pt_grumb_pb_v_kernel(
             copy_x_t(0, 1, 0, "S")
             quantize("dz1_t", 0, 0)
             quantize("dz1", 0, 0)
+            interleave_dz1_part(1, 0, 1, "G", "by_gpsimd", 2)
             both(square_mem, 0, 1)
             for t in range(4):
                 make_dz1(0, 1, t)
@@ -512,7 +520,7 @@ def tile_pt_grumb_pb_v_kernel(
             quantize("dz1_t", 1, 1, 0)
             interleave_dz1(1, 1, "V")
             copy_dz1_t(1, 1, 1, "V")
-            quantize("dz1", 1, 0)
+            both(quantize, "dz1", 1, 0)
             quantize("dz1_t", 1, 1, 1)
             for z in range(2):
                 for t in range(2 * z, 2 * z + 2):
@@ -538,7 +546,7 @@ def tile_pt_grumb_pb_v_kernel(
                 for t in range(4):
                     for h in range(2):
                         out_product("out_0", c, t, h, (1, 5, 2, 7, 0, 3, 4, 6)[2 * t + h])
-                        out_copy("out_0", c, t, h, "V" if h and 4 * c + t >= 5 else "S")
+                        out_copy("out_0", c, t, h, "V" if h and 4 * c + t >= 4 else "S")
                         if c == 1 and t == 3:
                             store_piece("out_0", c, t, h)
                     if c == 0 or t < 3:

@@ -17,14 +17,12 @@ P = 128
 PACK = 4
 HALF = 512
 QUARTER = 256
-PIECES = 14
-SLABS = 1
+AREA_BYTES = 4096
+AREAS = 16
 GROUPED = 5
-TURNED = 5
-Y_SQUARED = 5
+TURNED = 7
+Y_SQUARED = 4
 MEM_SQUARED = 4
-PIECE_BYTES = 4096
-HANDED_ON = ("dz1_t", 1, 0)
 
 FLOPS = 3 * 2 * SIZE * SIZE * SIZE
 BYTES = 4 * SIZE * SIZE * 2 + 2 * SIZE * SIZE * 4 + 2 * SIZE * SIZE * 4
@@ -40,6 +38,7 @@ def tile_pt_grumb_pb_v_kernel(
 
     hbm = {
         "w_hid": rows_by_four(w_hid_out),
+        "w_rg": rows_by_four(w_readgate),
         "y": rows_by_four(y),
         "grad": rows_by_four(grad_out),
         "mem": rows_by_four(mem_out),
@@ -68,13 +67,16 @@ def tile_pt_grumb_pb_v_kernel(
         ident = keep_tile([P, P], F32, "ident")
         ident_bf16 = keep_tile([P, P], BF16, "ident_bf16")
         minus_half = keep_tile([P, 1], F32, "minus_half")
-        held = {}
+        held = {"next_area": 0}
 
         def work_tile(shape, dtype, tag, bufs):
             return work.tile(shape, dtype, name=tag, tag=tag, align_bytes=256, bufs=bufs)
 
-        def piece(shape, dtype):
-            return moved.tile(shape, dtype, name="piece", tag="piece", align_bytes=2048, bufs=PIECES, offset=0)
+        def area(shape, dtype, count):
+            first = held["next_area"] if held["next_area"] + count <= AREAS else 0
+            held["next_area"] = first + count
+            tag = "area_%d_%d" % (first, count)
+            return moved.tile(shape, dtype, name=tag, tag=tag, align_bytes=2048, bufs=1, offset=first * AREA_BYTES)
 
         def grouped_tile(columns, tag="grouped", bufs=GROUPED):
             return work_tile([P, columns, PACK], BF16, tag, bufs)
@@ -112,53 +114,69 @@ def tile_pt_grumb_pb_v_kernel(
                 in_=grouped.rearrange("p n j -> p (n j)"),
             )
 
-        def product_pass(k, out, lhs, lhs_first, rhs, rhs_half):
+        def product_pass(k, out, lhs, lhs_first, rhs, rhs_cols):
             lhs_cols = slice(lhs_first, lhs_first + P)
             nc.tensor.matmul_mx(
                 out=out,
                 lhsT=operand[lhs][0][k][:, lhs_cols].bitcast(fp8[lhs]),
                 lhsT_scale=operand[lhs][1][k][:, lhs_cols],
-                rhs=operand[rhs][0][k][:, half(rhs_half)].bitcast(fp8[rhs]),
-                rhs_scale=operand[rhs][1][k][:, half(rhs_half)],
+                rhs=operand[rhs][0][k][:, rhs_cols].bitcast(fp8[rhs]),
+                rhs_scale=operand[rhs][1][k][:, rhs_cols],
                 start=(k == 0),
                 stop=(k == 1),
             )
 
         def load_half(name, k, c):
-            held["raw", name, k, c] = piece([P, PACK, HALF], BF16)
-            nc.sync.dma_start(out=held["raw", name, k, c][:], in_=hbm[name][k][:, :, half(c)])
-
-        def slab(shape, dtype):
-            return moved.tile(shape, dtype, name="slab", tag="slab", align_bytes=2048, bufs=SLABS, offset=PIECES * PIECE_BYTES)
+            tile = area([P, PACK, HALF], BF16, 1)
+            nc.sync.dma_start(out=tile[:], in_=hbm[name][k][:, :, half(c)])
+            held["raw", name, k, c] = tile[:]
 
         def load_rows(name, k):
-            tile = slab([P, PACK, SIZE], BF16)
+            tile = area([P, PACK, SIZE], BF16, 2)
             nc.sync.dma_start(out=tile[:], in_=hbm[name][k])
             for c in range(2):
                 held["raw", name, k, c] = tile[:, :, half(c)]
 
-        def load_mem_quarter(g, h):
-            tile = slab([P, PACK, HALF], F32)
-            nc.sync.dma_start(out=tile[:], in_=hbm["mem"][g][:, :, half(h)])
-            for z in range(2):
-                held["raw", "mem", g, h, z] = tile[:, pair(z), :]
+        def load_y(k, h, v=None):
+            if v is None:
+                tile = area([P, PACK, HALF], F32, 2)
+                nc.sync.dma_start(out=tile[:], in_=hbm["y"][k][:, :, half(h)])
+                held["raw", "y", k, h, None] = tile[:]
+                for part in range(2):
+                    held["raw", "y", k, h, part] = tile[:, :, quarter(part)]
+            else:
+                tile = area([P, PACK, QUARTER], F32, 1)
+                nc.sync.dma_start(out=tile[:], in_=hbm["y"][k][:, :, quarter(2 * h + v)])
+                held["raw", "y", k, h, v] = tile[:]
 
-        def load_y(k, h, v):
-            held["raw", "y", k, h, v] = piece([P, PACK, QUARTER], F32)
-            nc.sync.dma_start(out=held["raw", "y", k, h, v][:], in_=hbm["y"][k][:, :, quarter(2 * h + v)])
-
-        def load_mem(g, h, z):
-            held["raw", "mem", g, h, z] = piece([P, 2, HALF], F32)
-            nc.sync.dma_start(out=held["raw", "mem", g, h, z][:], in_=hbm["mem"][g][:, pair(z), half(h)])
+        def load_mem(g, h, z=None):
+            if z is None:
+                tile = area([P, PACK, HALF], F32, 2)
+                nc.sync.dma_start(out=tile[:], in_=hbm["mem"][g][:, :, half(h)])
+                for part in range(2):
+                    held["raw", "mem", g, h, part] = tile[:, pair(part), :]
+            else:
+                tile = area([P, 2, HALF], F32, 1)
+                nc.sync.dma_start(out=tile[:], in_=hbm["mem"][g][:, pair(z), half(h)])
+                held["raw", "mem", g, h, z] = tile[:]
 
         def load_w_rg():
-            at = PIECES * PIECE_BYTES + SLABS * 2 * PIECE_BYTES
-            tile = moved.tile([P, 2, PACK, SIZE], BF16, name="w_rg_raw", tag="w_rg_raw", align_bytes=2048, bufs=1, offset=at)
+            tile = moved.tile([P, 2, PACK, SIZE], BF16, name="w_rg_raw", tag="w_rg_raw", align_bytes=2048, bufs=1, offset=AREAS * AREA_BYTES)
             nc.sync.dma_start(
                 out=tile[:].rearrange("p k j c -> p k (j c)"), in_=w_readgate.rearrange("(k p j) c -> p k (j c)", p=P, j=PACK)
             )
             for k in range(2):
-                held["raw", "w_rg", k] = tile[:, k]
+                for c in range(2):
+                    held["raw", "w_rg", k, c] = tile[:, k, :, half(c)]
+
+        def load_grad(h):
+            tile = area([P, 2, PACK, HALF], BF16, 2)
+            nc.sync.dma_start(
+                out=tile[:].rearrange("p k j c -> p (k j) c"),
+                in_=grad_out.rearrange("(k p j) c -> p k j c", p=P, j=PACK)[:, :, :, half(h)],
+            )
+            for k in range(2):
+                held["raw", "grad", k, h] = tile[:, k]
 
         load_order = [
             (load_half, "w_hid", 0, 0),
@@ -175,20 +193,20 @@ def tile_pt_grumb_pb_v_kernel(
             (load_mem, 0, 0, 1),
             (load_mem, 1, 0, 0),
             (load_mem, 1, 0, 1),
-            (load_half, "x", 0, 0),
-            (load_half, "grad", 0, 1),
             (load_y, 0, 1, 0),
+            (load_half, "grad", 0, 1),
             (load_y, 0, 1, 1),
+            (load_half, "x", 0, 0),
             (load_half, "grad", 1, 1),
             (load_y, 1, 1, 0),
             (load_y, 1, 1, 1),
             (load_half, "x", 0, 1),
             (load_mem, 0, 1, 0),
             (load_mem, 0, 1, 1),
-            (load_half, "x", 1, 0),
-            (load_half, "x", 1, 1),
             (load_mem, 1, 1, 0),
+            (load_half, "x", 1, 0),
             (load_mem, 1, 1, 1),
+            (load_half, "x", 1, 1),
             (load_w_rg,),
         ]
         issued = set()
@@ -201,20 +219,21 @@ def tile_pt_grumb_pb_v_kernel(
             return held[("raw",) + key]
 
         def square_y(k, h, v, u):
-            t = work_tile([P, P // 2, 2, PACK], F32, "y_squared", Y_SQUARED)
+            words = P if v is None else P // 2
+            t = work_tile([P, words, 2, PACK], F32, "y_squared", Y_SQUARED)
             nc.scalar.activation(
                 out=t[:].rearrange("p w e j -> p w j e"),
-                in_=raw("y", k, h, v)[:].rearrange("p j (w u e) -> p u w j e", u=2, e=2)[:, u],
+                in_=raw("y", k, h, v).rearrange("p j (w u e) -> p u w j e", u=2, e=2)[:, u],
                 func=ACT.Square,
             )
             held["y_squared", k, h, v, u] = t
 
-        def park_grad(k, h, u, side):
-            ps = bank(side, [P, PACK, P, 2], BF16)
-            source = raw("grad", k, h)[:].rearrange("p j (w u e) -> p u j w e", u=2, e=2)[:, u]
-            for z in range(2):
-                nc.tensor.matmul(out=ps[:, pair(z)], lhsT=ident_bf16[:], rhs=source[:, pair(z)], start=True, stop=True)
-            held["grad_ps", k, h, u] = ps
+        def park_grad(k, h, v, side):
+            ps = bank(side, [P, 2, PACK, P // 2, 2], BF16)
+            source = raw("grad", k, h)[:, :, quarter(v)].rearrange("p j (w u e) -> p u j w e", u=2, e=2)
+            for u in range(2):
+                nc.tensor.matmul(out=ps[:, u], lhsT=ident_bf16[:], rhs=source[:, u], start=True, stop=True)
+            held["grad_ps", k, h, v] = ps
 
         def make_dz2(k, h, v, u):
             if ("dz2", k, h) not in held:
@@ -224,7 +243,7 @@ def tile_pt_grumb_pb_v_kernel(
                 out=held["dz2", k, h][:, first : first + P, :],
                 in0=held["y_squared", k, h, v, u][:].rearrange("p w e j -> p (w e) j"),
                 scalar=1.0,
-                in1=held["grad_ps", k, h, u][:].rearrange("p j w e -> p (w e) j")[:, v * P : (v + 1) * P, :],
+                in1=held["grad_ps", k, h, v][:, u].rearrange("p j w e -> p (w e) j"),
                 op0=ALU.subtract,
                 op1=ALU.mult,
             )
@@ -233,20 +252,18 @@ def tile_pt_grumb_pb_v_kernel(
             sq = work_tile([P, 2, 2, QUARTER], F32, "mem_squared", MEM_SQUARED)
             nc.scalar.activation(
                 out=sq[:].rearrange("p u a (w e) -> p u (a w) e", e=2),
-                in_=raw("mem", g, h, z)[:].rearrange("p a (w u e) -> p u (a w) e", u=2, e=2),
+                in_=raw("mem", g, h, z).rearrange("p a (w u e) -> p u (a w) e", u=2, e=2),
                 func=ACT.Square,
                 bias=minus_half[:],
             )
             held["mem_squared", g, h, z] = sq
 
-        def interleave_w_hid(k, g, engine, part=None):
-            if ("w_hid", k, g) not in held:
-                held["w_hid", k, g] = grouped_tile(HALF)
-            rows = slice(0, P) if part is None else slice(part * P // 2, (part + 1) * P // 2)
+        def interleave_w_hid(k, g, engine):
+            held["w_hid", k, g] = grouped_tile(HALF)
             move(
                 engine,
-                held["w_hid", k, g][:].rearrange("p (t m) j -> p m j t", t=PACK)[:, rows],
-                raw("w_hid", k, g)[:].rearrange("p j (m t) -> p m j t", t=PACK)[:, rows],
+                held["w_hid", k, g][:].rearrange("p (t m) j -> p m j t", t=PACK),
+                raw("w_hid", k, g).rearrange("p j (m t) -> p m j t", t=PACK),
             )
 
         def interleave(engine, grouped, rows):
@@ -255,46 +272,21 @@ def tile_pt_grumb_pb_v_kernel(
             else:
                 move(engine, grouped.rearrange("p (c i) j -> p c j i", i=4), rows.rearrange("p j (c i) -> p c j i", i=4))
 
-        def interleave_w_rg(k, c, z, engine):
-            if ("w_rg", k, c) not in held:
-                held["w_rg", k, c] = grouped_tile(HALF)
-            interleave(engine, held["w_rg", k, c][:, quarter(z), :], raw("w_rg", k)[:, :, quarter(2 * c + z)])
+        def rows_of(name, k, c):
+            return dz1[k][c][:] if name == "dz1" else raw(name, k, c)
 
-        def interleave_dz1(g, h, engine, cols=slice(0, HALF), tag="grouped", bufs=GROUPED):
-            if ("dz1", g, h) not in held:
-                held["dz1", g, h] = grouped_tile(HALF, tag, bufs)
-            interleave(engine, held["dz1", g, h][:, cols, :], dz1[g][h][:, :, cols])
-
-        def interleave_on_tensor(g, h, part, side):
-            ps = bank(side, [P, QUARTER, PACK], BF16)
-            for s in range(2):
-                first = part * QUARTER + s * P
-                nc.tensor.matmul(
-                    out=ps[:, s * P : (s + 1) * P, :].rearrange("p c j -> p j c"),
-                    lhsT=ident_bf16[:],
-                    rhs=dz1[g][h][:, :, first : first + P],
-                    start=True,
-                    stop=True,
-                )
-            held["dz1_ps", g, h, part] = ps
-
-        def copy_interleaved(g, h, part, engine):
-            if ("dz1", g, h) not in held:
-                held["dz1", g, h] = grouped_tile(HALF)
-            move(
-                engine,
-                held["dz1", g, h][:, quarter(part), :].rearrange("p c j -> p (c j)").bitcast(F32),
-                held["dz1_ps", g, h, part][:].rearrange("p c j -> p (c j)").bitcast(F32),
-            )
-
-        def interleave_dz1_part(g, h, part, engine, tag, bufs):
-            held["dz1", g, h, part] = grouped_tile(QUARTER, tag, bufs)
-            interleave(engine, held["dz1", g, h, part][:], dz1[g][h][:, :, quarter(part)])
+        def group(name, k, c, engine, part=None, tag="grouped", bufs=GROUPED):
+            if part is None:
+                held[name, k, c] = grouped_tile(HALF, tag, bufs)
+                interleave(engine, held[name, k, c][:], rows_of(name, k, c))
+            else:
+                held[name, k, c, part] = grouped_tile(QUARTER, tag, bufs)
+                interleave(engine, held[name, k, c, part][:], rows_of(name, k, c)[:, :, quarter(part)])
 
         def hidden_pass(k, g, h, t, side=None):
             if k == 0:
                 held["dh", g, h, t] = bank(side, [P, HALF])
-            product_pass(k, held["dh", g, h, t][:], "w_hid", g * HALF + t * P, "dz2", h)
+            product_pass(k, held["dh", g, h, t][:], "w_hid", g * HALF + t * P, "dz2", half(h))
 
         def make_dz1(g, h, t):
             nc.vector.scalar_tensor_tensor(
@@ -316,31 +308,29 @@ def tile_pt_grumb_pb_v_kernel(
             held["dz1_t_ps", g, h, z] = ps
 
         def transpose_x(n, h, z, side):
-            words = raw("x", n, h)[:].rearrange("p a b -> p (a b)").bitcast(F32)
+            words = raw("x", n, h).bitcast(F32)
             ps = bank(side, [P, 2, 2, P])
             for a in range(2):
                 for u in range(2):
-                    first = (2 * z + a) * QUARTER + u
-                    nc.tensor.transpose(ps[:, a, u, :], words[:, first : first + QUARTER - 1 : 2], ident[:])
+                    nc.tensor.transpose(ps[:, a, u, :], words[:, 2 * z + a, u : u + QUARTER - 1 : 2], ident[:])
             held["x_t_ps", n, h, z] = ps
 
-        def turned_words(name, h, c):
+        def turned_words(name, h, c, tag, bufs):
             if (name, h, c) not in held:
-                tag, bufs = ("handed_on", 1) if (name, h, c) == HANDED_ON else ("turned", TURNED)
                 held[name, h, c] = grouped_tile(HALF, tag, bufs)
             return held[name, h, c][:].rearrange("p n j -> p (n j)").bitcast(F32)
 
-        def copy_dz1_t(g, h, z, engine):
+        def copy_dz1_t(g, h, z, engine, tag="turned", bufs=TURNED):
             move(
                 engine,
-                turned_words("dz1_t", h, g)[:, half(z)].rearrange("p (a r u) -> p a r u", a=2, u=2),
+                turned_words("dz1_t", h, g, tag, bufs)[:, half(z)].rearrange("p (a r u) -> p a r u", a=2, u=2),
                 held["dz1_t_ps", g, h, z][:].rearrange("p a u r -> p a r u"),
             )
 
-        def copy_x_t(n, h, z, engine):
+        def copy_x_t(n, h, z, engine, tag="turned", bufs=TURNED):
             move(
                 engine,
-                turned_words("x_t", h, n).rearrange("p (r z a u) -> p z r a u", z=2, a=2, u=2)[:, z],
+                turned_words("x_t", h, n, tag, bufs).rearrange("p (r z a u) -> p z r a u", z=2, a=2, u=2)[:, z],
                 held["x_t_ps", n, h, z][:].rearrange("p a u r -> p r a u"),
             )
 
@@ -348,19 +338,16 @@ def tile_pt_grumb_pb_v_kernel(
             if k == 0:
                 held["ps", name, c, t, n] = bank(side, [P, HALF])
             lhs, rhs = ("w_rg", "dz1") if name == "out_0" else ("dz1_t", "x_t")
-            product_pass(k, held["ps", name, c, t, n][:], lhs, c * HALF + t * P, rhs, n)
+            product_pass(k, held["ps", name, c, t, n][:], lhs, c * HALF + t * P, rhs, half(n))
 
         def out_product(name, c, t, n, side):
             for k in range(2):
                 out_pass(k, name, c, t, n, side)
 
-        def by_columns(name, c):
-            return name == "out_1" and c == 0
-
-        def out_copy(name, c, t, n, engine):
-            key, place = ((name, c, t // 2, n), t % 2) if by_columns(name, c) else ((name, c, t), n)
+        def out_copy(name, c, t, n, engine, by_columns=False):
+            key, place = ((name, c, t // 2, n), t % 2) if by_columns else ((name, c, t), n)
             if key not in held:
-                held[key] = piece([P, 2, HALF], F32)
+                held[key] = area([P, 2, HALF], F32, 1)
             staged, ps = held[key][:, place, :], held["ps", name, c, t, n][:]
             if name == "out_0":
                 staged = staged.rearrange("p (w u e) -> p w u e", u=2, e=2)
@@ -391,161 +378,157 @@ def tile_pt_grumb_pb_v_kernel(
             interleave_w_hid(1, 0, "V")
             quantize("w_hid", 1, 0)
             quantize("w_hid", 0, 1)
-            for u in range(2):
-                park_grad(0, 0, u, 4 + u)
+            for v in range(2):
+                park_grad(0, 0, v, 6 + v)
             for v in range(2):
                 both(square_y, 0, 0, v)
                 both(make_dz2, 0, 0, v)
+                park_grad(1, 0, v, 6 + v)
             quantize("dz2", 0, 0)
-            for u in range(2):
-                park_grad(1, 0, u, 6 + u)
             for t in range(4):
                 hidden_pass(0, 0, 0, t, t)
+            for t in range(2):
+                hidden_pass(0, 1, 0, t, 4 + t)
             for v in range(2):
                 both(square_y, 1, 0, v)
                 both(make_dz2, 1, 0, v)
-            for t in range(2):
-                hidden_pass(0, 1, 0, t, 6 + t)
             both(quantize, "dz2", 1, 0)
             for t in range(4):
                 hidden_pass(1, 0, 0, t)
+            for t in range(2, 4):
+                hidden_pass(0, 1, 0, t, 4 + t)
             both(square_mem, 0, 0)
             interleave_w_hid(1, 1, "V")
             for t in range(2):
                 make_dz1(0, 0, t)
-            for t in range(2, 4):
-                hidden_pass(0, 1, 0, t, 2 + t)
             transpose_dz1(0, 0, 0, 0)
             quantize("w_hid", 1, 1)
             for t in range(2, 4):
                 make_dz1(0, 0, t)
-            interleave_dz1(0, 0, "G", slice(0, HALF), "by_gpsimd", 2)
+            group("dz1", 0, 0, "G", None, "by_gpsimd", 1)
             for t in range(4):
                 hidden_pass(1, 1, 0, t)
             both(square_mem, 1, 0)
-            copy_dz1_t(0, 0, 0, "S")
-            for z in range(2):
-                transpose_x(0, 0, z, 2 + z)
-                copy_x_t(0, 0, z, "S")
-            park_grad(0, 1, 0, 0)
+            both(square_y, 0, 1, 0)
             transpose_dz1(0, 0, 1, 1)
+            park_grad(0, 1, 0, 2)
+            for z in range(2):
+                copy_dz1_t(0, 0, z, "S")
             for t in range(4):
                 make_dz1(1, 0, t)
-            interleave_dz1_part(1, 0, 0, "G", "by_gpsimd", 2)
-            copy_dz1_t(0, 0, 1, "V")
-            for z in range(2):
-                transpose_dz1(1, 0, z, (7, 4)[z])
-            park_grad(0, 1, 1, 6)
-            for v in range(2):
-                both(square_y, 0, 1, v)
-                both(make_dz2, 0, 1, v)
+            transpose_dz1(1, 0, 0, 3)
+            park_grad(0, 1, 1, 4)
+            transpose_dz1(1, 0, 1, 0)
+            both(make_dz2, 0, 1, 0)
+            both(square_y, 0, 1, 1)
+            both(make_dz2, 0, 1, 1)
+            both(quantize, "dz2", 0, 1)
             for z in range(2):
                 copy_dz1_t(1, 0, z, "S")
-            for u in range(2):
-                park_grad(1, 1, u, (5, 2)[u])
-            quantize("x_t", 0, 0)
-            quantize("dz2", 0, 1)
+            for z in range(2):
+                transpose_x(0, 0, z, 5 + z)
+            park_grad(1, 1, 0, 7)
             for t in range(4):
-                hidden_pass(0, 0, 1, t, (3, 1, 7, 4)[t])
+                hidden_pass(0, 0, 1, t, 1 + t)
+            copy_x_t(0, 0, 0, "S")
+            quantize("dz1_t", 0, 0)
+            quantize("dz1", 0, 0)
+            group("dz1", 1, 0, "G", 0, "by_gpsimd", 1)
+            copy_x_t(0, 0, 1, "V")
+            park_grad(1, 1, 1, 6)
+            for z in range(2):
+                transpose_x(0, 1, z, (5, 0)[z])
             for v in range(2):
                 both(square_y, 1, 1, v)
                 both(make_dz2, 1, 1, v)
+                hidden_pass(0, 1, 1, v, 7 - v)
             both(quantize, "dz2", 1, 1)
-            for z in range(2):
-                transpose_x(0, 1, z, 6 * z)
-            for t in range(2):
-                hidden_pass(0, 1, 1, t, (5, 2)[t])
             for t in range(4):
                 hidden_pass(1, 0, 1, t)
             for t in range(2):
                 hidden_pass(1, 1, 1, t)
+            quantize("x_t", 0, 0)
+            quantize("dz1", 1, 0, 0)
+            group("dz1", 1, 0, "G", 1, "by_gpsimd", 1)
             copy_x_t(0, 1, 0, "S")
-            quantize("dz1_t", 0, 0)
-            quantize("dz1", 0, 0)
-            interleave_dz1_part(1, 0, 1, "G", "by_gpsimd", 2)
             both(square_mem, 0, 1)
+            copy_x_t(0, 1, 1, "S")
             for t in range(4):
                 make_dz1(0, 1, t)
-            copy_x_t(0, 1, 1, "S")
+            for k in range(2):
+                hidden_pass(k, 1, 1, 2, 5)
+            transpose_dz1(0, 1, 0, 1)
             transpose_x(1, 0, 0, 0)
-            transpose_dz1(0, 1, 0, 3)
-            for t in range(2):
-                out_pass(0, "out_1", 0, t, 0, (1, 7)[t])
-            transpose_dz1(0, 1, 1, 4)
-            transpose_x(1, 0, 1, 6)
+            out_pass(0, "out_1", 0, 0, 0, 2)
+            for k in range(2):
+                hidden_pass(k, 1, 1, 3, 3)
+            square_mem(1, 1, 0)
             copy_dz1_t(0, 1, 0, "S")
             copy_x_t(1, 0, 0, "S")
+            transpose_dz1(0, 1, 1, 4)
+            transpose_x(1, 0, 1, 0)
+            square_mem(1, 1, 1)
             copy_dz1_t(0, 1, 1, "S")
             quantize("x_t", 1, 0)
+            make_dz1(1, 1, 0)
             quantize("dz1_t", 1, 0, 0)
-            quantize("dz1_t", 0, 1)
+            quantize("dz1", 1, 0, 1)
+            group("dz1", 0, 1, "G", 0, "by_gpsimd", 1)
+            make_dz1(1, 1, 1)
             copy_x_t(1, 0, 1, "V")
+            for t in range(2, 4):
+                make_dz1(1, 1, t)
+            out_pass(1, "out_1", 0, 0, 0)
+            out_product("out_1", 0, 1, 0, 1)
+            transpose_dz1(1, 1, 0, 7)
+            transpose_x(1, 1, 0, 4)
             quantize("dz1_t", 1, 0, 1)
-            interleave_dz1(0, 1, "G", slice(0, 256), "handed_on", 1)
-            for t in range(2):
-                out_pass(1, "out_1", 0, t, 0)
-            for z in range(2):
-                transpose_x(1, 1, z, 3 * z)
-            for t in range(2, 4):
-                out_product("out_1", 0, t, 0, (4, 6)[t - 2])
-            square_mem(1, 1, 0)
-            copy_x_t(1, 1, 0, "V")
-            for t in range(2):
-                make_dz1(1, 1, t)
-            copy_x_t(1, 1, 1, "V")
-            for h in range(2):
-                quantize("x_t", h, 1)
-            raw("w_rg", 0)
-            for t in range(2):
-                out_copy("out_1", 0, t, 0, "S")
-            store_columns("out_1", 0, 0, 0)
-            for t in range(2, 4):
-                for k in range(2):
-                    hidden_pass(k, 1, 1, t, (5, 2)[t - 2])
+            raw("w_rg", 0, 0)
             operand["w_rg"] = codes_pair("w_hid")
-            transpose_dz1(1, 1, 0, 1)
-            square_mem(1, 1, 1)
-            for t in range(2, 4):
-                out_copy("out_1", 0, t, 0, "S")
-            store_columns("out_1", 0, 1, 0)
-            for t in range(2, 4):
-                make_dz1(1, 1, t)
-            copy_dz1_t(1, 1, 0, "S")
-            for z in range(2):
-                for k in range(2):
-                    for t in range(2 * z, 2 * z + 2):
-                        out_pass(k, "out_1", 0, t, 1, (7, 0, 3, 4)[t])
-            transpose_dz1(1, 1, 1, 6)
-            interleave_dz1(0, 1, "V", slice(256, HALF))
-            quantize("dz1_t", 1, 1, 0)
-            interleave_dz1(1, 1, "V")
-            copy_dz1_t(1, 1, 1, "V")
-            both(quantize, "dz1", 1, 0)
-            quantize("dz1_t", 1, 1, 1)
-            for z in range(2):
-                for t in range(2 * z, 2 * z + 2):
-                    out_copy("out_1", 0, t, 1, "S")
-                store_columns("out_1", 0, z, 1)
+            for t in range(2):
+                out_copy("out_1", 0, t, 0, "S", True)
+            store_columns("out_1", 0, 0, 0)
             for k in range(2):
-                interleave_w_rg(k, 0, 0, "V")
+                for t in range(2, 4):
+                    out_pass(k, "out_1", 0, t, 0, (6, 2)[t - 2])
+            transpose_dz1(1, 1, 1, 5)
+            transpose_x(1, 1, 1, 3)
+            quantize("dz1_t", 0, 1)
+            quantize("x_t", 0, 1)
+            copy_dz1_t(1, 1, 0, "S")
+            copy_x_t(1, 1, 0, "S")
+            for t in range(2, 4):
+                out_copy("out_1", 0, t, 0, "S", True)
+            store_columns("out_1", 0, 1, 0)
+            copy_dz1_t(1, 1, 1, "S")
+            quantize("dz1_t", 1, 1, 0)
+            group("dz1", 0, 1, "V", 1)
+            copy_x_t(1, 1, 1, "V")
+            quantize("dz1_t", 1, 1, 1)
+            quantize("x_t", 1, 1)
+            group("dz1", 1, 1, "V")
+            for k in range(2):
+                group("w_rg", k, 0, "V", 0)
+            both(quantize, "dz1", 0, 1)
             for k in range(2):
                 quantize("w_rg", k, 0, 0)
-            for g in range(2):
-                quantize("dz1", g, 1)
-            for t in range(4):
-                for n in range(2):
-                    out_product("out_1", 1, t, n, (1, 5, 2, 7, 0, 3, 4, 6)[2 * t + n])
-                    out_copy("out_1", 1, t, n, "S")
-                store_row("out_1", 1, t)
+            quantize("dz1", 1, 1)
+            sides = (1, 0, 7, 4, 6, 2, 5, 3)
+            for b, (c, n) in enumerate(((1, 0), (0, 1), (1, 1))):
+                for t in range(4):
+                    out_product("out_1", c, t, n, sides[(4 * b + t) % 8])
+                    out_copy("out_1", c, t, n, "S", True)
+                    if t % 2:
+                        store_columns("out_1", c, t // 2, n)
             for c, z in ((0, 1), (1, 0), (1, 1)):
                 for k in range(2):
-                    interleave_w_rg(k, c, z, "V")
+                    group("w_rg", k, c, "V", z)
                 for k in range(2):
                     quantize("w_rg", k, c, z)
             for c in range(2):
                 for t in range(4):
                     for h in range(2):
-                        out_product("out_0", c, t, h, (1, 5, 2, 7, 0, 3, 4, 6)[2 * t + h])
+                        out_product("out_0", c, t, h, sides[(4 + 2 * t + h) % 8])
                         out_copy("out_0", c, t, h, "V" if h and 4 * c + t >= 4 else "S")
                         if c == 1 and t == 3:
                             store_piece("out_0", c, t, h)

@@ -21,7 +21,7 @@ AREA_BYTES = 4096
 AREAS = 16
 GROUPED = 5
 TURNED = 7
-Y_SQUARED = 4
+Y_SQUARED = 3
 MEM_SQUARED = 4
 
 FLOPS = 3 * 2 * SIZE * SIZE * SIZE
@@ -114,12 +114,12 @@ def tile_pt_grumb_pb_v_kernel(
                 in_=grouped.rearrange("p n j -> p (n j)"),
             )
 
-        def product_pass(k, out, lhs, lhs_first, rhs, rhs_cols):
+        def product_pass(k, out, lhs, lhs_tile, lhs_first, rhs, rhs_cols):
             lhs_cols = slice(lhs_first, lhs_first + P)
             nc.tensor.matmul_mx(
                 out=out,
-                lhsT=operand[lhs][0][k][:, lhs_cols].bitcast(fp8[lhs]),
-                lhsT_scale=operand[lhs][1][k][:, lhs_cols],
+                lhsT=operand[lhs][0][lhs_tile][:, lhs_cols].bitcast(fp8[lhs]),
+                lhsT_scale=operand[lhs][1][lhs_tile][:, lhs_cols],
                 rhs=operand[rhs][0][k][:, rhs_cols].bitcast(fp8[rhs]),
                 rhs_scale=operand[rhs][1][k][:, rhs_cols],
                 start=(k == 0),
@@ -160,23 +160,17 @@ def tile_pt_grumb_pb_v_kernel(
                 nc.sync.dma_start(out=tile[:], in_=hbm["mem"][g][:, pair(z), half(h)])
                 held["raw", "mem", g, h, z] = tile[:]
 
+        def load_x(n, z):
+            tile = area([P, 2, SIZE], BF16, 1)
+            nc.sync.dma_start(out=tile[:], in_=hbm["x"][n][:, pair(z), :])
+            held["raw", "x", n, z] = tile[:]
+
         def load_w_rg():
             tile = moved.tile([P, 2, PACK, SIZE], BF16, name="w_rg_raw", tag="w_rg_raw", align_bytes=2048, bufs=1, offset=AREAS * AREA_BYTES)
             nc.sync.dma_start(
                 out=tile[:].rearrange("p k j c -> p k (j c)"), in_=w_readgate.rearrange("(k p j) c -> p k (j c)", p=P, j=PACK)
             )
-            for k in range(2):
-                for c in range(2):
-                    held["raw", "w_rg", k, c] = tile[:, k, :, half(c)]
-
-        def load_grad(h):
-            tile = area([P, 2, PACK, HALF], BF16, 2)
-            nc.sync.dma_start(
-                out=tile[:].rearrange("p k j c -> p (k j) c"),
-                in_=grad_out.rearrange("(k p j) c -> p k j c", p=P, j=PACK)[:, :, :, half(h)],
-            )
-            for k in range(2):
-                held["raw", "grad", k, h] = tile[:, k]
+            held["raw", "w_rg"] = tile[:]
 
         load_order = [
             (load_half, "w_hid", 0, 0),
@@ -196,17 +190,17 @@ def tile_pt_grumb_pb_v_kernel(
             (load_y, 0, 1, 0),
             (load_half, "grad", 0, 1),
             (load_y, 0, 1, 1),
-            (load_half, "x", 0, 0),
+            (load_x, 0, 0),
             (load_half, "grad", 1, 1),
             (load_y, 1, 1, 0),
             (load_y, 1, 1, 1),
-            (load_half, "x", 0, 1),
+            (load_x, 0, 1),
             (load_mem, 0, 1, 0),
             (load_mem, 0, 1, 1),
             (load_mem, 1, 1, 0),
-            (load_half, "x", 1, 0),
+            (load_x, 1, 0),
             (load_mem, 1, 1, 1),
-            (load_half, "x", 1, 1),
+            (load_x, 1, 1),
             (load_w_rg,),
         ]
         issued = set()
@@ -219,31 +213,30 @@ def tile_pt_grumb_pb_v_kernel(
             return held[("raw",) + key]
 
         def square_y(k, h, v, u):
-            words = P if v is None else P // 2
-            t = work_tile([P, words, 2, PACK], F32, "y_squared", Y_SQUARED)
+            if u == 0:
+                held["y_squared", k, h, v] = work_tile([P, 2, P // 2, 2, PACK], F32, "y_squared", Y_SQUARED)
             nc.scalar.activation(
-                out=t[:].rearrange("p w e j -> p w j e"),
+                out=held["y_squared", k, h, v][:, u].rearrange("p w e j -> p w j e"),
                 in_=raw("y", k, h, v).rearrange("p j (w u e) -> p u w j e", u=2, e=2)[:, u],
                 func=ACT.Square,
             )
-            held["y_squared", k, h, v, u] = t
 
         def park_grad(k, h, v, side):
-            ps = bank(side, [P, 2, PACK, P // 2, 2], BF16)
+            ps = bank(side, [P, PACK, 2, P // 2, 2], BF16)
             source = raw("grad", k, h)[:, :, quarter(v)].rearrange("p j (w u e) -> p u j w e", u=2, e=2)
             for u in range(2):
-                nc.tensor.matmul(out=ps[:, u], lhsT=ident_bf16[:], rhs=source[:, u], start=True, stop=True)
+                nc.tensor.matmul(out=ps[:, :, u], lhsT=ident_bf16[:], rhs=source[:, u], start=True, stop=True)
             held["grad_ps", k, h, v] = ps
 
-        def make_dz2(k, h, v, u):
+        def make_dz2(k, h, v, u=None):
             if ("dz2", k, h) not in held:
                 held["dz2", k, h] = grouped_tile(HALF)
-            first = u * QUARTER + v * P
+            us = slice(0, 2) if u is None else slice(u, u + 1)
             nc.vector.scalar_tensor_tensor(
-                out=held["dz2", k, h][:, first : first + P, :],
-                in0=held["y_squared", k, h, v, u][:].rearrange("p w e j -> p (w e) j"),
+                out=held["dz2", k, h][:].rearrange("p (u v n) j -> p v u n j", u=2, v=2)[:, v, us],
+                in0=held["y_squared", k, h, v][:, us].rearrange("p u w e j -> p u (w e) j"),
                 scalar=1.0,
-                in1=held["grad_ps", k, h, v][:, u].rearrange("p j w e -> p (w e) j"),
+                in1=held["grad_ps", k, h, v][:, :, us].rearrange("p j u w e -> p u (w e) j"),
                 op0=ALU.subtract,
                 op1=ALU.mult,
             )
@@ -283,10 +276,17 @@ def tile_pt_grumb_pb_v_kernel(
                 held[name, k, c, part] = grouped_tile(QUARTER, tag, bufs)
                 interleave(engine, held[name, k, c, part][:], rows_of(name, k, c)[:, :, quarter(part)])
 
+        def group_w_rg(c, z):
+            held["w_rg", c, z] = grouped_tile(HALF)
+            nc.vector.tensor_copy(
+                out=held["w_rg", c, z][:].rearrange("p (k c i) j -> p k c j i", k=2, i=4),
+                in_=raw("w_rg")[:, :, :, quarter(2 * c + z)].rearrange("p k j (c i) -> p k c j i", i=4),
+            )
+
         def hidden_pass(k, g, h, t, side=None):
             if k == 0:
                 held["dh", g, h, t] = bank(side, [P, HALF])
-            product_pass(k, held["dh", g, h, t][:], "w_hid", g * HALF + t * P, "dz2", half(h))
+            product_pass(k, held["dh", g, h, t][:], "w_hid", k, g * HALF + t * P, "dz2", half(h))
 
         def make_dz1(g, h, t):
             nc.vector.scalar_tensor_tensor(
@@ -308,11 +308,11 @@ def tile_pt_grumb_pb_v_kernel(
             held["dz1_t_ps", g, h, z] = ps
 
         def transpose_x(n, h, z, side):
-            words = raw("x", n, h).bitcast(F32)
+            words = raw("x", n, z).bitcast(F32)
             ps = bank(side, [P, 2, 2, P])
             for a in range(2):
                 for u in range(2):
-                    nc.tensor.transpose(ps[:, a, u, :], words[:, 2 * z + a, u : u + QUARTER - 1 : 2], ident[:])
+                    nc.tensor.transpose(ps[:, a, u, :], words[:, a, h * QUARTER + u : (h + 1) * QUARTER : 2], ident[:])
             held["x_t_ps", n, h, z] = ps
 
         def turned_words(name, h, c, tag, bufs):
@@ -337,8 +337,11 @@ def tile_pt_grumb_pb_v_kernel(
         def out_pass(k, name, c, t, n, side=None):
             if k == 0:
                 held["ps", name, c, t, n] = bank(side, [P, HALF])
-            lhs, rhs = ("w_rg", "dz1") if name == "out_0" else ("dz1_t", "x_t")
-            product_pass(k, held["ps", name, c, t, n][:], lhs, c * HALF + t * P, rhs, half(n))
+            if name == "out_0":
+                first = (t // 2) * HALF + k * QUARTER + (t % 2) * P
+                product_pass(k, held["ps", name, c, t, n][:], "w_rg", c, first, "dz1", half(n))
+            else:
+                product_pass(k, held["ps", name, c, t, n][:], "dz1_t", k, c * HALF + t * P, "x_t", half(n))
 
         def out_product(name, c, t, n, side):
             for k in range(2):
@@ -425,8 +428,8 @@ def tile_pt_grumb_pb_v_kernel(
             both(quantize, "dz2", 0, 1)
             for z in range(2):
                 copy_dz1_t(1, 0, z, "S")
-            for z in range(2):
-                transpose_x(0, 0, z, 5 + z)
+            for h in range(2):
+                transpose_x(0, h, 0, 5 + h)
             park_grad(1, 1, 0, 7)
             for t in range(4):
                 hidden_pass(0, 0, 1, t, 1 + t)
@@ -434,10 +437,10 @@ def tile_pt_grumb_pb_v_kernel(
             quantize("dz1_t", 0, 0)
             quantize("dz1", 0, 0)
             group("dz1", 1, 0, "G", 0, "by_gpsimd", 1)
-            copy_x_t(0, 0, 1, "V")
+            copy_x_t(0, 1, 0, "V")
             park_grad(1, 1, 1, 6)
-            for z in range(2):
-                transpose_x(0, 1, z, (5, 0)[z])
+            for h in range(2):
+                transpose_x(0, h, 1, (5, 0)[h])
             for v in range(2):
                 both(square_y, 1, 1, v)
                 both(make_dz2, 1, 1, v)
@@ -447,10 +450,10 @@ def tile_pt_grumb_pb_v_kernel(
                 hidden_pass(1, 0, 1, t)
             for t in range(2):
                 hidden_pass(1, 1, 1, t)
+            copy_x_t(0, 0, 1, "S")
             quantize("x_t", 0, 0)
             quantize("dz1", 1, 0, 0)
             group("dz1", 1, 0, "G", 1, "by_gpsimd", 1)
-            copy_x_t(0, 1, 0, "S")
             both(square_mem, 0, 1)
             copy_x_t(0, 1, 1, "S")
             for t in range(4):
@@ -466,7 +469,7 @@ def tile_pt_grumb_pb_v_kernel(
             copy_dz1_t(0, 1, 0, "S")
             copy_x_t(1, 0, 0, "S")
             transpose_dz1(0, 1, 1, 4)
-            transpose_x(1, 0, 1, 0)
+            transpose_x(1, 1, 0, 0)
             square_mem(1, 1, 1)
             copy_dz1_t(0, 1, 1, "S")
             quantize("x_t", 1, 0)
@@ -475,15 +478,15 @@ def tile_pt_grumb_pb_v_kernel(
             quantize("dz1", 1, 0, 1)
             group("dz1", 0, 1, "G", 0, "by_gpsimd", 1)
             make_dz1(1, 1, 1)
-            copy_x_t(1, 0, 1, "V")
+            copy_x_t(1, 1, 0, "V")
             for t in range(2, 4):
                 make_dz1(1, 1, t)
             out_pass(1, "out_1", 0, 0, 0)
             out_product("out_1", 0, 1, 0, 1)
             transpose_dz1(1, 1, 0, 7)
-            transpose_x(1, 1, 0, 4)
+            transpose_x(1, 0, 1, 4)
             quantize("dz1_t", 1, 0, 1)
-            raw("w_rg", 0, 0)
+            raw("w_rg")
             operand["w_rg"] = codes_pair("w_hid")
             for t in range(2):
                 out_copy("out_1", 0, t, 0, "S", True)
@@ -494,24 +497,22 @@ def tile_pt_grumb_pb_v_kernel(
             transpose_dz1(1, 1, 1, 5)
             transpose_x(1, 1, 1, 3)
             quantize("dz1_t", 0, 1)
-            quantize("x_t", 0, 1)
             copy_dz1_t(1, 1, 0, "S")
-            copy_x_t(1, 1, 0, "S")
+            copy_x_t(1, 0, 1, "S")
             for t in range(2, 4):
                 out_copy("out_1", 0, t, 0, "S", True)
             store_columns("out_1", 0, 1, 0)
             copy_dz1_t(1, 1, 1, "S")
             quantize("dz1_t", 1, 1, 0)
+            quantize("x_t", 0, 1)
             group("dz1", 0, 1, "V", 1)
             copy_x_t(1, 1, 1, "V")
             quantize("dz1_t", 1, 1, 1)
             quantize("x_t", 1, 1)
             group("dz1", 1, 1, "V")
-            for k in range(2):
-                group("w_rg", k, 0, "V", 0)
+            group_w_rg(0, 0)
             both(quantize, "dz1", 0, 1)
-            for k in range(2):
-                quantize("w_rg", k, 0, 0)
+            quantize("w_rg", 0, 0)
             quantize("dz1", 1, 1)
             sides = (1, 0, 7, 4, 6, 2, 5, 3)
             for b, (c, n) in enumerate(((1, 0), (0, 1), (1, 1))):
@@ -520,16 +521,16 @@ def tile_pt_grumb_pb_v_kernel(
                     out_copy("out_1", c, t, n, "S", True)
                     if t % 2:
                         store_columns("out_1", c, t // 2, n)
-            for c, z in ((0, 1), (1, 0), (1, 1)):
-                for k in range(2):
-                    group("w_rg", k, c, "V", z)
-                for k in range(2):
-                    quantize("w_rg", k, c, z)
+            group_w_rg(0, 1)
+            for c, z in ((0, 1), (1, 0)):
+                group_w_rg(1, 1 - z)
+                quantize("w_rg", c, z)
+            quantize("w_rg", 1, 1)
             for c in range(2):
                 for t in range(4):
                     for h in range(2):
                         out_product("out_0", c, t, h, sides[(4 + 2 * t + h) % 8])
-                        out_copy("out_0", c, t, h, "V" if h and 4 * c + t >= 4 else "S")
+                        out_copy("out_0", c, t, h, "V" if h and 4 * c + t >= 3 else "S")
                         if c == 1 and t == 3:
                             store_piece("out_0", c, t, h)
                     if c == 0 or t < 3:

@@ -395,11 +395,10 @@ def tile_pt_grumb_pb_v_kernel(
             for v in range(2):
                 both(square_y, 1, 0, v)
                 both(make_dz2, 1, 0, v)
+                hidden_pass(0, 1, 0, 2 + v, 6 + v)
             both(quantize, "dz2", 1, 0)
             for t in range(4):
                 hidden_pass(1, 0, 0, t)
-            for t in range(2, 4):
-                hidden_pass(0, 1, 0, t, 4 + t)
             both(square_mem, 0, 0)
             interleave_w_hid(1, 1, "V")
             for t in range(2):
@@ -431,7 +430,7 @@ def tile_pt_grumb_pb_v_kernel(
             for h in range(2):
                 transpose_x(0, h, 0, 5 + h)
             park_grad(1, 1, 0, 7)
-            for t in range(4):
+            for t in range(3):
                 hidden_pass(0, 0, 1, t, 1 + t)
             copy_x_t(0, 0, 0, "S")
             quantize("dz1_t", 0, 0)
@@ -441,6 +440,7 @@ def tile_pt_grumb_pb_v_kernel(
             park_grad(1, 1, 1, 6)
             for h in range(2):
                 transpose_x(0, h, 1, (5, 0)[h])
+            hidden_pass(0, 0, 1, 3, 4)
             for v in range(2):
                 both(square_y, 1, 1, v)
                 both(make_dz2, 1, 1, v)
@@ -502,11 +502,11 @@ def tile_pt_grumb_pb_v_kernel(
             for t in range(2, 4):
                 out_copy("out_1", 0, t, 0, "S", True)
             store_columns("out_1", 0, 1, 0)
-            copy_dz1_t(1, 1, 1, "S")
+            copy_x_t(1, 1, 1, "S")
             quantize("dz1_t", 1, 1, 0)
             quantize("x_t", 0, 1)
+            copy_dz1_t(1, 1, 1, "V")
             group("dz1", 0, 1, "V", 1)
-            copy_x_t(1, 1, 1, "V")
             quantize("dz1_t", 1, 1, 1)
             quantize("x_t", 1, 1)
             group("dz1", 1, 1, "V")

@@ -395,10 +395,12 @@ def tile_pt_grumb_pb_v_kernel(
             for v in range(2):
                 both(square_y, 1, 0, v)
                 both(make_dz2, 1, 0, v)
-                hidden_pass(0, 1, 0, 2 + v, 6 + v)
+                if v == 0:
+                    hidden_pass(0, 1, 0, 2, 6)
             both(quantize, "dz2", 1, 0)
             for t in range(4):
                 hidden_pass(1, 0, 0, t)
+            hidden_pass(0, 1, 0, 3, 7)
             both(square_mem, 0, 0)
             interleave_w_hid(1, 1, "V")
             for t in range(2):
@@ -469,7 +471,7 @@ def tile_pt_grumb_pb_v_kernel(
             copy_dz1_t(0, 1, 0, "S")
             copy_x_t(1, 0, 0, "S")
             transpose_dz1(0, 1, 1, 4)
-            transpose_x(1, 1, 0, 0)
+            transpose_x(1, 1, 0, 1)
             square_mem(1, 1, 1)
             copy_dz1_t(0, 1, 1, "S")
             quantize("x_t", 1, 0)
@@ -482,7 +484,7 @@ def tile_pt_grumb_pb_v_kernel(
             for t in range(2, 4):
                 make_dz1(1, 1, t)
             out_pass(1, "out_1", 0, 0, 0)
-            out_product("out_1", 0, 1, 0, 1)
+            out_product("out_1", 0, 1, 0, 0)
             transpose_dz1(1, 1, 0, 7)
             transpose_x(1, 0, 1, 4)
             quantize("dz1_t", 1, 0, 1)
@@ -514,7 +516,7 @@ def tile_pt_grumb_pb_v_kernel(
             both(quantize, "dz1", 0, 1)
             quantize("w_rg", 0, 0)
             quantize("dz1", 1, 1)
-            sides = (1, 0, 7, 4, 6, 2, 5, 3)
+            sides = (0, 1, 7, 4, 6, 2, 5, 3)
             for b, (c, n) in enumerate(((1, 0), (0, 1), (1, 1))):
                 for t in range(4):
                     out_product("out_1", c, t, n, sides[(4 * b + t) % 8])

@@ -187,8 +187,8 @@ def tile_pt_grumb_pb_v_kernel(
             (load_mem, 0, 0, 1),
             (load_mem, 1, 0, 0),
             (load_mem, 1, 0, 1),
-            (load_y, 0, 1, 0),
             (load_half, "grad", 0, 1),
+            (load_y, 0, 1, 0),
             (load_y, 0, 1, 1),
             (load_x, 0, 0),
             (load_half, "grad", 1, 1),
@@ -197,8 +197,8 @@ def tile_pt_grumb_pb_v_kernel(
             (load_x, 0, 1),
             (load_mem, 0, 1, 0),
             (load_mem, 0, 1, 1),
-            (load_mem, 1, 1, 0),
             (load_x, 1, 0),
+            (load_mem, 1, 1, 0),
             (load_mem, 1, 1, 1),
             (load_x, 1, 1),
             (load_w_rg,),

from contextlib import ExitStack

import concourse.mybir as mybir
from concourse.masks import make_identity

F32 = mybir.dt.float32
BF16 = mybir.dt.bfloat16
U32 = mybir.dt.uint32
U8 = mybir.dt.uint8
E4M3 = mybir.dt.float8_e4m3fn_x4
E5M2 = mybir.dt.float8_e5m2_x4
ACT = mybir.ActivationFunctionType
ALU = mybir.AluOpType

SIZE = 1024
P = 128
PACK = 4
HALF = 512
QUARTER = 256
AREA_BYTES = 4096
AREAS = 16
GROUPED = 5
TURNED = 7
Y_SQUARED = 3
MEM_SQUARED = 4

FLOPS = 3 * 2 * SIZE * SIZE * SIZE
BYTES = 4 * SIZE * SIZE * 2 + 2 * SIZE * SIZE * 4 + 2 * SIZE * SIZE * 4


def tile_pt_grumb_pb_v_kernel(
    tc, x, out0, mem0, inp_out, w_readgate, w_rec_readgate, w_mem_readgate, w_hid_out, mem_out, y, grad_out, out_0, out_1
):
    nc = tc.nc

    def rows_by_four(hbm):
        return hbm.rearrange("(k p j) c -> k p j c", p=P, j=PACK)

    hbm = {
        "w_hid": rows_by_four(w_hid_out),
        "w_rg": rows_by_four(w_readgate),
        "y": rows_by_four(y),
        "grad": rows_by_four(grad_out),
        "mem": rows_by_four(mem_out),
        "x": rows_by_four(x),
        "out_0": out_0.rearrange("(c t p) b -> c p t b", p=P, t=PACK),
        "out_1": rows_by_four(out_1),
    }

    with ExitStack() as ctx:
        keep = ctx.enter_context(tc.tile_pool(name="keep", bufs=1))
        work = ctx.enter_context(tc.tile_pool(name="work", bufs=1))
        moved = ctx.enter_context(tc.tile_pool(name="moved", bufs=1))
        psum = ctx.enter_context(tc.psum_pool(name="psum", bufs=1))

        def keep_tile(shape, dtype, name):
            return keep.tile(shape, dtype, name=name, tag=name, align_bytes=256)

        def codes_pair(name):
            codes = [keep_tile([P, SIZE], U32, "%s_codes_%d" % (name, k)) for k in range(2)]
            scales = [keep_tile([P, SIZE], U8, "%s_scales_%d" % (name, k)) for k in range(2)]
            return codes, scales

        operand = {name: codes_pair(name) for name in ("w_hid", "dz2", "dz1", "dz1_t", "x_t")}
        fp8 = {"w_hid": E4M3, "w_rg": E4M3, "x_t": E4M3, "dz2": E5M2, "dz1": E5M2, "dz1_t": E5M2}
        dz1 = [[keep_tile([P, PACK, HALF], BF16, "dz1_%d_%d" % (g, h)) for h in range(2)] for g in range(2)]
        ident = keep_tile([P, P], F32, "ident")
        ident_bf16 = keep_tile([P, P], BF16, "ident_bf16")
        minus_half = keep_tile([P, 1], F32, "minus_half")
        held = {"next_area": 0}

        def work_tile(shape, dtype, tag, bufs):
            return work.tile(shape, dtype, name=tag, tag=tag, align_bytes=256, bufs=bufs)

        def area(shape, dtype, count):
            first = held["next_area"] if held["next_area"] + count <= AREAS else 0
            held["next_area"] = first + count
            tag = "area_%d_%d" % (first, count)
            return moved.tile(shape, dtype, name=tag, tag=tag, align_bytes=2048, bufs=1, offset=first * AREA_BYTES)

        def grouped_tile(columns, tag="grouped", bufs=GROUPED):
            return work_tile([P, columns, PACK], BF16, tag, bufs)

        def bank(side, shape, dtype=F32):
            return psum.tile(shape, dtype, name="bank_%d" % side, tag="bank_%d" % side)

        def half(n):
            return slice(n * HALF, (n + 1) * HALF)

        def quarter(n):
            return slice(n * QUARTER, (n + 1) * QUARTER)

        def pair(z):
            return slice(2 * z, 2 * z + 2)

        def move(engine, out, in_):
            if engine == "S":
                nc.scalar.copy(out=out, in_=in_)
            elif engine == "V":
                nc.vector.tensor_copy(out=out, in_=in_)
            else:
                nc.gpsimd.tensor_scalar(out=out, in0=in_, scalar1=1.0, scalar2=-0.0, op0=ALU.mult, op1=ALU.add)

        def quantize(name, k, c, part=None):
            codes, scales = operand[name]
            if (name, k, c, part) in held:
                grouped = held[name, k, c, part][:]
            else:
                grouped = held[name, k, c][:] if part is None else held[name, k, c][:, quarter(part), :]
            cols = half(c) if part is None else quarter(2 * c + part)
            nc.vector.quantize_mx(
                out=codes[k][:, cols].bitcast(fp8[name]),
                scales=scales[k][:, cols],
                in_=grouped.rearrange("p n j -> p (n j)"),
            )

        def product_pass(k, out, lhs, lhs_tile, lhs_first, rhs, rhs_cols):
            lhs_cols = slice(lhs_first, lhs_first + P)
            nc.tensor.matmul_mx(
                out=out,
                lhsT=operand[lhs][0][lhs_tile][:, lhs_cols].bitcast(fp8[lhs]),
                lhsT_scale=operand[lhs][1][lhs_tile][:, lhs_cols],
                rhs=operand[rhs][0][k][:, rhs_cols].bitcast(fp8[rhs]),
                rhs_scale=operand[rhs][1][k][:, rhs_cols],
                start=(k == 0),
                stop=(k == 1),
            )

        def load_half(name, k, c):
            tile = area([P, PACK, HALF], BF16, 1)
            nc.sync.dma_start(out=tile[:], in_=hbm[name][k][:, :, half(c)])
            held["raw", name, k, c] = tile[:]

        def load_rows(name, k):
            tile = area([P, PACK, SIZE], BF16, 2)
            nc.sync.dma_start(out=tile[:], in_=hbm[name][k])
            for c in range(2):
                held["raw", name, k, c] = tile[:, :, half(c)]

        def load_y(k, h, v=None):
            if v is None:
                tile = area([P, PACK, HALF], F32, 2)
                nc.sync.dma_start(out=tile[:], in_=hbm["y"][k][:, :, half(h)])
                held["raw", "y", k, h, None] = tile[:]
                for part in range(2):
                    held["raw", "y", k, h, part] = tile[:, :, quarter(part)]
            else:
                tile = area([P, PACK, QUARTER], F32, 1)
                nc.sync.dma_start(out=tile[:], in_=hbm["y"][k][:, :, quarter(2 * h + v)])
                held["raw", "y", k, h, v] = tile[:]

        def load_mem(g, h, z=None):
            if z is None:
                tile = area([P, PACK, HALF], F32, 2)
                nc.sync.dma_start(out=tile[:], in_=hbm["mem"][g][:, :, half(h)])
                for part in range(2):
                    held["raw", "mem", g, h, part] = tile[:, pair(part), :]
            else:
                tile = area([P, 2, HALF], F32, 1)
                nc.sync.dma_start(out=tile[:], in_=hbm["mem"][g][:, pair(z), half(h)])
                held["raw", "mem", g, h, z] = tile[:]

        def load_x(n, z):
            tile = area([P, 2, SIZE], BF16, 1)
            nc.sync.dma_start(out=tile[:], in_=hbm["x"][n][:, pair(z), :])
            held["raw", "x", n, z] = tile[:]

        def load_w_rg():
            tile = moved.tile([P, 2, PACK, SIZE], BF16, name="w_rg_raw", tag="w_rg_raw", align_bytes=2048, bufs=1, offset=AREAS * AREA_BYTES)
            nc.sync.dma_start(
                out=tile[:].rearrange("p k j c -> p k (j c)"), in_=w_readgate.rearrange("(k p j) c -> p k (j c)", p=P, j=PACK)
            )
            held["raw", "w_rg"] = tile[:]

        load_order = [
            (load_half, "w_hid", 0, 0),
            (load_half, "w_hid", 0, 1),
            (load_half, "w_hid", 1, 0),
            (load_half, "grad", 0, 0),
            (load_y, 0, 0, 0),
            (load_y, 0, 0, 1),
            (load_half, "grad", 1, 0),
            (load_y, 1, 0, 0),
            (load_y, 1, 0, 1),
            (load_mem, 0, 0, 0),
            (load_half, "w_hid", 1, 1),
            (load_mem, 0, 0, 1),
            (load_mem, 1, 0, 0),
            (load_mem, 1, 0, 1),
            (load_half, "grad", 0, 1),
            (load_y, 0, 1, 0),
            (load_y, 0, 1, 1),
            (load_x, 0, 0),
            (load_half, "grad", 1, 1),
            (load_y, 1, 1, 0),
            (load_y, 1, 1, 1),
            (load_x, 0, 1),
            (load_mem, 0, 1, 0),
            (load_mem, 0, 1, 1),
            (load_x, 1, 0),
            (load_mem, 1, 1, 0),
            (load_mem, 1, 1, 1),
            (load_x, 1, 1),
            (load_w_rg,),
        ]
        issued = set()

        def raw(*key):
            for step in load_order:
                if ("raw",) + key not in held and step not in issued:
                    issued.add(step)
                    step[0](*step[1:])
            return held[("raw",) + key]

        def square_y(k, h, v, u):
            if u == 0:
                held["y_squared", k, h, v] = work_tile([P, 2, P // 2, 2, PACK], F32, "y_squared", Y_SQUARED)
            nc.scalar.activation(
                out=held["y_squared", k, h, v][:, u].rearrange("p w e j -> p w j e"),
                in_=raw("y", k, h, v).rearrange("p j (w u e) -> p u w j e", u=2, e=2)[:, u],
                func=ACT.Square,
            )

        def park_grad(k, h, v, side):
            ps = bank(side, [P, PACK, 2, P // 2, 2], BF16)
            source = raw("grad", k, h)[:, :, quarter(v)].rearrange("p j (w u e) -> p u j w e", u=2, e=2)
            for u in range(2):
                nc.tensor.matmul(out=ps[:, :, u], lhsT=ident_bf16[:], rhs=source[:, u], start=True, stop=True)
            held["grad_ps", k, h, v] = ps

        def make_dz2(k, h, v, u=None):
            if ("dz2", k, h) not in held:
                held["dz2", k, h] = grouped_tile(HALF)
            us = slice(0, 2) if u is None else slice(u, u + 1)
            nc.vector.scalar_tensor_tensor(
                out=held["dz2", k, h][:].rearrange("p (u v n) j -> p v u n j", u=2, v=2)[:, v, us],
                in0=held["y_squared", k, h, v][:, us].rearrange("p u w e j -> p u (w e) j"),
                scalar=1.0,
                in1=held["grad_ps", k, h, v][:, :, us].rearrange("p j u w e -> p u (w e) j"),
                op0=ALU.subtract,
                op1=ALU.mult,
            )

        def square_mem(g, h, z):
            sq = work_tile([P, 2, 2, QUARTER], F32, "mem_squared", MEM_SQUARED)
            nc.scalar.activation(
                out=sq[:].rearrange("p u a (w e) -> p u (a w) e", e=2),
                in_=raw("mem", g, h, z).rearrange("p a (w u e) -> p u (a w) e", u=2, e=2),
                func=ACT.Square,
                bias=minus_half[:],
            )
            held["mem_squared", g, h, z] = sq

        def interleave_w_hid(k, g, engine):
            held["w_hid", k, g] = grouped_tile(HALF)
            move(
                engine,
                held["w_hid", k, g][:].rearrange("p (t m) j -> p m j t", t=PACK),
                raw("w_hid", k, g).rearrange("p j (m t) -> p m j t", t=PACK),
            )

        def interleave(engine, grouped, rows):
            if engine == "G":
                move(engine, grouped, rows.rearrange("p j c -> p c j"))
            else:
                move(engine, grouped.rearrange("p (c i) j -> p c j i", i=4), rows.rearrange("p j (c i) -> p c j i", i=4))

        def rows_of(name, k, c):
            return dz1[k][c][:] if name == "dz1" else raw(name, k, c)

        def group(name, k, c, engine, part=None, tag="grouped", bufs=GROUPED):
            if part is None:
                held[name, k, c] = grouped_tile(HALF, tag, bufs)
                interleave(engine, held[name, k, c][:], rows_of(name, k, c))
            else:
                held[name, k, c, part] = grouped_tile(QUARTER, tag, bufs)
                interleave(engine, held[name, k, c, part][:], rows_of(name, k, c)[:, :, quarter(part)])

        def group_w_rg(c, z):
            held["w_rg", c, z] = grouped_tile(HALF)
            nc.vector.tensor_copy(
                out=held["w_rg", c, z][:].rearrange("p (k c i) j -> p k c j i", k=2, i=4),
                in_=raw("w_rg")[:, :, :, quarter(2 * c + z)].rearrange("p k j (c i) -> p k c j i", i=4),
            )

        def hidden_pass(k, g, h, t, side=None):
            if k == 0:
                held["dh", g, h, t] = bank(side, [P, HALF])
            product_pass(k, held["dh", g, h, t][:], "w_hid", k, g * HALF + t * P, "dz2", half(h))

        def make_dz1(g, h, t):
            nc.vector.scalar_tensor_tensor(
                out=dz1[g][h][:, t, :].rearrange("p (u n) -> p u n", u=2),
                in0=held["mem_squared", g, h, t // 2][:, :, t % 2, :],
                scalar=0.25,
                in1=held["dh", g, h, t][:].rearrange("p (u n) -> p u n", u=2),
                op0=ALU.subtract,
                op1=ALU.mult,
            )

        def transpose_dz1(g, h, z, side):
            words = dz1[g][h][:].rearrange("p t n -> p (t n)").bitcast(F32)
            ps = bank(side, [P, 2, 2, P])
            for a in range(2):
                for u in range(2):
                    first = (2 * z + a) * QUARTER + u * P
                    nc.tensor.transpose(ps[:, a, u, :], words[:, first : first + P], ident[:])
            held["dz1_t_ps", g, h, z] = ps

        def transpose_x(n, h, z, side):
            words = raw("x", n, z).bitcast(F32)
            ps = bank(side, [P, 2, 2, P])
            for a in range(2):
                for u in range(2):
                    nc.tensor.transpose(ps[:, a, u, :], words[:, a, h * QUARTER + u : (h + 1) * QUARTER : 2], ident[:])
            held["x_t_ps", n, h, z] = ps

        def turned_words(name, h, c, tag, bufs):
            if (name, h, c) not in held:
                held[name, h, c] = grouped_tile(HALF, tag, bufs)
            return held[name, h, c][:].rearrange("p n j -> p (n j)").bitcast(F32)

        def copy_dz1_t(g, h, z, engine, tag="turned", bufs=TURNED):
            move(
                engine,
                turned_words("dz1_t", h, g, tag, bufs)[:, half(z)].rearrange("p (a r u) -> p a r u", a=2, u=2),
                held["dz1_t_ps", g, h, z][:].rearrange("p a u r -> p a r u"),
            )

        def copy_x_t(n, h, z, engine, tag="turned", bufs=TURNED):
            move(
                engine,
                turned_words("x_t", h, n, tag, bufs).rearrange("p (r z a u) -> p z r a u", z=2, a=2, u=2)[:, z],
                held["x_t_ps", n, h, z][:].rearrange("p a u r -> p r a u"),
            )

        def out_pass(k, name, c, t, n, side=None):
            if k == 0:
                held["ps", name, c, t, n] = bank(side, [P, HALF])
            if name == "out_0":
                first = (t // 2) * HALF + k * QUARTER + (t % 2) * P
                product_pass(k, held["ps", name, c, t, n][:], "w_rg", c, first, "dz1", half(n))
            else:
                product_pass(k, held["ps", name, c, t, n][:], "dz1_t", k, c * HALF + t * P, "x_t", half(n))

        def out_product(name, c, t, n, side):
            for k in range(2):
                out_pass(k, name, c, t, n, side)

        def out_copy(name, c, t, n, engine, by_columns=False):
            key, place = ((name, c, t // 2, n), t % 2) if by_columns else ((name, c, t), n)
            if key not in held:
                held[key] = area([P, 2, HALF], F32, 1)
            staged, ps = held[key][:, place, :], held["ps", name, c, t, n][:]
            if name == "out_0":
                staged = staged.rearrange("p (w u e) -> p w u e", u=2, e=2)
                ps = ps.rearrange("p (u w e) -> p w u e", u=2, e=2)
            move(engine, staged, ps)

        def store_row(name, c, t):
            nc.sync.dma_start(out=hbm[name][c][:, t, :], in_=held[name, c, t][:].rearrange("p n w -> p (n w)"))

        def store_columns(name, c, z, n):
            nc.sync.dma_start(out=hbm[name][c][:, pair(z), half(n)], in_=held[name, c, z, n][:])

        def store_piece(name, c, t, n):
            nc.sync.dma_start(out=hbm[name][c][:, t, half(n)], in_=held[name, c, t][:, n, :])

        def both(step, *args):
            for u in range(2):
                step(*args, u)

        nc.vector.memset(minus_half[:], -0.5)
        make_identity(nc, ident_bf16[:])
        make_identity(nc, ident[:])

        with tc.manual_schedule():
            interleave_w_hid(0, 0, "V")
            interleave_w_hid(0, 1, "S")
            quantize("w_hid", 0, 0)
            interleave_w_hid(1, 0, "V")
            quantize("w_hid", 1, 0)
            quantize("w_hid", 0, 1)
            for v in range(2):
                park_grad(0, 0, v, 6 + v)
            for v in range(2):
                both(square_y, 0, 0, v)
                both(make_dz2, 0, 0, v)
                park_grad(1, 0, v, 6 + v)
            quantize("dz2", 0, 0)
            for t in range(4):
                hidden_pass(0, 0, 0, t, t)
            for t in range(2):
                hidden_pass(0, 1, 0, t, 4 + t)
            for v in range(2):
                both(square_y, 1, 0, v)
                both(make_dz2, 1, 0, v)
                if v == 0:
                    hidden_pass(0, 1, 0, 2, 6)
            both(quantize, "dz2", 1, 0)
            for t in range(4):
                hidden_pass(1, 0, 0, t)
            hidden_pass(0, 1, 0, 3, 7)
            both(square_mem, 0, 0)
            interleave_w_hid(1, 1, "V")
            for t in range(2):
                make_dz1(0, 0, t)
            transpose_dz1(0, 0, 0, 0)
            quantize("w_hid", 1, 1)
            for t in range(2, 4):
                make_dz1(0, 0, t)
            group("dz1", 0, 0, "G", None, "by_gpsimd", 1)
            for t in range(4):
                hidden_pass(1, 1, 0, t)
            both(square_mem, 1, 0)
            both(square_y, 0, 1, 0)
            transpose_dz1(0, 0, 1, 1)
            park_grad(0, 1, 0, 2)
            for z in range(2):
                copy_dz1_t(0, 0, z, "S")
            for t in range(4):
                make_dz1(1, 0, t)
            transpose_dz1(1, 0, 0, 3)
            park_grad(0, 1, 1, 4)
            transpose_dz1(1, 0, 1, 0)
            both(make_dz2, 0, 1, 0)
            both(square_y, 0, 1, 1)
            both(make_dz2, 0, 1, 1)
            both(quantize, "dz2", 0, 1)
            for z in range(2):
                copy_dz1_t(1, 0, z, "S")
            for h in range(2):
                transpose_x(0, h, 0, 5 + h)
            park_grad(1, 1, 0, 7)
            for t in range(3):
                hidden_pass(0, 0, 1, t, 1 + t)
            copy_x_t(0, 0, 0, "S")
            quantize("dz1_t", 0, 0)
            quantize("dz1", 0, 0)
            group("dz1", 1, 0, "G", 0, "by_gpsimd", 1)
            copy_x_t(0, 1, 0, "V")
            park_grad(1, 1, 1, 6)
            for h in range(2):
                transpose_x(0, h, 1, (5, 0)[h])
            hidden_pass(0, 0, 1, 3, 4)
            for v in range(2):
                both(square_y, 1, 1, v)
                both(make_dz2, 1, 1, v)
                hidden_pass(0, 1, 1, v, 7 - v)
            both(quantize, "dz2", 1, 1)
            for t in range(4):
                hidden_pass(1, 0, 1, t)
            for t in range(2):
                hidden_pass(1, 1, 1, t)
            copy_x_t(0, 0, 1, "S")
            quantize("x_t", 0, 0)
            quantize("dz1", 1, 0, 0)
            group("dz1", 1, 0, "G", 1, "by_gpsimd", 1)
            both(square_mem, 0, 1)
            copy_x_t(0, 1, 1, "S")
            for t in range(4):
                make_dz1(0, 1, t)
            for k in range(2):
                hidden_pass(k, 1, 1, 2, 5)
            transpose_dz1(0, 1, 0, 1)
            transpose_x(1, 0, 0, 0)
            out_pass(0, "out_1", 0, 0, 0, 2)
            for k in range(2):
                hidden_pass(k, 1, 1, 3, 3)
            square_mem(1, 1, 0)
            copy_dz1_t(0, 1, 0, "S")
            copy_x_t(1, 0, 0, "S")
            transpose_dz1(0, 1, 1, 4)
            transpose_x(1, 1, 0, 1)
            square_mem(1, 1, 1)
            copy_dz1_t(0, 1, 1, "S")
            quantize("x_t", 1, 0)
            make_dz1(1, 1, 0)
            quantize("dz1_t", 1, 0, 0)
            quantize("dz1", 1, 0, 1)
            group("dz1", 0, 1, "G", 0, "by_gpsimd", 1)
            make_dz1(1, 1, 1)
            copy_x_t(1, 1, 0, "V")
            for t in range(2, 4):
                make_dz1(1, 1, t)
            out_pass(1, "out_1", 0, 0, 0)
            out_product("out_1", 0, 1, 0, 0)
            transpose_dz1(1, 1, 0, 7)
            transpose_x(1, 0, 1, 4)
            quantize("dz1_t", 1, 0, 1)
            raw("w_rg")
            operand["w_rg"] = codes_pair("w_hid")
            for t in range(2):
                out_copy("out_1", 0, t, 0, "S", True)
            store_columns("out_1", 0, 0, 0)
            for k in range(2):
                for t in range(2, 4):
                    out_pass(k, "out_1", 0, t, 0, (6, 2)[t - 2])
            transpose_dz1(1, 1, 1, 5)
            transpose_x(1, 1, 1, 3)
            quantize("dz1_t", 0, 1)
            copy_dz1_t(1, 1, 0, "S")
            copy_x_t(1, 0, 1, "S")
            for t in range(2, 4):
                out_copy("out_1", 0, t, 0, "S", True)
            store_columns("out_1", 0, 1, 0)
            copy_x_t(1, 1, 1, "S")
            quantize("dz1_t", 1, 1, 0)
            quantize("x_t", 0, 1)
            copy_dz1_t(1, 1, 1, "V")
            group("dz1", 0, 1, "V", 1)
            quantize("dz1_t", 1, 1, 1)
            quantize("x_t", 1, 1)
            group("dz1", 1, 1, "V")
            group_w_rg(0, 0)
            both(quantize, "dz1", 0, 1)
            quantize("w_rg", 0, 0)
            quantize("dz1", 1, 1)
            sides = (0, 1, 7, 4, 6, 2, 5, 3)
            for b, (c, n) in enumerate(((1, 0), (0, 1), (1, 1))):
                for t in range(4):
                    out_product("out_1", c, t, n, sides[(4 * b + t) % 8])
                    out_copy("out_1", c, t, n, "S", True)
                    if t % 2:
                        store_columns("out_1", c, t // 2, n)
            group_w_rg(0, 1)
            for c, z in ((0, 1), (1, 0)):
                group_w_rg(1, 1 - z)
                quantize("w_rg", c, z)
            quantize("w_rg", 1, 1)
            for c in range(2):
                for t in range(4):
                    for h in range(2):
                        out_product("out_0", c, t, h, sides[(4 + 2 * t + h) % 8])
                        out_copy("out_0", c, t, h, "V" if h and 4 * c + t >= 3 else "S")
                        if c == 1 and t == 3:
                            store_piece("out_0", c, t, h)
                    if c == 0 or t < 3:
                        store_row("out_0", c, t)
